import numpy as np
import ml_dtypes


def mxq(x, axis, fmt="e4m3"):
    dtype, down = {"e4m3": (ml_dtypes.float8_e4m3fn, 7), "e5m2": (ml_dtypes.float8_e5m2, 14)}[fmt]
    v = np.moveaxis(np.asarray(x, np.float32).astype(ml_dtypes.bfloat16).astype(np.float64), axis, -1)
    blocks = v.reshape(v.shape[:-1] + (-1, 32))
    amax = np.abs(blocks).max(-1, keepdims=True)
    byte = np.maximum(np.where(amax > 0, np.frexp(amax)[1] - 1 + 127, 0) - down, 1)
    scale = np.exp2(byte - 127.0)
    codes = (blocks / scale).astype(np.float32).astype(dtype).astype(np.float64)
    return np.moveaxis((codes * scale).reshape(v.shape), -1, axis)


WIDE = False


def mx_kscale(k):
    if not WIDE:
        return np.ones(k)
    levels = np.array([10, -10, 5, -5, 0])
    a = np.random.permutation(np.resize(levels, k // 512 * 4)).reshape(k // 512, 4)
    idx = np.arange(k)
    return np.exp2(a[idx // 512, idx % 128 // 32])


BF16 = ml_dtypes.bfloat16


def bf(x):
    return np.asarray(x, np.float32).astype(BF16)


def f64(x):
    return np.asarray(x).astype(np.float64)


E2M1 = np.array([0.0, 0.5, 1.0, 1.5, 2.0, 3.0, 4.0, 6.0, -0.0, -0.5, -1.0, -1.5, -2.0, -3.0, -4.0, -6.0])


def pack_weight(w, fmt):
    k, n = w.shape
    w = f64(bf(w)).reshape(k // 32, 32, n)
    amax = np.abs(w).max(1)
    if fmt == "e4m3":
        byte = np.frexp(amax)[1] - 1 + 127 - 7
    else:
        mant, ex = np.frexp(amax / 6.0)
        byte = np.where(mant > 0.5, ex, ex - 1) + 127
    byte = np.clip(np.where(amax > 0, byte, 1), 1, 254)
    scaled = (w * np.exp2(127.0 - byte)[:, None, :]).reshape(k, n).astype(np.float32)
    by_word = np.ascontiguousarray(scaled.reshape(k // 512, 128, 4, n).transpose(0, 1, 3, 2))
    if fmt == "e4m3":
        words = by_word.astype(ml_dtypes.float8_e4m3fn).view(np.uint8)
    else:
        c = by_word.astype(ml_dtypes.float4_e2m1fn).view(np.uint8) & 0xF
        words = c[..., 0::2] | (c[..., 1::2] << 4)
    return np.ascontiguousarray(words), np.ascontiguousarray(byte.astype(np.uint8).reshape(k // 512, 16, n))


def unpack_weight(words, scales, fmt):
    g, p, n, _ = words.shape
    if fmt == "e4m3":
        vals = np.ascontiguousarray(words).view(ml_dtypes.float8_e4m3fn).astype(np.float64)
    else:
        nib = np.empty((g, p, n, 4), np.uint8)
        nib[..., 0::2] = words & 0xF
        nib[..., 1::2] = words >> 4
        vals = E2M1[nib]
    vals = vals * np.repeat(np.exp2(scales.astype(np.float64) - 127.0), 8, axis=1)[..., None]
    return vals.transpose(0, 1, 3, 2).reshape(g * 512, n)

def pack4(w):
    words, scales = pack_weight(w, "e2m1")
    return words.reshape(words.shape[0], 128, -1), scales


def unpack4(words, scales):
    return unpack_weight(words.reshape(words.shape[0], 128, -1, 2), scales, "e2m1")


B, CIN, H, W, CR, COUT, SP, K = 4, 512, 32, 32, 512, 1024, 32, 7
PAD = K // 2
KK = K * K
HN = COUT // SP
HW = H * W
OFFS = [(dy, dx) for dy in range(K) for dx in range(K)]


def setup_inputs():
    s = mx_kscale(CIN)
    logits = bf(np.random.standard_normal((B, HN, KK, HW)) * 1.5)
    x = bf(np.random.standard_normal((B, CIN, H, W)) * s[None, :, None, None])
    w3c = np.random.standard_normal((COUT, CIN)) * 2.0 / np.sqrt(CIN) / s[None, :]
    b3c = bf(np.random.standard_normal(COUT) * 0.5)
    words, scales = pack4(np.ascontiguousarray(w3c.T))
    return {
        "logits": logits,
        "x": x,
        "w3c_words": words,
        "w3c_scales": scales,
        "b3c": b3c,
    }


def reference(logits, x, w3c_words, w3c_scales, b3c):
    x3 = (unpack4(w3c_words, w3c_scales).T @ mxq(f64(x).reshape(B, CIN, HW), 1, "e4m3")) + f64(b3c)[None, :, None]
    x3 = x3.reshape(B, COUT, H, W)
    lg = f64(logits)
    e = np.exp(lg - lg.max(axis=2, keepdims=True))
    wgt = (e / e.sum(axis=2, keepdims=True)).reshape(B, HN, KK, H, W)
    x3p = np.pad(x3, ((0, 0), (0, 0), (PAD, PAD), (PAD, PAD)), mode="reflect")
    acc = np.zeros((B, HN, SP, H, W))
    for k, (dy, dx) in enumerate(OFFS):
        patch = x3p[:, :, dy:dy + H, dx:dx + W].reshape(B, HN, SP, H, W)
        acc = acc + patch * wgt[:, :, k][:, :, None]
    return acc.reshape(B, COUT, H, W)

@@ -1,0 +1,231 @@
+from contextlib import ExitStack
+
+import concourse.mybir as mybir
+from concourse.masks import make_identity
+
+F32 = mybir.dt.float32
+BF16 = mybir.dt.bfloat16
+U8 = mybir.dt.uint8
+U32 = mybir.dt.uint32
+I32 = mybir.dt.int32
+FP8X4 = mybir.dt.float8_e4m3fn_x4
+FP4X4 = mybir.dt.float4_e2m1fn_x4
+ALU = mybir.AluOpType
+ACT = mybir.ActivationFunctionType
+
+P = 128
+B, CIN, H, W, COUT = 4, 512, 32, 32, 1024
+HEADS, SP = 32, 32
+K = 7
+KK = K * K
+PAD = K // 2
+HW = H * W
+PACK = 4
+
+BAND = 4
+NB = BAND * W
+BANDS = H // BAND
+ROWS = BAND + 2 * PAD
+WP = W + 2 * PAD
+CG = 16
+GROUPS = SP // CG
+PER_BANK = 4
+BANKS = CG // PER_BANK
+
+FLOPS = 2 * B * COUT * HW * CIN + 2 * B * COUT * HW * KK
+
+
+def reflect(u, size):
+    if u < 0:
+        return -u
+    if u > size - 1:
+        return 2 * (size - 1) - u
+    return u
+
+
+def tile_sam_pb_t_kernel(tc, logits, x, w3c_words, w3c_scales, b3c, out):
+    nc = tc.nc
+    logits_v = logits.rearrange("b h l n -> (b h) l n")
+    out_v = out.rearrange("b (h c) i j -> (b h) c (i j)", c=SP)
+
+    with ExitStack() as ctx:
+        const = ctx.enter_context(tc.tile_pool(name="const", bufs=1))
+        lg_pool = ctx.enter_context(tc.tile_pool(name="lg", bufs=1))
+        stat_pool = ctx.enter_context(tc.tile_pool(name="stat", bufs=2))
+        wgt_pool = ctx.enter_context(tc.tile_pool(name="wgt", bufs=2))
+        acc_pool = ctx.enter_context(tc.psum_pool(name="acc", bufs=1))
+        stage = ctx.enter_context(tc.psum_pool(name="stage", bufs=4))
+
+        ident = const.tile([P, P], F32)
+        make_identity(nc, ident[:])
+
+        w_words = const.tile([P, 2 * COUT], U8, align_bytes=64)
+        w_plane = const.tile([P, COUT], U8, align_bytes=64)
+        nc.vector.memset(w_plane[:].bitcast(I32), 0)
+        words_src = w3c_words[0].bitcast(I32).rearrange("p (h g w) -> p g h w", g=GROUPS, h=HEADS)
+        words_dst = w_words[:].bitcast(I32).rearrange("p (g h w) -> p g h w", g=GROUPS, h=HEADS)
+        scales_src = w3c_scales[0].bitcast(I32).rearrange("q (h g w) -> q g h w", g=GROUPS, h=HEADS)
+        for g in range(GROUPS):
+            nc.sync.dma_start(out=words_dst[:, g], in_=words_src[:, g])
+        for quad in range(4):
+            plane_dst = w_plane[32 * quad : 32 * quad + 4, :].bitcast(I32)
+            plane_dst = plane_dst.rearrange("q (g h w) -> q g h w", g=GROUPS, h=HEADS)
+            for g in range(GROUPS):
+                nc.sync.dma_start(out=plane_dst[:, g], in_=scales_src[4 * quad : 4 * quad + 4, g])
+
+        bias_bf = const.tile([P, SP], BF16)
+        for b in range(B):
+            nc.sync.dma_start(
+                out=bias_bf[b * HEADS : (b + 1) * HEADS, :], in_=b3c.rearrange("(h c) -> h c", c=SP)
+            )
+        bias = const.tile([P, SP], F32)
+        nc.vector.tensor_copy(out=bias[:], in_=bias_bf[:])
+
+        x_codes = const.tile([P, B, HW], U32, align_bytes=64)
+        x_plane = const.tile([P, B, HW], U8, align_bytes=64)
+        with tc.tile_pool(name="xin", bufs=2) as xin:
+            for b in range(B):
+                raw = xin.tile([P, PACK, HW], BF16)
+                nc.sync.dma_start(out=raw[:], in_=x[b].rearrange("(p t) i j -> p t (i j)", t=PACK))
+                grouped = xin.tile([P, HW, PACK], BF16, align_bytes=64)
+                nc.vector.tensor_copy(out=grouped[:], in_=raw[:].rearrange("p t n -> p n t"))
+                nc.vector.quantize_mx(
+                    out=x_codes[:, b, :].bitcast(FP8X4),
+                    scales=x_plane[:, b, :],
+                    in_=grouped[:].rearrange("p n t -> p (n t)"),
+                )
+
+        map_pool = ctx.enter_context(tc.tile_pool(name="map", bufs=2))
+        turn_pool = ctx.enter_context(tc.tile_pool(name="turn", bufs=2))
+        prod_pool = ctx.enter_context(tc.tile_pool(name="prod", bufs=4))
+        out_pool = ctx.enter_context(tc.tile_pool(name="outp", bufs=2))
+
+        def softmax_weights(band):
+            lg = lg_pool.tile([P, KK, NB], BF16)
+            nc.sync.dma_start(out=lg[:], in_=logits_v[:, :, band * NB : (band + 1) * NB])
+            top = lg_pool.tile([P, KK // 2, NB], BF16)
+            nc.vector.tensor_tensor(out=top[:], in0=lg[:, 0:24, :], in1=lg[:, 24:48, :], op=ALU.max)
+            for half in (12, 6, 3):
+                nc.vector.tensor_tensor(
+                    out=top[:, 0:half, :], in0=top[:, 0:half, :], in1=top[:, half : 2 * half, :], op=ALU.max
+                )
+            for other in (top[:, 1, :], top[:, 2, :], lg[:, KK - 1, :]):
+                nc.vector.tensor_tensor(out=top[:, 0, :], in0=top[:, 0, :], in1=other, op=ALU.max)
+            neg_top = stat_pool.tile([P, NB], F32)
+            nc.vector.tensor_scalar_mul(out=neg_top[:], in0=top[:, 0, :], scalar1=-1.0)
+            wgt = wgt_pool.tile([P, KK, NB], F32)
+            total = stat_pool.tile([P, NB], F32)
+            for n in range(NB):
+                nc.scalar.activation(
+                    out=wgt[:, :, n],
+                    in_=lg[:, :, n],
+                    func=ACT.Exp,
+                    bias=neg_top[:, n : n + 1],
+                    scale=1.0,
+                    accum_out=total[:, n : n + 1],
+                )
+            inv_total = stat_pool.tile([P, NB], F32)
+            nc.vector.reciprocal(out=inv_total[:], in_=total[:])
+            for n in range(NB):
+                nc.scalar.activation(
+                    out=wgt[:, :, n], in_=wgt[:, :, n], func=ACT.Copy, scale=inv_total[:, n : n + 1]
+                )
+            return wgt
+
+        def padded_map(band, g):
+            first_row = band * BAND - PAD
+            x3p = map_pool.tile([P, CG, ROWS, WP], F32)
+            for block in range(max(band - 1, 0), min(band + 1, BANDS - 1) + 1):
+                turned = turn_pool.tile([P, CG, B, HEADS], F32)
+                cols = slice(block * NB, (block + 1) * NB)
+                for b in range(B):
+                    x3t = stage.tile([P, HEADS * CG], F32, tag="stage")
+                    nc.tensor.matmul_mx(
+                        out=x3t[:],
+                        lhsT=x_codes[:, b, cols].bitcast(FP8X4),
+                        lhsT_scale=x_plane[:, b, cols],
+                        rhs=w_words[:, 2 * g * 512 : 2 * (g + 1) * 512].bitcast(FP4X4),
+                        rhs_scale=w_plane[:, g * 512 : (g + 1) * 512],
+                        start=True,
+                        stop=True,
+                    )
+                    nc.scalar.copy(out=turned[:, :, b, :], in_=x3t[:].rearrange("p (h c) -> p c h", c=CG))
+                lo = max(block * BAND, first_row)
+                hi = min((block + 1) * BAND, first_row + ROWS)
+                for bank in range(BANKS):
+                    x3 = stage.tile([P, PER_BANK, BAND, W], F32, tag="stage")
+                    for j in range(PER_BANK):
+                        nc.tensor.transpose(
+                            x3[:, j].rearrange("p r q -> p (r q)"),
+                            turned[:, bank * PER_BANK + j].rearrange("p b h -> p (b h)"),
+                            ident[:],
+                        )
+                    nc.scalar.copy(
+                        out=x3p[
+                            :, bank * PER_BANK : (bank + 1) * PER_BANK, lo - first_row : hi - first_row, PAD : PAD + W
+                        ],
+                        in_=x3[:, :, lo - block * BAND : hi - block * BAND, :],
+                    )
+            for r in range(ROWS):
+                src = reflect(first_row + r, H) - first_row
+                if src != r:
+                    nc.scalar.copy(out=x3p[:, :, r, PAD : PAD + W], in_=x3p[:, :, src, PAD : PAD + W])
+            for q in range(WP):
+                src = reflect(q - PAD, W) + PAD
+                if src != q:
+                    nc.scalar.copy(out=x3p[:, :, :, q : q + 1], in_=x3p[:, :, :, src : src + 1])
+            return x3p
+
+        def aggregate(band, g, wgt, x3p):
+            sums = [acc_pool.tile([P, PER_BANK, P], F32, name="sums%d" % bank) for bank in range(BANKS)]
+            for l in range(KK):
+                dy, dx = divmod(l, K)
+                prod = prod_pool.tile([P, CG, BAND, W], F32)
+                nc.vector.tensor_tensor(
+                    out=prod[:],
+                    in0=x3p[:, :, dy : dy + BAND, dx : dx + W],
+                    in1=wgt[:, l, :].rearrange("p (r q) -> p r q", q=W).unsqueeze(1).to_broadcast([P, CG, BAND, W]),
+                    op=ALU.mult,
+                )
+                for c in range(CG):
+                    bank, j = divmod(c, PER_BANK)
+                    nc.tensor.matmul(
+                        out=sums[bank][:, j, :],
+                        lhsT=prod[:, c].rearrange("p r q -> p (r q)"),
+                        rhs=ident[:],
+                        is_transpose=True,
+                        start=(l == 0 and j == 0),
+                        stop=(l == KK - 1 and j == PER_BANK - 1),
+                    )
+            sums_sb = out_pool.tile([P, CG, P], F32)
+            result = out_pool.tile([P, CG, NB], F32)
+            for bank in range(BANKS):
+                nc.scalar.copy(out=sums_sb[:, bank * PER_BANK : (bank + 1) * PER_BANK, :], in_=sums[bank][:])
+            for bank in range(BANKS):
+                back = stage.tile([P, PER_BANK, NB], F32, tag="stage")
+                for j in range(PER_BANK):
+                    nc.tensor.transpose(back[:, j, :], sums_sb[:, bank * PER_BANK + j, :], ident[:])
+                for j in range(PER_BANK):
+                    c = bank * PER_BANK + j
+                    nc.scalar.activation(
+                        out=result[:, c, :],
+                        in_=back[:, j, :],
+                        func=ACT.Identity,
+                        bias=bias[:, g * CG + c : g * CG + c + 1],
+                        scale=1.0,
+                    )
+            nc.sync.dma_start(
+                out=out_v[:, g * CG : (g + 1) * CG, band * NB : (band + 1) * NB], in_=result[:]
+            )
+
+        units = [(band, g) for band in range(BANDS) for g in range(GROUPS)]
+        wgt = softmax_weights(0)
+        x3p = padded_map(0, 0)
+        for i, (band, g) in enumerate(units):
+            next_wgt, next_x3p = wgt, None
+            if i + 1 < len(units):
+                next_x3p = padded_map(units[i + 1][0], units[i + 1][1])
+                if units[i + 1][0] != band:
+                    next_wgt = softmax_weights(units[i + 1][0])
+            aggregate(band, g, wgt, x3p)
+            wgt, x3p = next_wgt, next_x3p

@@ -27,10 +27,20 @@ NB = BAND * W
 BANDS = H // BAND
 ROWS = BAND + 2 * PAD
 WP = W + 2 * PAD
+HP = H + 2 * PAD
+NPAD = HP * W
 CG = 16
 GROUPS = SP // CG
 PER_BANK = 4
 BANKS = CG // PER_BANK
+LP = 52
+
+LG = [l for l in range(KK) if l % 3 == 1] + [KK - 1]
+LV = [l for l in range(KK) if l not in LG]
+NG = len(LG)
+NV = len(LV)
+VGROUPS = NV // PER_BANK
+GCHUNKS = [LG[i : i + PER_BANK] for i in range(0, NG, PER_BANK)]
 
 FLOPS = 2 * B * COUT * HW * CIN + 2 * B * COUT * HW * KK
 
@@ -47,146 +57,330 @@ def tile_sam_pb_t_kernel(tc, logits, x, w3c_words, w3c_scales, b3c, out):
     nc = tc.nc
     logits_v = logits.rearrange("b h l n -> (b h) l n")
     out_v = out.rearrange("b (h c) i j -> (b h) c (i j)", c=SP)
+    units = [(band, g) for band in range(BANDS) for g in range(GROUPS)]
 
     with ExitStack() as ctx:
+        ctx.enter_context(tc.manual_schedule())
         const = ctx.enter_context(tc.tile_pool(name="const", bufs=1))
         lg_pool = ctx.enter_context(tc.tile_pool(name="lg", bufs=1))
         stat_pool = ctx.enter_context(tc.tile_pool(name="stat", bufs=2))
-        wgt_pool = ctx.enter_context(tc.tile_pool(name="wgt", bufs=2))
+        wtg_pool = ctx.enter_context(tc.tile_pool(name="wtg", bufs=3))
+        wgtg_pool = ctx.enter_context(tc.tile_pool(name="wgtg", bufs=2))
+        turn_pool = ctx.enter_context(tc.tile_pool(name="turn", bufs=1))
         acc_pool = ctx.enter_context(tc.psum_pool(name="acc", bufs=1))
-        stage = ctx.enter_context(tc.psum_pool(name="stage", bufs=4))
+        wps_pool = ctx.enter_context(tc.psum_pool(name="wps", bufs=2))
+        stage = ctx.enter_context(tc.psum_pool(name="stage", bufs=2))
 
         ident = const.tile([P, P], F32)
         make_identity(nc, ident[:])
 
         w_words = const.tile([P, 2 * COUT], U8, align_bytes=64)
         w_plane = const.tile([P, COUT], U8, align_bytes=64)
-        nc.vector.memset(w_plane[:].bitcast(I32), 0)
-        words_src = w3c_words[0].bitcast(I32).rearrange("p (h g w) -> p g h w", g=GROUPS, h=HEADS)
-        words_dst = w_words[:].bitcast(I32).rearrange("p (g h w) -> p g h w", g=GROUPS, h=HEADS)
-        scales_src = w3c_scales[0].bitcast(I32).rearrange("q (h g w) -> q g h w", g=GROUPS, h=HEADS)
-        for g in range(GROUPS):
-            nc.sync.dma_start(out=words_dst[:, g], in_=words_src[:, g])
-        for quad in range(4):
-            plane_dst = w_plane[32 * quad : 32 * quad + 4, :].bitcast(I32)
-            plane_dst = plane_dst.rearrange("q (g h w) -> q g h w", g=GROUPS, h=HEADS)
-            for g in range(GROUPS):
-                nc.sync.dma_start(out=plane_dst[:, g], in_=scales_src[4 * quad : 4 * quad + 4, g])
-
         bias_bf = const.tile([P, SP], BF16)
-        for b in range(B):
-            nc.sync.dma_start(
-                out=bias_bf[b * HEADS : (b + 1) * HEADS, :], in_=b3c.rearrange("(h c) -> h c", c=SP)
-            )
         bias = const.tile([P, SP], F32)
-        nc.vector.tensor_copy(out=bias[:], in_=bias_bf[:])
+        x_codes = const.tile([P, B, NPAD], U32, align_bytes=64)
+        x_plane = const.tile([P, B, NPAD], U8, align_bytes=64)
+        neg_top = const.tile([P, HW], F32)
+        w_nl = const.tile([P, NB, LP], F32)
+        wtv = const.tile([P, NV, P], F32)
+        x3p_a = const.tile([P, CG, ROWS, WP], F32)
+        x3p_b = const.tile([P, CG, ROWS, WP], F32)
+        x3p = [x3p_a, x3p_b]
 
-        x_codes = const.tile([P, B, HW], U32, align_bytes=64)
-        x_plane = const.tile([P, B, HW], U8, align_bytes=64)
-        with tc.tile_pool(name="xin", bufs=2) as xin:
-            for b in range(B):
-                raw = xin.tile([P, PACK, HW], BF16)
-                nc.sync.dma_start(out=raw[:], in_=x[b].rearrange("(p t) i j -> p t (i j)", t=PACK))
-                grouped = xin.tile([P, HW, PACK], BF16, align_bytes=64)
-                nc.vector.tensor_copy(out=grouped[:], in_=raw[:].rearrange("p t n -> p n t"))
-                nc.vector.quantize_mx(
-                    out=x_codes[:, b, :].bitcast(FP8X4),
-                    scales=x_plane[:, b, :],
-                    in_=grouped[:].rearrange("p n t -> p (n t)"),
-                )
-
-        map_pool = ctx.enter_context(tc.tile_pool(name="map", bufs=2))
-        turn_pool = ctx.enter_context(tc.tile_pool(name="turn", bufs=2))
-        prod_pool = ctx.enter_context(tc.tile_pool(name="prod", bufs=4))
-        out_pool = ctx.enter_context(tc.tile_pool(name="outp", bufs=2))
-
-        def softmax_weights(band):
-            lg = lg_pool.tile([P, KK, NB], BF16)
+        def softmax_load(band, st):
+            lg = lg_pool.tile([P, KK, NB], BF16, name="lg")
             nc.sync.dma_start(out=lg[:], in_=logits_v[:, :, band * NB : (band + 1) * NB])
-            top = lg_pool.tile([P, KK // 2, NB], BF16)
-            nc.vector.tensor_tensor(out=top[:], in0=lg[:, 0:24, :], in1=lg[:, 24:48, :], op=ALU.max)
-            for half in (12, 6, 3):
-                nc.vector.tensor_tensor(
-                    out=top[:, 0:half, :], in0=top[:, 0:half, :], in1=top[:, half : 2 * half, :], op=ALU.max
-                )
-            for other in (top[:, 1, :], top[:, 2, :], lg[:, KK - 1, :]):
-                nc.vector.tensor_tensor(out=top[:, 0, :], in0=top[:, 0, :], in1=other, op=ALU.max)
-            neg_top = stat_pool.tile([P, NB], F32)
-            nc.vector.tensor_scalar_mul(out=neg_top[:], in0=top[:, 0, :], scalar1=-1.0)
-            wgt = wgt_pool.tile([P, KK, NB], F32)
-            total = stat_pool.tile([P, NB], F32)
-            for n in range(NB):
-                nc.scalar.activation(
-                    out=wgt[:, :, n],
-                    in_=lg[:, :, n],
-                    func=ACT.Exp,
-                    bias=neg_top[:, n : n + 1],
-                    scale=1.0,
-                    accum_out=total[:, n : n + 1],
-                )
-            inv_total = stat_pool.tile([P, NB], F32)
-            nc.vector.reciprocal(out=inv_total[:], in_=total[:])
-            for n in range(NB):
-                nc.scalar.activation(
-                    out=wgt[:, :, n], in_=wgt[:, :, n], func=ACT.Copy, scale=inv_total[:, n : n + 1]
-                )
-            return wgt
+            total = stat_pool.tile([P, NB], F32, name="total")
+            st["lg"] = lg
+            st["total"] = total
 
-        def padded_map(band, g):
-            first_row = band * BAND - PAD
-            x3p = map_pool.tile([P, CG, ROWS, WP], F32)
-            for block in range(max(band - 1, 0), min(band + 1, BANDS - 1) + 1):
-                turned = turn_pool.tile([P, CG, B, HEADS], F32)
-                cols = slice(block * NB, (block + 1) * NB)
-                for b in range(B):
-                    x3t = stage.tile([P, HEADS * CG], F32, tag="stage")
-                    nc.tensor.matmul_mx(
-                        out=x3t[:],
-                        lhsT=x_codes[:, b, cols].bitcast(FP8X4),
-                        lhsT_scale=x_plane[:, b, cols],
-                        rhs=w_words[:, 2 * g * 512 : 2 * (g + 1) * 512].bitcast(FP4X4),
-                        rhs_scale=w_plane[:, g * 512 : (g + 1) * 512],
-                        start=True,
-                        stop=True,
+        def softmax_exp(band, st, n0, n1):
+            for n in range(n0, n1):
+                nc.scalar.activation(
+                    out=w_nl[:, n, 0:KK],
+                    in_=st["lg"][:, :, n],
+                    func=ACT.Exp,
+                    bias=neg_top[:, band * NB + n : band * NB + n + 1],
+                    scale=1.0,
+                    accum_out=st["total"][:, n : n + 1],
+                )
+
+        def softmax_recip(st):
+            inv_total = stat_pool.tile([P, NB], F32, name="inv_total")
+            nc.vector.reciprocal(out=inv_total[:], in_=st["total"][:])
+            st["inv"] = inv_total
+
+        def softmax_norm(st, n0, n1):
+            for n in range(n0, n1):
+                nc.scalar.activation(
+                    out=w_nl[:, n, 0:KK], in_=w_nl[:, n, 0:KK], func=ACT.Copy, scale=st["inv"][:, n : n + 1]
+                )
+
+        def turn_weights(ls, dest):
+            ps = stage.tile([P, PER_BANK, P], F32, tag="stage")
+            for j, l in enumerate(ls):
+                nc.tensor.transpose(ps[:, j, :], w_nl[:, :, l], ident[:])
+            nc.scalar.copy(out=dest, in_=ps[:, 0 : len(ls), :])
+
+        def spread_tasks(st):
+            def v_task(k):
+                return lambda: turn_weights(LV[PER_BANK * k : PER_BANK * (k + 1)], wtv[:, PER_BANK * k : PER_BANK * (k + 1), :])
+
+            def ga(i):
+                wtg = wtg_pool.tile([P, PER_BANK, P], F32, name="wtg")
+                st["wtg%d" % i] = wtg
+                turn_weights(GCHUNKS[i], wtg[:, 0 : len(GCHUNKS[i]), :])
+
+            def gb(i):
+                if i == 0:
+                    wgtg = wgtg_pool.tile([P, NG, NB], F32, name="wgtg")
+                    st["wgtg"] = wgtg
+                cnt = len(GCHUNKS[i])
+                ps = stage.tile([P, PER_BANK, NB], F32, tag="stage")
+                for j in range(cnt):
+                    nc.tensor.transpose(ps[:, j, :], st["wtg%d" % i][:, j, :], ident[:])
+                nc.scalar.copy(out=st["wgtg"][:, PER_BANK * i : PER_BANK * i + cnt, :], in_=ps[:, 0:cnt, :])
+
+            def ga_task(i):
+                return lambda: ga(i)
+
+            def gb_task(i):
+                return lambda: gb(i)
+
+            return (
+                [v_task(k) for k in range(5)]
+                + [ga_task(0), ga_task(1), gb_task(0), ga_task(2), gb_task(1)]
+                + [v_task(k) for k in range(5, VGROUPS)]
+                + [ga_task(3), gb_task(2), ga_task(4), gb_task(3), gb_task(4)]
+            )
+
+        def load_wps(k):
+            wps = wps_pool.tile([P, PER_BANK, NB], F32, name="wps")
+            for j in range(PER_BANK):
+                nc.tensor.transpose(wps[:, j, :], wtv[:, PER_BANK * k + j, :], ident[:])
+            return wps
+
+        def window_tasks(g, row0, dst0, nrows):
+            st = {}
+            cols = slice(row0 * W, row0 * W + NB)
+
+            def mx(b):
+                if b == 0:
+                    turned = turn_pool.tile([P, CG, B, HEADS], F32, name="turned")
+                    st["turned"] = turned
+                x3t = stage.tile([P, HEADS * CG], F32, tag="stage")
+                nc.tensor.matmul_mx(
+                    out=x3t[:],
+                    lhsT=x_codes[:, b, cols].bitcast(FP8X4),
+                    lhsT_scale=x_plane[:, b, cols],
+                    rhs=w_words[:, 2 * g * 512 : 2 * (g + 1) * 512].bitcast(FP4X4),
+                    rhs_scale=w_plane[:, g * 512 : (g + 1) * 512],
+                    start=True,
+                    stop=True,
+                )
+                nc.scalar.copy(out=st["turned"][:, :, b, :], in_=x3t[:].rearrange("p (h c) -> p c h", c=CG))
+
+            def turn(bank):
+                x3 = stage.tile([P, PER_BANK, BAND, W], F32, tag="stage")
+                for j in range(PER_BANK):
+                    nc.tensor.transpose(
+                        x3[:, j].rearrange("p r q -> p (r q)"),
+                        st["turned"][:, bank * PER_BANK + j].rearrange("p b h -> p (b h)"),
+                        ident[:],
                     )
-                    nc.scalar.copy(out=turned[:, :, b, :], in_=x3t[:].rearrange("p (h c) -> p c h", c=CG))
-                lo = max(block * BAND, first_row)
-                hi = min((block + 1) * BAND, first_row + ROWS)
-                for bank in range(BANKS):
-                    x3 = stage.tile([P, PER_BANK, BAND, W], F32, tag="stage")
-                    for j in range(PER_BANK):
-                        nc.tensor.transpose(
-                            x3[:, j].rearrange("p r q -> p (r q)"),
-                            turned[:, bank * PER_BANK + j].rearrange("p b h -> p (b h)"),
-                            ident[:],
-                        )
-                    nc.scalar.copy(
-                        out=x3p[
-                            :, bank * PER_BANK : (bank + 1) * PER_BANK, lo - first_row : hi - first_row, PAD : PAD + W
-                        ],
-                        in_=x3[:, :, lo - block * BAND : hi - block * BAND, :],
-                    )
-            for r in range(ROWS):
-                src = reflect(first_row + r, H) - first_row
-                if src != r:
-                    nc.scalar.copy(out=x3p[:, :, r, PAD : PAD + W], in_=x3p[:, :, src, PAD : PAD + W])
+                nc.scalar.copy(
+                    out=x3p[g][:, bank * PER_BANK : (bank + 1) * PER_BANK, dst0 : dst0 + nrows, PAD : PAD + W],
+                    in_=x3[:, :, 0:nrows, :],
+                )
+
+            def mx_task(b):
+                return lambda: mx(b)
+
+            def turn_task(bank):
+                return lambda: turn(bank)
+
+            return [mx_task(b) for b in range(B)] + [turn_task(bank) for bank in range(BANKS)]
+
+        def pad_columns(g, r0, r1):
             for q in range(WP):
                 src = reflect(q - PAD, W) + PAD
                 if src != q:
-                    nc.scalar.copy(out=x3p[:, :, :, q : q + 1], in_=x3p[:, :, :, src : src + 1])
-            return x3p
+                    nc.scalar.copy(out=x3p[g][:, :, r0:r1, q : q + 1], in_=x3p[g][:, :, r0:r1, src : src + 1])
 
-        def aggregate(band, g, wgt, x3p):
-            sums = [acc_pool.tile([P, PER_BANK, P], F32, name="sums%d" % bank) for bank in range(BANKS)]
-            for l in range(KK):
-                dy, dx = divmod(l, K)
-                prod = prod_pool.tile([P, CG, BAND, W], F32)
-                nc.vector.tensor_tensor(
-                    out=prod[:],
-                    in0=x3p[:, :, dy : dy + BAND, dx : dx + W],
-                    in1=wgt[:, l, :].rearrange("p (r q) -> p r q", q=W).unsqueeze(1).to_broadcast([P, CG, BAND, W]),
-                    op=ALU.mult,
+        def roll(g, part):
+            if part == 0:
+                nc.scalar.copy(out=x3p[g][:, :, 0:BAND, :], in_=x3p[g][:, :, BAND : 2 * BAND, :])
+            else:
+                nc.scalar.copy(out=x3p[g][:, :, BAND : ROWS - BAND, :], in_=x3p[g][:, :, 2 * BAND : ROWS, :])
+
+        def first_map_tasks(g):
+            return (
+                window_tasks(g, 0, 0, BAND)
+                + window_tasks(g, BAND, BAND, BAND)
+                + window_tasks(g, 2 * BAND, 2 * BAND, ROWS - 2 * BAND)
+                + [lambda: pad_columns(g, 0, ROWS)]
+            )
+
+        state = {0: {}}
+        with tc.tile_pool(name="xin", bufs=2) as xin, tc.tile_pool(name="xg", bufs=1) as xg, tc.tile_pool(
+            name="lgp", bufs=2
+        ) as lgp:
+
+            def load_early(band):
+                lge = lgp.tile([P, KK, NB], BF16, name="lge")
+                nc.sync.dma_start(out=lge[:], in_=logits_v[:, :, band * NB : (band + 1) * NB])
+                return lge
+
+            def top_of(band, lge):
+                top = xg.tile([P, KK // 2, NB], BF16, name="top")
+                nc.vector.tensor_tensor(out=top[:], in0=lge[:, 0:24, :], in1=lge[:, 24:48, :], op=ALU.max)
+                for half in (12, 6, 3):
+                    nc.vector.tensor_tensor(
+                        out=top[:, 0:half, :], in0=top[:, 0:half, :], in1=top[:, half : 2 * half, :], op=ALU.max
+                    )
+                for other in (top[:, 1, :], top[:, 2, :], lge[:, KK - 1, :]):
+                    nc.vector.tensor_tensor(out=top[:, 0, :], in0=top[:, 0, :], in1=other, op=ALU.max)
+                nc.vector.tensor_scalar_mul(
+                    out=neg_top[:, band * NB : (band + 1) * NB], in0=top[:, 0, :], scalar1=-1.0
                 )
+
+            def load_x(b):
+                raw = xin.tile([P, PACK, HW], BF16, name="raw")
+                nc.sync.dma_start(out=raw[:], in_=x[b].rearrange("(p t) i j -> p t (i j)", t=PACK))
+                return raw
+
+            def quantise_x(b, raw):
+                grouped = xg.tile([P, NPAD, PACK], BF16, align_bytes=64, name="grouped")
+                nc.vector.tensor_copy(
+                    out=grouped[:, PAD * W : PAD * W + HW, :], in_=raw[:].rearrange("p t n -> p n t")
+                )
+                for r in range(HP):
+                    src = reflect(r - PAD, H) + PAD
+                    if src != r:
+                        nc.vector.tensor_copy(
+                            out=grouped[:, r * W : (r + 1) * W, :], in_=grouped[:, src * W : (src + 1) * W, :]
+                        )
+                flat = grouped[:].rearrange("p n t -> p (n t)")
+                first = 0
+                for width in (1024, 128, 64):
+                    nc.vector.quantize_mx(
+                        out=x_codes[:, b, first : first + width].bitcast(FP8X4),
+                        scales=x_plane[:, b, first : first + width],
+                        in_=flat[:, PACK * first : PACK * (first + width)],
+                    )
+                    first += width
+
+            early = {0: load_early(0)}
+            softmax_load(0, state[0])
+            nc.vector.memset(w_plane[:].bitcast(I32), 0)
+            words_src = w3c_words[0].bitcast(I32).rearrange("p (h g w) -> p g h w", g=GROUPS, h=HEADS)
+            words_dst = w_words[:].bitcast(I32).rearrange("p (g h w) -> p g h w", g=GROUPS, h=HEADS)
+            scales_src = w3c_scales[0].bitcast(I32).rearrange("q (h g w) -> q g h w", g=GROUPS, h=HEADS)
+            raws = {0: load_x(0), 1: load_x(1)}
+            for g in range(GROUPS):
+                nc.sync.dma_start(out=words_dst[:, g], in_=words_src[:, g])
+            for quad in range(4):
+                plane_dst = w_plane[32 * quad : 32 * quad + 4, :].bitcast(I32)
+                plane_dst = plane_dst.rearrange("q (g h w) -> q g h w", g=GROUPS, h=HEADS)
+                for g in range(GROUPS):
+                    nc.sync.dma_start(out=plane_dst[:, g], in_=scales_src[4 * quad : 4 * quad + 4, g])
+            for b in range(B):
+                nc.sync.dma_start(
+                    out=bias_bf[b * HEADS : (b + 1) * HEADS, :], in_=b3c.rearrange("(h c) -> h c", c=SP)
+                )
+            early[1] = load_early(1)
+
+            top_of(0, early[0])
+            softmax_exp(0, state[0], 0, NB)
+            early[2] = load_early(2)
+            for b in range(B):
+                quantise_x(b, raws[b])
+                if b + 2 < B:
+                    raws[b + 2] = load_x(b + 2)
+            nc.vector.tensor_copy(out=bias[:], in_=bias_bf[:])
+            for t in first_map_tasks(0):
+                t()
+            top_of(1, early[1])
+            early[3] = load_early(3)
+            softmax_recip(state[0])
+            softmax_norm(state[0], 0, NB)
+            for band in range(2, BANDS):
+                top_of(band, early[band])
+                if band + 2 < BANDS:
+                    early[band + 2] = load_early(band + 2)
+            for t in spread_tasks(state[0]):
+                t()
+
+        prodv_pool = ctx.enter_context(tc.tile_pool(name="prodv", bufs=4))
+        prodg_pool = ctx.enter_context(tc.tile_pool(name="prodg", bufs=2))
+        sums_pool = ctx.enter_context(tc.tile_pool(name="sums", bufs=1))
+        res_pool = ctx.enter_context(tc.tile_pool(name="res", bufs=2))
+
+        def back_task(band, g, sums_sb, bank):
+            def run():
+                back = stage.tile([P, PER_BANK, NB], F32, tag="stage")
+                for j in range(PER_BANK):
+                    nc.tensor.transpose(back[:, j, :], sums_sb[:, bank * PER_BANK + j, :], ident[:])
+                result = res_pool.tile([P, PER_BANK, NB], F32, name="result")
+                for j in range(PER_BANK):
+                    c = g * CG + bank * PER_BANK + j
+                    nc.scalar.activation(
+                        out=result[:, j, :], in_=back[:, j, :], func=ACT.Identity, bias=bias[:, c : c + 1], scale=1.0
+                    )
+                c0 = g * CG + bank * PER_BANK
+                nc.sync.dma_start(out=out_v[:, c0 : c0 + PER_BANK, band * NB : (band + 1) * NB], in_=result[:])
+
+            return run
+
+        def put(side, step, task):
+            side.setdefault(step, []).append(task)
+
+        def window(g, l):
+            dy, dx = divmod(l, K)
+            return x3p[g][:, :, dy : dy + BAND, dx : dx + W]
+
+        def spread(row):
+            return row.rearrange("p (r q) -> p r q", q=W).unsqueeze(1).to_broadcast([P, CG, BAND, W])
+
+        wps_of = {(0, 0): load_wps(0), (0, 1): load_wps(1)}
+        finish = []
+        for u, (band, g) in enumerate(units):
+            small = {}
+            side = {}
+            for i, t in enumerate(finish):
+                put(side, i, t)
+            if u == 0:
+                for i, t in enumerate(first_map_tasks(1)):
+                    put(side, i, t)
+            elif u + 1 < len(units):
+                nband, ng = units[u + 1]
+                put(small, 1, lambda ng=ng: roll(ng, 0))
+                put(small, 2, lambda ng=ng: roll(ng, 1))
+                for i, t in enumerate(window_tasks(ng, BAND * nband + ROWS - BAND, ROWS - BAND, BAND)):
+                    put(side, 4 + i, t)
+                put(side, 12, lambda ng=ng: pad_columns(ng, ROWS - BAND, ROWS))
+            if band + 1 < BANDS:
+                if g == 0:
+                    state[band + 1] = {}
+                    st = state[band + 1]
+                    put(small, 0, lambda st=st, nb=band + 1: softmax_load(nb, st))
+                    for i in range(22):
+                        put(small, 1 + i, lambda st=st, nb=band + 1, i=i: softmax_exp(nb, st, 6 * i, min(6 * i + 6, NB)))
+                    put(small, 24, lambda st=st: softmax_recip(st))
+                    for i in range(7):
+                        put(small, 25 + i, lambda st=st, i=i: softmax_norm(st, 8 * i, 8 * i + 8))
+                else:
+                    st = state[band + 1]
+                    for i in range(7, 16):
+                        put(small, i - 7, lambda st=st, i=i: softmax_norm(st, 8 * i, 8 * i + 8))
+                    for i, t in enumerate(spread_tasks(st)):
+                        put(side, 12 + i, t)
+
+            sums = [acc_pool.tile([P, PER_BANK, P], F32, name="sums%d" % bank) for bank in range(BANKS)]
+            wgtg = state[band]["wgtg"]
+            added = [0]
+
+            def add(prod):
                 for c in range(CG):
                     bank, j = divmod(c, PER_BANK)
                     nc.tensor.matmul(
@@ -194,38 +388,47 @@ def tile_sam_pb_t_kernel(tc, logits, x, w3c_words, w3c_scales, b3c, out):
                         lhsT=prod[:, c].rearrange("p r q -> p (r q)"),
                         rhs=ident[:],
                         is_transpose=True,
-                        start=(l == 0 and j == 0),
-                        stop=(l == KK - 1 and j == PER_BANK - 1),
+                        start=(added[0] == 0 and j == 0),
+                        stop=(added[0] == KK - 1 and j == PER_BANK - 1),
                     )
-            sums_sb = out_pool.tile([P, CG, P], F32)
-            result = out_pool.tile([P, CG, NB], F32)
+                added[0] += 1
+
+            issued = 0
+            taken = 0
+            prodg = {}
+            for s in range(NV):
+                while issued < NG and issued * NV <= s * NG:
+                    pg = prodg_pool.tile([P, CG, BAND, W], F32, name="pg")
+                    nc.gpsimd.tensor_tensor(
+                        out=pg[:], in0=window(g, LG[issued]), in1=spread(wgtg[:, issued, :]), op=ALU.mult
+                    )
+                    prodg[issued] = pg
+                    issued += 1
+                pv = prodv_pool.tile([P, CG, BAND, W], F32, name="pv")
+                nc.vector.tensor_tensor(
+                    out=pv[:],
+                    in0=window(g, LV[s]),
+                    in1=spread(wps_of[(u, s // PER_BANK)][:, s % PER_BANK, :]),
+                    op=ALU.mult,
+                )
+                for t in small.get(s, []):
+                    t()
+                add(pv)
+                while taken < NG and (taken + 1) * NV <= (s + 1) * NG:
+                    add(prodg[taken])
+                    taken += 1
+                if s % PER_BANK == PER_BANK - 1:
+                    k = s // PER_BANK + 2
+                    if k < VGROUPS:
+                        wps_of[(u, k)] = load_wps(k)
+                    elif u + 1 < len(units):
+                        wps_of[(u + 1, k - VGROUPS)] = load_wps(k - VGROUPS)
+                for t in side.get(s, []):
+                    t()
+
+            sums_sb = sums_pool.tile([P, CG, P], F32, name="sums_sb")
             for bank in range(BANKS):
                 nc.scalar.copy(out=sums_sb[:, bank * PER_BANK : (bank + 1) * PER_BANK, :], in_=sums[bank][:])
-            for bank in range(BANKS):
-                back = stage.tile([P, PER_BANK, NB], F32, tag="stage")
-                for j in range(PER_BANK):
-                    nc.tensor.transpose(back[:, j, :], sums_sb[:, bank * PER_BANK + j, :], ident[:])
-                for j in range(PER_BANK):
-                    c = bank * PER_BANK + j
-                    nc.scalar.activation(
-                        out=result[:, c, :],
-                        in_=back[:, j, :],
-                        func=ACT.Identity,
-                        bias=bias[:, g * CG + c : g * CG + c + 1],
-                        scale=1.0,
-                    )
-            nc.sync.dma_start(
-                out=out_v[:, g * CG : (g + 1) * CG, band * NB : (band + 1) * NB], in_=result[:]
-            )
-
-        units = [(band, g) for band in range(BANDS) for g in range(GROUPS)]
-        wgt = softmax_weights(0)
-        x3p = padded_map(0, 0)
-        for i, (band, g) in enumerate(units):
-            next_wgt, next_x3p = wgt, None
-            if i + 1 < len(units):
-                next_x3p = padded_map(units[i + 1][0], units[i + 1][1])
-                if units[i + 1][0] != band:
-                    next_wgt = softmax_weights(units[i + 1][0])
-            aggregate(band, g, wgt, x3p)
-            wgt, x3p = next_wgt, next_x3p
+            finish = [back_task(band, g, sums_sb, bank) for bank in range(BANKS)]
+        for t in finish:
+            t()

@@ -35,12 +35,14 @@ PER_BANK = 4
 BANKS = CG // PER_BANK
 LP = 52
 
-LG = [l for l in range(KK) if l % 3 == 1] + [KK - 1]
+GSTEP = 3
+NG = 16
+LG = [GSTEP * i for i in range(NG)]
 LV = [l for l in range(KK) if l not in LG]
-NG = len(LG)
 NV = len(LV)
-VGROUPS = NV // PER_BANK
-GCHUNKS = [LG[i : i + PER_BANK] for i in range(0, NG, PER_BANK)]
+NCHUNKS = -(-NV // PER_BANK)
+CSTART = [k * NV // NCHUNKS for k in range(NCHUNKS + 1)]
+CHUNK_OF = [k for k in range(NCHUNKS) for s in range(CSTART[k], CSTART[k + 1])]
 
 FLOPS = 2 * B * COUT * HW * CIN + 2 * B * COUT * HW * KK
 
@@ -64,7 +66,6 @@ def tile_sam_pb_t_kernel(tc, logits, x, w3c_words, w3c_scales, b3c, out):
         const = ctx.enter_context(tc.tile_pool(name="const", bufs=1))
         lg_pool = ctx.enter_context(tc.tile_pool(name="lg", bufs=1))
         stat_pool = ctx.enter_context(tc.tile_pool(name="stat", bufs=2))
-        wtg_pool = ctx.enter_context(tc.tile_pool(name="wtg", bufs=3))
         wgtg_pool = ctx.enter_context(tc.tile_pool(name="wgtg", bufs=2))
         turn_pool = ctx.enter_context(tc.tile_pool(name="turn", bufs=1))
         acc_pool = ctx.enter_context(tc.psum_pool(name="acc", bufs=1))
@@ -122,42 +123,23 @@ def tile_sam_pb_t_kernel(tc, logits, x, w3c_words, w3c_scales, b3c, out):
                 nc.tensor.transpose(ps[:, j, :], w_nl[:, :, l], ident[:])
             nc.scalar.copy(out=dest, in_=ps[:, 0 : len(ls), :])
 
-        def spread_tasks(st):
-            def v_task(k):
-                return lambda: turn_weights(LV[PER_BANK * k : PER_BANK * (k + 1)], wtv[:, PER_BANK * k : PER_BANK * (k + 1), :])
+        def v_task(k):
+            return lambda: turn_weights(LV[CSTART[k] : CSTART[k + 1]], wtv[:, CSTART[k] : CSTART[k + 1], :])
 
-            def ga(i):
-                wtg = wtg_pool.tile([P, PER_BANK, P], F32, name="wtg")
-                st["wtg%d" % i] = wtg
-                turn_weights(GCHUNKS[i], wtg[:, 0 : len(GCHUNKS[i]), :])
-
-            def gb(i):
-                if i == 0:
-                    wgtg = wgtg_pool.tile([P, NG, NB], F32, name="wgtg")
-                    st["wgtg"] = wgtg
-                cnt = len(GCHUNKS[i])
-                ps = stage.tile([P, PER_BANK, NB], F32, tag="stage")
-                for j in range(cnt):
-                    nc.tensor.transpose(ps[:, j, :], st["wtg%d" % i][:, j, :], ident[:])
-                nc.scalar.copy(out=st["wgtg"][:, PER_BANK * i : PER_BANK * i + cnt, :], in_=ps[:, 0:cnt, :])
-
-            def ga_task(i):
-                return lambda: ga(i)
-
-            def gb_task(i):
-                return lambda: gb(i)
-
-            return (
-                [v_task(k) for k in range(5)]
-                + [ga_task(0), ga_task(1), gb_task(0), ga_task(2), gb_task(1)]
-                + [v_task(k) for k in range(5, VGROUPS)]
-                + [ga_task(3), gb_task(2), ga_task(4), gb_task(3), gb_task(4)]
+        def gpsimd_weights(st, part):
+            if part == 0:
+                wgtg = wgtg_pool.tile([P, NG, NB], F32, name="wgtg")
+                st["wgtg"] = wgtg
+            half = NB // 2
+            cols = slice(part * half, (part + 1) * half)
+            nc.scalar.copy(
+                out=st["wgtg"][:, :, cols], in_=w_nl[:, cols, 0 : GSTEP * NG : GSTEP].rearrange("p n l -> p l n")
             )
 
         def load_wps(k):
             wps = wps_pool.tile([P, PER_BANK, NB], F32, name="wps")
-            for j in range(PER_BANK):
-                nc.tensor.transpose(wps[:, j, :], wtv[:, PER_BANK * k + j, :], ident[:])
+            for j in range(CSTART[k + 1] - CSTART[k]):
+                nc.tensor.transpose(wps[:, j, :], wtv[:, CSTART[k] + j, :], ident[:])
             return wps
 
         def window_tasks(g, row0, dst0, nrows):
@@ -308,8 +290,10 @@ def tile_sam_pb_t_kernel(tc, logits, x, w3c_words, w3c_scales, b3c, out):
                 top_of(band, early[band])
                 if band + 2 < BANDS:
                     early[band + 2] = load_early(band + 2)
-            for t in spread_tasks(state[0]):
-                t()
+            gpsimd_weights(state[0], 0)
+            gpsimd_weights(state[0], 1)
+            for k in range(NCHUNKS):
+                v_task(k)()
 
         prodv_pool = ctx.enter_context(tc.tile_pool(name="prodv", bufs=4))
         prodg_pool = ctx.enter_context(tc.tile_pool(name="prodg", bufs=2))
@@ -373,8 +357,10 @@ def tile_sam_pb_t_kernel(tc, logits, x, w3c_words, w3c_scales, b3c, out):
                     st = state[band + 1]
                     for i in range(7, 16):
                         put(small, i - 7, lambda st=st, i=i: softmax_norm(st, 8 * i, 8 * i + 8))
-                    for i, t in enumerate(spread_tasks(st)):
-                        put(side, 12 + i, t)
+                    put(small, 10, lambda st=st: gpsimd_weights(st, 0))
+                    put(small, 11, lambda st=st: gpsimd_weights(st, 1))
+                    for k in range(NCHUNKS):
+                        put(side, max(12 + k, CSTART[max(k - 1, 0)]), v_task(k))
 
             sums = [acc_pool.tile([P, PER_BANK, P], F32, name="sums%d" % bank) for bank in range(BANKS)]
             wgtg = state[band]["wgtg"]
@@ -408,7 +394,7 @@ def tile_sam_pb_t_kernel(tc, logits, x, w3c_words, w3c_scales, b3c, out):
                 nc.vector.tensor_tensor(
                     out=pv[:],
                     in0=window(g, LV[s]),
-                    in1=spread(wps_of[(u, s // PER_BANK)][:, s % PER_BANK, :]),
+                    in1=spread(wps_of[(u, CHUNK_OF[s])][:, s - CSTART[CHUNK_OF[s]], :]),
                     op=ALU.mult,
                 )
                 for t in small.get(s, []):
@@ -417,12 +403,12 @@ def tile_sam_pb_t_kernel(tc, logits, x, w3c_words, w3c_scales, b3c, out):
                 while taken < NG and (taken + 1) * NV <= (s + 1) * NG:
                     add(prodg[taken])
                     taken += 1
-                if s % PER_BANK == PER_BANK - 1:
-                    k = s // PER_BANK + 2
-                    if k < VGROUPS:
+                if s + 1 == CSTART[CHUNK_OF[s] + 1]:
+                    k = CHUNK_OF[s] + 2
+                    if k < NCHUNKS:
                         wps_of[(u, k)] = load_wps(k)
                     elif u + 1 < len(units):
-                        wps_of[(u + 1, k - VGROUPS)] = load_wps(k - VGROUPS)
+                        wps_of[(u + 1, k - NCHUNKS)] = load_wps(k - NCHUNKS)
                 for t in side.get(s, []):
                     t()
 

@@ -38,7 +38,8 @@ LP = 52
 GSTEP = 3
 NG = 16
 LG = [GSTEP * i for i in range(NG)]
-LV = [l for l in range(KK) if l not in LG]
+CV = 5
+LV = [l for l in range(KK) if l not in LG] + [LG[NG - 1]]
 NV = len(LV)
 NCHUNKS = -(-NV // PER_BANK)
 CSTART = [k * NV // NCHUNKS for k in range(NCHUNKS + 1)]
@@ -319,12 +320,12 @@ def tile_sam_pb_t_kernel(tc, logits, x, w3c_words, w3c_scales, b3c, out):
         def put(side, step, task):
             side.setdefault(step, []).append(task)
 
-        def window(g, l):
+        def window(g, l, c0, c1):
             dy, dx = divmod(l, K)
-            return x3p[g][:, :, dy : dy + BAND, dx : dx + W]
+            return x3p[g][:, c0:c1, dy : dy + BAND, dx : dx + W]
 
-        def spread(row):
-            return row.rearrange("p (r q) -> p r q", q=W).unsqueeze(1).to_broadcast([P, CG, BAND, W])
+        def spread(row, channels):
+            return row.rearrange("p (r q) -> p r q", q=W).unsqueeze(1).to_broadcast([P, channels, BAND, W])
 
         wps_of = {(0, 0): load_wps(0), (0, 1): load_wps(1)}
         finish = []
@@ -364,20 +365,20 @@ def tile_sam_pb_t_kernel(tc, logits, x, w3c_words, w3c_scales, b3c, out):
 
             sums = [acc_pool.tile([P, PER_BANK, P], F32, name="sums%d" % bank) for bank in range(BANKS)]
             wgtg = state[band]["wgtg"]
-            added = [0]
+            added = [0] * CG
 
-            def add(prod):
-                for c in range(CG):
+            def add(prod, c0, c1):
+                for c in range(c0, c1):
                     bank, j = divmod(c, PER_BANK)
                     nc.tensor.matmul(
                         out=sums[bank][:, j, :],
                         lhsT=prod[:, c].rearrange("p r q -> p (r q)"),
                         rhs=ident[:],
                         is_transpose=True,
-                        start=(added[0] == 0 and j == 0),
-                        stop=(added[0] == KK - 1 and j == PER_BANK - 1),
+                        start=(added[c] == 0 and j == 0),
+                        stop=(added[c] == KK - 1 and j == PER_BANK - 1),
                     )
-                added[0] += 1
+                    added[c] += 1
 
             issued = 0
             taken = 0
@@ -385,23 +386,28 @@ def tile_sam_pb_t_kernel(tc, logits, x, w3c_words, w3c_scales, b3c, out):
             for s in range(NV):
                 while issued < NG and issued * NV <= s * NG:
                     pg = prodg_pool.tile([P, CG, BAND, W], F32, name="pg")
+                    c0 = CV if issued == NG - 1 else 0
                     nc.gpsimd.tensor_tensor(
-                        out=pg[:], in0=window(g, LG[issued]), in1=spread(wgtg[:, issued, :]), op=ALU.mult
+                        out=pg[:, c0:CG],
+                        in0=window(g, LG[issued], c0, CG),
+                        in1=spread(wgtg[:, issued, :], CG - c0),
+                        op=ALU.mult,
                     )
                     prodg[issued] = pg
                     issued += 1
                 pv = prodv_pool.tile([P, CG, BAND, W], F32, name="pv")
+                c1 = CV if s == NV - 1 else CG
                 nc.vector.tensor_tensor(
-                    out=pv[:],
-                    in0=window(g, LV[s]),
-                    in1=spread(wps_of[(u, CHUNK_OF[s])][:, s - CSTART[CHUNK_OF[s]], :]),
+                    out=pv[:, 0:c1],
+                    in0=window(g, LV[s], 0, c1),
+                    in1=spread(wps_of[(u, CHUNK_OF[s])][:, s - CSTART[CHUNK_OF[s]], :], c1),
                     op=ALU.mult,
                 )
                 for t in small.get(s, []):
                     t()
-                add(pv)
+                add(pv, 0, c1)
                 while taken < NG and (taken + 1) * NV <= (s + 1) * NG:
-                    add(prodg[taken])
+                    add(prodg[taken], CV if taken == NG - 1 else 0, CG)
                     taken += 1
                 if s + 1 == CSTART[CHUNK_OF[s] + 1]:
                     k = CHUNK_OF[s] + 2

@@ -36,10 +36,13 @@ BANKS = CG // PER_BANK
 LP = 52
 
 GSTEP = 3
-NG = 16
-LG = [GSTEP * i for i in range(NG)]
-CV = 5
-LV = [l for l in range(KK) if l not in LG] + [LG[NG - 1]]
+PAIR = BAND * K
+GJOBS = [(GSTEP * i, 2 if GSTEP * i + PAIR < KK else 1) for i in range(9)]
+NPAIRS = len([1 for l, cnt in GJOBS if cnt == 2])
+LG = [l + PAIR * a for l, cnt in GJOBS for a in range(cnt)]
+NG = len(LG)
+GFIRST = [sum(cnt for l, cnt in GJOBS[:i]) for i in range(len(GJOBS) + 1)]
+LV = [l for l in range(KK) if l not in LG]
 NV = len(LV)
 NCHUNKS = -(-NV // PER_BANK)
 CSTART = [k * NV // NCHUNKS for k in range(NCHUNKS + 1)]
@@ -131,11 +134,17 @@ def tile_sam_pb_t_kernel(tc, logits, x, w3c_words, w3c_scales, b3c, out):
             if part == 0:
                 wgtg = wgtg_pool.tile([P, NG, NB], F32, name="wgtg")
                 st["wgtg"] = wgtg
-            half = NB // 2
-            cols = slice(part * half, (part + 1) * half)
-            nc.scalar.copy(
-                out=st["wgtg"][:, :, cols], in_=w_nl[:, cols, 0 : GSTEP * NG : GSTEP].rearrange("p n l -> p l n")
-            )
+            p0, p1 = (0, 2) if part == 0 else (2, NPAIRS)
+            for a in range(2):
+                nc.scalar.copy(
+                    out=st["wgtg"][:, 2 * p0 + a : 2 * p1 : 2, :],
+                    in_=w_nl[:, :, GSTEP * p0 + PAIR * a : GSTEP * p1 + PAIR * a : GSTEP].rearrange("p n l -> p l n"),
+                )
+            if part == 1:
+                nc.scalar.copy(
+                    out=st["wgtg"][:, 2 * NPAIRS : NG, :],
+                    in_=w_nl[:, :, GSTEP * NPAIRS : GSTEP * len(GJOBS) : GSTEP].rearrange("p n l -> p l n"),
+                )
 
         def load_wps(k):
             wps = wps_pool.tile([P, PER_BANK, NB], F32, name="wps")
@@ -205,12 +214,10 @@ def tile_sam_pb_t_kernel(tc, logits, x, w3c_words, w3c_scales, b3c, out):
             )
 
         state = {0: {}}
-        with tc.tile_pool(name="xin", bufs=2) as xin, tc.tile_pool(name="xg", bufs=1) as xg, tc.tile_pool(
-            name="lgp", bufs=2
-        ) as lgp:
+        with tc.tile_pool(name="xin", bufs=4) as xin, tc.tile_pool(name="xg", bufs=1) as xg:
 
             def load_early(band):
-                lge = lgp.tile([P, KK, NB], BF16, name="lge")
+                lge = xin.tile([P, KK, NB], BF16, tag="inp")
                 nc.sync.dma_start(out=lge[:], in_=logits_v[:, :, band * NB : (band + 1) * NB])
                 return lge
 
@@ -228,7 +235,7 @@ def tile_sam_pb_t_kernel(tc, logits, x, w3c_words, w3c_scales, b3c, out):
                 )
 
             def load_x(b):
-                raw = xin.tile([P, PACK, HW], BF16, name="raw")
+                raw = xin.tile([P, PACK, HW], BF16, tag="inp")
                 nc.sync.dma_start(out=raw[:], in_=x[b].rearrange("(p t) i j -> p t (i j)", t=PACK))
                 return raw
 
@@ -253,13 +260,12 @@ def tile_sam_pb_t_kernel(tc, logits, x, w3c_words, w3c_scales, b3c, out):
                     )
                     first += width
 
-            early = {0: load_early(0)}
             softmax_load(0, state[0])
+            raws = [load_x(b) for b in range(B)]
             nc.vector.memset(w_plane[:].bitcast(I32), 0)
             words_src = w3c_words[0].bitcast(I32).rearrange("p (h g w) -> p g h w", g=GROUPS, h=HEADS)
             words_dst = w_words[:].bitcast(I32).rearrange("p (g h w) -> p g h w", g=GROUPS, h=HEADS)
             scales_src = w3c_scales[0].bitcast(I32).rearrange("q (h g w) -> q g h w", g=GROUPS, h=HEADS)
-            raws = {0: load_x(0), 1: load_x(1)}
             for g in range(GROUPS):
                 nc.sync.dma_start(out=words_dst[:, g], in_=words_src[:, g])
             for quad in range(4):
@@ -271,30 +277,35 @@ def tile_sam_pb_t_kernel(tc, logits, x, w3c_words, w3c_scales, b3c, out):
                 nc.sync.dma_start(
                     out=bias_bf[b * HEADS : (b + 1) * HEADS, :], in_=b3c.rearrange("(h c) -> h c", c=SP)
                 )
-            early[1] = load_early(1)
+            early = {}
 
-            top_of(0, early[0])
+            def later_top(band):
+                top_of(band, early[band])
+                if band + 4 < BANDS:
+                    early[band + 4] = load_early(band + 4)
+
+            top_of(0, state[0]["lg"])
             softmax_exp(0, state[0], 0, NB)
-            early[2] = load_early(2)
             for b in range(B):
                 quantise_x(b, raws[b])
-                if b + 2 < B:
-                    raws[b + 2] = load_x(b + 2)
+                early[b + 1] = load_early(b + 1)
             nc.vector.tensor_copy(out=bias[:], in_=bias_bf[:])
             for t in first_map_tasks(0):
                 t()
-            top_of(1, early[1])
-            early[3] = load_early(3)
+            for band in (1, 2, 3, 4):
+                later_top(band)
             softmax_recip(state[0])
-            softmax_norm(state[0], 0, NB)
-            for band in range(2, BANDS):
-                top_of(band, early[band])
-                if band + 2 < BANDS:
-                    early[band + 2] = load_early(band + 2)
+            nc.vector.tensor_tensor(
+                out=w_nl[:, :, 0:KK],
+                in0=w_nl[:, :, 0:KK],
+                in1=state[0]["inv"][:].unsqueeze(2).to_broadcast([P, NB, KK]),
+                op=ALU.mult,
+            )
+            for band in range(5, BANDS):
+                later_top(band)
+            v_task(0)()
             gpsimd_weights(state[0], 0)
-            gpsimd_weights(state[0], 1)
-            for k in range(NCHUNKS):
-                v_task(k)()
+            v_task(1)()
 
         prodv_pool = ctx.enter_context(tc.tile_pool(name="prodv", bufs=4))
         prodg_pool = ctx.enter_context(tc.tile_pool(name="prodg", bufs=2))
@@ -320,12 +331,12 @@ def tile_sam_pb_t_kernel(tc, logits, x, w3c_words, w3c_scales, b3c, out):
         def put(side, step, task):
             side.setdefault(step, []).append(task)
 
-        def window(g, l, c0, c1):
+        def window(g, l, cnt):
             dy, dx = divmod(l, K)
-            return x3p[g][:, c0:c1, dy : dy + BAND, dx : dx + W]
+            return x3p[g][:, :, dy : dy + cnt * BAND, dx : dx + W]
 
-        def spread(row, channels):
-            return row.rearrange("p (r q) -> p r q", q=W).unsqueeze(1).to_broadcast([P, channels, BAND, W])
+        def spread(rows, cnt):
+            return rows.rearrange("p a (r q) -> p (a r) q", q=W).unsqueeze(1).to_broadcast([P, CG, cnt * BAND, W])
 
         wps_of = {(0, 0): load_wps(0), (0, 1): load_wps(1)}
         finish = []
@@ -335,8 +346,11 @@ def tile_sam_pb_t_kernel(tc, logits, x, w3c_words, w3c_scales, b3c, out):
             for i, t in enumerate(finish):
                 put(side, i, t)
             if u == 0:
+                put(side, 0, lambda: gpsimd_weights(state[0], 1))
+                for k in range(2, NCHUNKS):
+                    put(side, 0, v_task(k))
                 for i, t in enumerate(first_map_tasks(1)):
-                    put(side, i, t)
+                    put(side, 1 + i, t)
             elif u + 1 < len(units):
                 nband, ng = units[u + 1]
                 put(small, 1, lambda ng=ng: roll(ng, 0))
@@ -365,49 +379,50 @@ def tile_sam_pb_t_kernel(tc, logits, x, w3c_words, w3c_scales, b3c, out):
 
             sums = [acc_pool.tile([P, PER_BANK, P], F32, name="sums%d" % bank) for bank in range(BANKS)]
             wgtg = state[band]["wgtg"]
-            added = [0] * CG
+            added = [0]
 
-            def add(prod, c0, c1):
-                for c in range(c0, c1):
+            def add(prod, a):
+                for c in range(CG):
                     bank, j = divmod(c, PER_BANK)
                     nc.tensor.matmul(
                         out=sums[bank][:, j, :],
-                        lhsT=prod[:, c].rearrange("p r q -> p (r q)"),
+                        lhsT=prod[:, c, a * BAND : (a + 1) * BAND, :].rearrange("p r q -> p (r q)"),
                         rhs=ident[:],
                         is_transpose=True,
-                        start=(added[c] == 0 and j == 0),
-                        stop=(added[c] == KK - 1 and j == PER_BANK - 1),
+                        start=(added[0] == 0 and j == 0),
+                        stop=(added[0] == KK - 1 and j == PER_BANK - 1),
                     )
-                    added[c] += 1
+                added[0] += 1
 
             issued = 0
             taken = 0
             prodg = {}
             for s in range(NV):
-                while issued < NG and issued * NV <= s * NG:
-                    pg = prodg_pool.tile([P, CG, BAND, W], F32, name="pg")
-                    c0 = CV if issued == NG - 1 else 0
+                while issued < len(GJOBS) and GFIRST[issued] * NV <= s * NG:
+                    l, cnt = GJOBS[issued]
+                    pg = prodg_pool.tile([P, CG, 2 * BAND, W], F32, name="pg")
                     nc.gpsimd.tensor_tensor(
-                        out=pg[:, c0:CG],
-                        in0=window(g, LG[issued], c0, CG),
-                        in1=spread(wgtg[:, issued, :], CG - c0),
+                        out=pg[:, :, 0 : cnt * BAND, :],
+                        in0=window(g, l, cnt),
+                        in1=spread(wgtg[:, GFIRST[issued] : GFIRST[issued] + cnt, :], cnt),
                         op=ALU.mult,
                     )
                     prodg[issued] = pg
                     issued += 1
                 pv = prodv_pool.tile([P, CG, BAND, W], F32, name="pv")
-                c1 = CV if s == NV - 1 else CG
+                j0 = s - CSTART[CHUNK_OF[s]]
                 nc.vector.tensor_tensor(
-                    out=pv[:, 0:c1],
-                    in0=window(g, LV[s], 0, c1),
-                    in1=spread(wps_of[(u, CHUNK_OF[s])][:, s - CSTART[CHUNK_OF[s]], :], c1),
+                    out=pv[:],
+                    in0=window(g, LV[s], 1),
+                    in1=spread(wps_of[(u, CHUNK_OF[s])][:, j0 : j0 + 1, :], 1),
                     op=ALU.mult,
                 )
                 for t in small.get(s, []):
                     t()
-                add(pv, 0, c1)
-                while taken < NG and (taken + 1) * NV <= (s + 1) * NG:
-                    add(prodg[taken], CV if taken == NG - 1 else 0, CG)
+                add(pv, 0)
+                while taken < len(GJOBS) and GFIRST[taken + 1] * NV <= (s + 1) * NG:
+                    for a in range(GJOBS[taken][1]):
+                        add(prodg[taken], a)
                     taken += 1
                 if s + 1 == CSTART[CHUNK_OF[s] + 1]:
                     k = CHUNK_OF[s] + 2

@@ -156,21 +156,25 @@ def tile_sam_pb_t_kernel(tc, logits, x, w3c_words, w3c_scales, b3c, out):
             st = {}
             cols = slice(row0 * W, row0 * W + NB)
 
-            def mx(b):
-                if b == 0:
+            def mx(b0):
+                if b0 == 0:
                     turned = turn_pool.tile([P, CG, B, HEADS], F32, name="turned")
                     st["turned"] = turned
-                x3t = stage.tile([P, HEADS * CG], F32, tag="stage")
-                nc.tensor.matmul_mx(
-                    out=x3t[:],
-                    lhsT=x_codes[:, b, cols].bitcast(FP8X4),
-                    lhsT_scale=x_plane[:, b, cols],
-                    rhs=w_words[:, 2 * g * 512 : 2 * (g + 1) * 512].bitcast(FP4X4),
-                    rhs_scale=w_plane[:, g * 512 : (g + 1) * 512],
-                    start=True,
-                    stop=True,
-                )
-                nc.scalar.copy(out=st["turned"][:, :, b, :], in_=x3t[:].rearrange("p (h c) -> p c h", c=CG))
+                banks = {}
+                for b in (b0, b0 + 1):
+                    x3t = stage.tile([P, HEADS * CG], F32, tag="stage")
+                    nc.tensor.matmul_mx(
+                        out=x3t[:],
+                        lhsT=x_codes[:, b, cols].bitcast(FP8X4),
+                        lhsT_scale=x_plane[:, b, cols],
+                        rhs=w_words[:, 2 * g * 512 : 2 * (g + 1) * 512].bitcast(FP4X4),
+                        rhs_scale=w_plane[:, g * 512 : (g + 1) * 512],
+                        start=True,
+                        stop=True,
+                    )
+                    banks[b] = x3t
+                for b in (b0, b0 + 1):
+                    nc.scalar.copy(out=st["turned"][:, :, b, :], in_=banks[b][:].rearrange("p (h c) -> p c h", c=CG))
 
             def turn(bank):
                 x3 = stage.tile([P, PER_BANK, BAND, W], F32, tag="stage")
@@ -191,7 +195,9 @@ def tile_sam_pb_t_kernel(tc, logits, x, w3c_words, w3c_scales, b3c, out):
             def turn_task(bank):
                 return lambda: turn(bank)
 
-            return [mx_task(b) for b in range(B)] + [turn_task(bank) for bank in range(BANKS)]
+            return (
+                [mx_task(0), lambda: None, mx_task(2), lambda: None] + [turn_task(bank) for bank in range(BANKS)]
+            )
 
         def pad_columns(g, r0, r1):
             for q in range(WP):

@@ -220,42 +220,31 @@ def tile_sam_pb_t_kernel(tc, logits, x, w3c_words, w3c_scales, b3c, out):
             )
 
         state = {0: {}}
-        with tc.tile_pool(name="xin", bufs=4) as xin, tc.tile_pool(name="xg", bufs=1) as xg:
-
-            def load_early(band):
-                lge = xin.tile([P, KK, NB], BF16, tag="inp")
-                nc.sync.dma_start(out=lge[:], in_=logits_v[:, :, band * NB : (band + 1) * NB])
-                return lge
-
-            def top_of(band, lge):
-                top = xg.tile([P, KK // 2, NB], BF16, name="top")
-                nc.vector.tensor_tensor(out=top[:], in0=lge[:, 0:24, :], in1=lge[:, 24:48, :], op=ALU.max)
-                for half in (12, 6, 3):
-                    nc.vector.tensor_tensor(
-                        out=top[:, 0:half, :], in0=top[:, 0:half, :], in1=top[:, half : 2 * half, :], op=ALU.max
-                    )
-                for other in (top[:, 1, :], top[:, 2, :], lge[:, KK - 1, :]):
-                    nc.vector.tensor_tensor(out=top[:, 0, :], in0=top[:, 0, :], in1=other, op=ALU.max)
-                nc.vector.tensor_scalar_mul(
-                    out=neg_top[:, band * NB : (band + 1) * NB], in0=top[:, 0, :], scalar1=-1.0
-                )
+        with tc.tile_pool(name="xin", bufs=3) as xin, tc.tile_pool(name="xg", bufs=2) as xg, tc.tile_pool(
+            name="xt", bufs=1
+        ) as xt:
+            rest = HW - NB
 
             def load_x(b):
                 raw = xin.tile([P, PACK, HW], BF16, tag="inp")
                 nc.sync.dma_start(out=raw[:], in_=x[b].rearrange("(p t) i j -> p t (i j)", t=PACK))
                 return raw
 
-            def quantise_x(b, raw):
+            def group_x(raw):
                 grouped = xg.tile([P, NPAD, PACK], BF16, align_bytes=64, name="grouped")
                 nc.vector.tensor_copy(
                     out=grouped[:, PAD * W : PAD * W + HW, :], in_=raw[:].rearrange("p t n -> p n t")
                 )
                 for r in range(HP):
-                    src = reflect(r - PAD, H) + PAD
-                    if src != r:
+                    src = reflect(r - PAD, H)
+                    if src != r - PAD:
                         nc.vector.tensor_copy(
-                            out=grouped[:, r * W : (r + 1) * W, :], in_=grouped[:, src * W : (src + 1) * W, :]
+                            out=grouped[:, r * W : (r + 1) * W, :],
+                            in_=raw[:, :, src * W : (src + 1) * W].rearrange("p t n -> p n t"),
                         )
+                return grouped
+
+            def quantise_x(b, grouped):
                 flat = grouped[:].rearrange("p n t -> p (n t)")
                 first = 0
                 for width in (1024, 128, 64):
@@ -266,8 +255,30 @@ def tile_sam_pb_t_kernel(tc, logits, x, w3c_words, w3c_scales, b3c, out):
                     )
                     first += width
 
+            def first_top(lg):
+                top = xt.tile([P, KK // 2, NB], BF16, name="top")
+                nc.vector.tensor_tensor(out=top[:], in0=lg[:, 0:24, :], in1=lg[:, 24:48, :], op=ALU.max)
+                for half in (12, 6, 3):
+                    nc.vector.tensor_tensor(
+                        out=top[:, 0:half, :], in0=top[:, 0:half, :], in1=top[:, half : 2 * half, :], op=ALU.max
+                    )
+                for other in (top[:, 1, :], top[:, 2, :], lg[:, KK - 1, :]):
+                    nc.vector.tensor_tensor(out=top[:, 0, :], in0=top[:, 0, :], in1=other, op=ALU.max)
+                nc.vector.tensor_scalar_mul(out=neg_top[:, 0:NB], in0=top[:, 0, :], scalar1=-1.0)
+
+            def load_rows(dy):
+                rows = xin.tile([P, K + 1, rest], BF16, tag="inp")
+                nc.sync.dma_start(out=rows[:, 0:K, :], in_=logits_v[:, K * dy : K * (dy + 1), NB:HW])
+                return rows
+
+            def best_of(rows, dest):
+                t4 = xt.tile([P, 4, rest], BF16, name="t4")
+                nc.vector.tensor_tensor(out=t4[:], in0=rows[:, 0:4, :], in1=rows[:, 4:8, :], op=ALU.max)
+                nc.vector.tensor_tensor(out=t4[:, 0:2, :], in0=t4[:, 0:2, :], in1=t4[:, 2:4, :], op=ALU.max)
+                nc.vector.tensor_tensor(out=dest, in0=t4[:, 0, :], in1=t4[:, 1, :], op=ALU.max)
+
             softmax_load(0, state[0])
-            raws = [load_x(b) for b in range(B)]
+            raws = {b: load_x(b) for b in range(3)}
             nc.vector.memset(w_plane[:].bitcast(I32), 0)
             words_src = w3c_words[0].bitcast(I32).rearrange("p (h g w) -> p g h w", g=GROUPS, h=HEADS)
             words_dst = w_words[:].bitcast(I32).rearrange("p (g h w) -> p g h w", g=GROUPS, h=HEADS)
@@ -279,27 +290,36 @@ def tile_sam_pb_t_kernel(tc, logits, x, w3c_words, w3c_scales, b3c, out):
                 plane_dst = plane_dst.rearrange("q (g h w) -> q g h w", g=GROUPS, h=HEADS)
                 for g in range(GROUPS):
                     nc.sync.dma_start(out=plane_dst[:, g], in_=scales_src[4 * quad : 4 * quad + 4, g])
+
+            first_top(state[0]["lg"])
+            softmax_exp(0, state[0], 0, NB)
+            rows_of = {}
+            grouped_of = {0: group_x(raws[0])}
+            raws[3] = load_x(3)
+            for b in range(B):
+                if b + 1 < B:
+                    grouped_of[b + 1] = group_x(raws[b + 1])
+                    rows_of[b] = load_rows(b)
+                quantise_x(b, grouped_of[b])
             for b in range(B):
                 nc.sync.dma_start(
                     out=bias_bf[b * HEADS : (b + 1) * HEADS, :], in_=b3c.rearrange("(h c) -> h c", c=SP)
                 )
-            early = {}
-
-            def later_top(band):
-                top_of(band, early[band])
-                if band + 4 < BANDS:
-                    early[band + 4] = load_early(band + 4)
-
-            top_of(0, state[0]["lg"])
-            softmax_exp(0, state[0], 0, NB)
-            for b in range(B):
-                quantise_x(b, raws[b])
-                early[b + 1] = load_early(b + 1)
-            nc.vector.tensor_copy(out=bias[:], in_=bias_bf[:])
             for t in first_map_tasks(0):
                 t()
-            for band in (1, 2, 3, 4):
-                later_top(band)
+
+            def later_top(dy):
+                if dy == 0:
+                    nc.vector.tensor_copy(out=rows_of[0][:, K, :], in_=rows_of[0][:, 0, :])
+                if dy + 1 < K:
+                    best_of(rows_of[dy], rows_of[dy + 1][:, K, :])
+                else:
+                    best_of(rows_of[dy], rows_of[dy][:, K, :])
+                    nc.vector.tensor_scalar_mul(out=neg_top[:, NB:HW], in0=rows_of[dy][:, K, :], scalar1=-1.0)
+                if dy + 3 < K:
+                    rows_of[dy + 3] = load_rows(dy + 3)
+
+            later_top(0)
             softmax_recip(state[0])
             nc.vector.tensor_tensor(
                 out=w_nl[:, :, 0:KK],
@@ -307,8 +327,9 @@ def tile_sam_pb_t_kernel(tc, logits, x, w3c_words, w3c_scales, b3c, out):
                 in1=state[0]["inv"][:].unsqueeze(2).to_broadcast([P, NB, KK]),
                 op=ALU.mult,
             )
-            for band in range(5, BANDS):
-                later_top(band)
+            for dy in range(1, K):
+                later_top(dy)
+            nc.vector.tensor_copy(out=bias[:], in_=bias_bf[:])
             v_task(0)()
             gpsimd_weights(state[0], 0)
             v_task(1)()

@@ -112,7 +112,8 @@ def tile_sam_pb_t_kernel(tc, logits, x, w3c_words, w3c_scales, b3c, out):
 
         def softmax_recip(st):
             inv_total = stat_pool.tile([P, NB], F32, name="inv_total")
-            nc.vector.reciprocal(out=inv_total[:], in_=st["total"][:])
+            nc.scalar.activation(out=inv_total[:], in_=st["total"][:], func=ACT.Ln)
+            nc.scalar.activation(out=inv_total[:], in_=inv_total[:], func=ACT.Exp, scale=-1.0)
             st["inv"] = inv_total
 
         def softmax_norm(st, n0, n1):
@@ -293,6 +294,7 @@ def tile_sam_pb_t_kernel(tc, logits, x, w3c_words, w3c_scales, b3c, out):
 
             first_top(state[0]["lg"])
             softmax_exp(0, state[0], 0, NB)
+            softmax_recip(state[0])
             rows_of = {}
             grouped_of = {0: group_x(raws[0])}
             raws[3] = load_x(3)
@@ -320,14 +322,14 @@ def tile_sam_pb_t_kernel(tc, logits, x, w3c_words, w3c_scales, b3c, out):
                     rows_of[dy + 3] = load_rows(dy + 3)
 
             later_top(0)
-            softmax_recip(state[0])
+            later_top(1)
             nc.vector.tensor_tensor(
                 out=w_nl[:, :, 0:KK],
                 in0=w_nl[:, :, 0:KK],
                 in1=state[0]["inv"][:].unsqueeze(2).to_broadcast([P, NB, KK]),
                 op=ALU.mult,
             )
-            for dy in range(1, K):
+            for dy in range(2, K):
                 later_top(dy)
             nc.vector.tensor_copy(out=bias[:], in_=bias_bf[:])
             v_task(0)()

@@ -234,7 +234,8 @@ def tile_sam_pb_t_kernel(tc, logits, x, w3c_words, w3c_scales, b3c, out):
             def group_x(raw):
                 grouped = xg.tile([P, NPAD, PACK], BF16, align_bytes=64, name="grouped")
                 nc.vector.tensor_copy(
-                    out=grouped[:, PAD * W : PAD * W + HW, :], in_=raw[:].rearrange("p t n -> p n t")
+                    out=grouped[:, PAD * W : PAD * W + HW, :].rearrange("p (c i) t -> p c t i", i=4),
+                    in_=raw[:].rearrange("p t (c i) -> p c t i", i=4),
                 )
                 for r in range(HP):
                     src = reflect(r - PAD, H)

@@ -21,32 +21,34 @@ KK = K * K
 PAD = K // 2
 HW = H * W
 PACK = 4
-
-BAND = 4
-NB = BAND * W
-BANDS = H // BAND
-ROWS = BAND + 2 * PAD
 WP = W + 2 * PAD
 HP = H + 2 * PAD
 NPAD = HP * W
+
+BAND = 4
+NB = BAND * W
+UROWS = 2
+NU = UROWS * W
+UNITS = H // UROWS
+RING = 12
+TROWS = 4
+TILES = -(-HP // TROWS)
 CG = 16
 GROUPS = SP // CG
 PER_BANK = 4
-BANKS = CG // PER_BANK
+BLOCKS = NU * SP // P
+BANKS = BLOCKS // PER_BANK
 LP = 52
 
-GSTEP = 3
-PAIR = BAND * K
-GJOBS = [(GSTEP * i, 2 if GSTEP * i + PAIR < KK else 1) for i in range(9)]
-NPAIRS = len([1 for l, cnt in GJOBS if cnt == 2])
-LG = [l + PAIR * a for l, cnt in GJOBS for a in range(cnt)]
-NG = len(LG)
-GFIRST = [sum(cnt for l, cnt in GJOBS[:i]) for i in range(len(GJOBS) + 1)]
-LV = [l for l in range(KK) if l not in LG]
-NV = len(LV)
-NCHUNKS = -(-NV // PER_BANK)
-CSTART = [k * NV // NCHUNKS for k in range(NCHUNKS + 1)]
-CHUNK_OF = [k for k in range(NCHUNKS) for s in range(CSTART[k], CSTART[k + 1])]
+NV = 28
+NG = 11
+NS = KK - NV - NG
+GADD = 3
+
+PAIRS = NV // 2
+CHUNK_PAIRS = 4
+NCHUNKS = -(-PAIRS // CHUNK_PAIRS)
+CSTART = [k * PAIRS // NCHUNKS for k in range(NCHUNKS + 1)]
 
 FLOPS = 2 * B * COUT * HW * CIN + 2 * B * COUT * HW * KK
 
@@ -63,107 +65,121 @@ def tile_sam_pb_t_kernel(tc, logits, x, w3c_words, w3c_scales, b3c, out):
     nc = tc.nc
     logits_v = logits.rearrange("b h l n -> (b h) l n")
     out_v = out.rearrange("b (h c) i j -> (b h) c (i j)", c=SP)
-    units = [(band, g) for band in range(BANDS) for g in range(GROUPS)]
 
     with ExitStack() as ctx:
         ctx.enter_context(tc.manual_schedule())
         const = ctx.enter_context(tc.tile_pool(name="const", bufs=1))
-        lg_pool = ctx.enter_context(tc.tile_pool(name="lg", bufs=1))
+        lg_pool = ctx.enter_context(tc.tile_pool(name="lg", bufs=2))
         stat_pool = ctx.enter_context(tc.tile_pool(name="stat", bufs=2))
-        wgtg_pool = ctx.enter_context(tc.tile_pool(name="wgtg", bufs=2))
+        wl_pool = ctx.enter_context(tc.tile_pool(name="wl", bufs=1))
+        wg_pool = ctx.enter_context(tc.tile_pool(name="wg", bufs=2))
+        ws_pool = ctx.enter_context(tc.tile_pool(name="ws", bufs=2))
+        wst_pool = ctx.enter_context(tc.tile_pool(name="wst", bufs=2))
         turn_pool = ctx.enter_context(tc.tile_pool(name="turn", bufs=1))
         acc_pool = ctx.enter_context(tc.psum_pool(name="acc", bufs=1))
         wps_pool = ctx.enter_context(tc.psum_pool(name="wps", bufs=2))
         stage = ctx.enter_context(tc.psum_pool(name="stage", bufs=2))
 
-        ident = const.tile([P, P], F32)
+        ident = const.tile([P, P], F32, name="ident")
         make_identity(nc, ident[:])
 
-        w_words = const.tile([P, 2 * COUT], U8, align_bytes=64)
-        w_plane = const.tile([P, COUT], U8, align_bytes=64)
-        bias_bf = const.tile([P, SP], BF16)
-        bias = const.tile([P, SP], F32)
-        x_codes = const.tile([P, B, NPAD], U32, align_bytes=64)
-        x_plane = const.tile([P, B, NPAD], U8, align_bytes=64)
-        neg_top = const.tile([P, HW], F32)
-        w_nl = const.tile([P, NB, LP], F32)
-        wtv = const.tile([P, NV, P], F32)
-        x3p_a = const.tile([P, CG, ROWS, WP], F32)
-        x3p_b = const.tile([P, CG, ROWS, WP], F32)
-        x3p = [x3p_a, x3p_b]
+        w_words = const.tile([P, 2 * COUT], U8, align_bytes=64, name="w_words")
+        w_plane = const.tile([P, COUT], U8, align_bytes=64, name="w_plane")
+        bias_bf = const.tile([P, SP], BF16, name="bias_bf")
+        bias = const.tile([P, SP], F32, name="bias")
+        x_codes = const.tile([P, B, NPAD], U32, align_bytes=64, name="x_codes")
+        x_plane = const.tile([P, B, NPAD], U8, align_bytes=64, name="x_plane")
+        neg_top = const.tile([P, HW], F32, name="neg_top")
+        wtv = const.tile([P, PAIRS, P], F32, name="wtv")
+        xmap = const.tile([P, RING, WP, SP], F32, name="xmap")
 
-        def softmax_load(band, st):
-            lg = lg_pool.tile([P, KK, NB], BF16, name="lg")
-            nc.sync.dma_start(out=lg[:], in_=logits_v[:, :, band * NB : (band + 1) * NB])
-            total = stat_pool.tile([P, NB], F32, name="total")
-            st["lg"] = lg
-            st["total"] = total
+        lgs = {}
 
-        def softmax_exp(band, st, n0, n1):
+        def load_logits(u):
+            lg = lg_pool.tile([P, KK, NU], BF16, name="lg")
+            nc.sync.dma_start(out=lg[:], in_=logits_v[:, :, u * NU : (u + 1) * NU])
+            lgs[u] = lg
+
+        def softmax_exp(u, st, n0, n1):
+            if n0 == 0:
+                wl = wl_pool.tile([P, NU, LP], F32, name="wl")
+                total = stat_pool.tile([P, NU], F32, name="total")
+                st["wl"] = wl
+                st["total"] = total
             for n in range(n0, n1):
                 nc.scalar.activation(
-                    out=w_nl[:, n, 0:KK],
-                    in_=st["lg"][:, :, n],
+                    out=st["wl"][:, n, 0:KK],
+                    in_=lgs[u][:, :, n],
                     func=ACT.Exp,
-                    bias=neg_top[:, band * NB + n : band * NB + n + 1],
+                    bias=neg_top[:, u * NU + n : u * NU + n + 1],
                     scale=1.0,
                     accum_out=st["total"][:, n : n + 1],
                 )
 
         def softmax_recip(st):
-            inv_total = stat_pool.tile([P, NB], F32, name="inv_total")
-            nc.scalar.activation(out=inv_total[:], in_=st["total"][:], func=ACT.Ln)
-            nc.scalar.activation(out=inv_total[:], in_=inv_total[:], func=ACT.Exp, scale=-1.0)
-            st["inv"] = inv_total
+            inv = stat_pool.tile([P, NU], F32, name="inv")
+            nc.vector.reciprocal(out=inv[:], in_=st["total"][:])
+            st["inv"] = inv
 
         def softmax_norm(st, n0, n1):
             for n in range(n0, n1):
                 nc.scalar.activation(
-                    out=w_nl[:, n, 0:KK], in_=w_nl[:, n, 0:KK], func=ACT.Copy, scale=st["inv"][:, n : n + 1]
+                    out=st["wl"][:, n, 0:KK], in_=st["wl"][:, n, 0:KK], func=ACT.Copy, scale=st["inv"][:, n : n + 1]
                 )
 
-        def turn_weights(ls, dest):
-            ps = stage.tile([P, PER_BANK, P], F32, tag="stage")
-            for j, l in enumerate(ls):
-                nc.tensor.transpose(ps[:, j, :], w_nl[:, :, l], ident[:])
-            nc.scalar.copy(out=dest, in_=ps[:, 0 : len(ls), :])
+        def other_weights(st):
+            ws = ws_pool.tile([P, NU, NS], F32, name="ws")
+            nc.scalar.copy(out=ws[:], in_=st["wl"][:, :, NV + NG : KK])
+            wg = wg_pool.tile([P, NG, NU], F32, name="wg")
+            nc.scalar.copy(out=wg[:], in_=st["wl"][:, :, NV : NV + NG].rearrange("p n l -> p l n"))
+            st["ws"] = ws
+            st["wg"] = wg
 
-        def v_task(k):
-            return lambda: turn_weights(LV[CSTART[k] : CSTART[k + 1]], wtv[:, CSTART[k] : CSTART[k + 1], :])
+        def v_weights(st, k):
+            p0, p1 = CSTART[k], CSTART[k + 1]
+            hold = {}
 
-        def gpsimd_weights(st, part):
-            if part == 0:
-                wgtg = wgtg_pool.tile([P, NG, NB], F32, name="wgtg")
-                st["wgtg"] = wgtg
-            p0, p1 = (0, 2) if part == 0 else (2, NPAIRS)
-            for a in range(2):
+            def gather():
+                wst = wst_pool.tile([P, 2 * CHUNK_PAIRS, NU], F32, name="wst")
                 nc.scalar.copy(
-                    out=st["wgtg"][:, 2 * p0 + a : 2 * p1 : 2, :],
-                    in_=w_nl[:, :, GSTEP * p0 + PAIR * a : GSTEP * p1 + PAIR * a : GSTEP].rearrange("p n l -> p l n"),
+                    out=wst[:, 0 : 2 * (p1 - p0), :], in_=st["wl"][:, :, 2 * p0 : 2 * p1].rearrange("p n l -> p l n")
                 )
-            if part == 1:
-                nc.scalar.copy(
-                    out=st["wgtg"][:, 2 * NPAIRS : NG, :],
-                    in_=w_nl[:, :, GSTEP * NPAIRS : GSTEP * len(GJOBS) : GSTEP].rearrange("p n l -> p l n"),
-                )
+                hold["wst"] = wst
+
+            def fill():
+                ps = stage.tile([P, PER_BANK, P], F32, tag="stage", name="ps")
+                for j in range(p1 - p0):
+                    nc.tensor.transpose(
+                        ps[:, j, :], hold["wst"][:, 2 * j : 2 * j + 2, :].rearrange("p l n -> p (l n)"), ident[:]
+                    )
+                hold["ps"] = ps
+
+            def drain():
+                nc.scalar.copy(out=wtv[:, p0:p1, :], in_=hold["ps"][:, 0 : p1 - p0, :])
+
+            return gather, fill, drain
 
         def load_wps(k):
-            wps = wps_pool.tile([P, PER_BANK, NB], F32, name="wps")
+            wps = wps_pool.tile([P, 2 * CHUNK_PAIRS, NU], F32, name="wps")
             for j in range(CSTART[k + 1] - CSTART[k]):
-                nc.tensor.transpose(wps[:, j, :], wtv[:, CSTART[k] + j, :], ident[:])
+                nc.tensor.transpose(
+                    wps[:, 2 * j : 2 * j + 2, :].rearrange("p l n -> p (l n)"), wtv[:, CSTART[k] + j, :], ident[:]
+                )
             return wps
 
-        def window_tasks(g, row0, dst0, nrows):
-            st = {}
-            cols = slice(row0 * W, row0 * W + NB)
+        turned_of = {}
 
-            def mx(b0):
+        def mx_task(t, g, b0):
+            row0 = min(TROWS * t, HP - TROWS)
+            cols = slice(row0 * W, row0 * W + P)
+            hold = {}
+
+            def fill():
                 if b0 == 0:
                     turned = turn_pool.tile([P, CG, B, HEADS], F32, name="turned")
-                    st["turned"] = turned
-                banks = {}
+                    turned_of[(t, g)] = turned
                 for b in (b0, b0 + 1):
-                    x3t = stage.tile([P, HEADS * CG], F32, tag="stage")
+                    x3t = stage.tile([P, HEADS * CG], F32, tag="stage", name="x3t")
                     nc.tensor.matmul_mx(
                         out=x3t[:],
                         lhsT=x_codes[:, b, cols].bitcast(FP8X4),
@@ -173,61 +189,57 @@ def tile_sam_pb_t_kernel(tc, logits, x, w3c_words, w3c_scales, b3c, out):
                         start=True,
                         stop=True,
                     )
-                    banks[b] = x3t
-                for b in (b0, b0 + 1):
-                    nc.scalar.copy(out=st["turned"][:, :, b, :], in_=banks[b][:].rearrange("p (h c) -> p c h", c=CG))
+                    hold[b] = x3t
 
-            def turn(bank):
-                x3 = stage.tile([P, PER_BANK, BAND, W], F32, tag="stage")
+            def drain():
+                for b in (b0, b0 + 1):
+                    nc.scalar.copy(
+                        out=turned_of[(t, g)][:, :, b, :], in_=hold[b][:].rearrange("p (h c) -> p c h", c=CG)
+                    )
+
+            return fill, drain
+
+        def turn_task(t, g, bank):
+            row0 = min(TROWS * t, HP - TROWS)
+            skip = TROWS * t - row0
+            slot = TROWS * t % RING
+            c0 = g * CG + bank * PER_BANK
+            hold = {}
+
+            def fill():
+                x3 = stage.tile([P, PER_BANK, TROWS, W], F32, tag="stage", name="x3")
                 for j in range(PER_BANK):
                     nc.tensor.transpose(
                         x3[:, j].rearrange("p r q -> p (r q)"),
-                        st["turned"][:, bank * PER_BANK + j].rearrange("p b h -> p (b h)"),
+                        turned_of[(t, g)][:, bank * PER_BANK + j].rearrange("p b h -> p (b h)"),
                         ident[:],
                     )
+                hold["x3"] = x3
+
+            def drain():
                 nc.scalar.copy(
-                    out=x3p[g][:, bank * PER_BANK : (bank + 1) * PER_BANK, dst0 : dst0 + nrows, PAD : PAD + W],
-                    in_=x3[:, :, 0:nrows, :],
+                    out=xmap[:, slot : slot + TROWS - skip, PAD : PAD + W, c0 : c0 + PER_BANK],
+                    in_=hold["x3"][:, :, skip:TROWS, :].rearrange("p j r q -> p r q j"),
                 )
 
-            def mx_task(b):
-                return lambda: mx(b)
+            return fill, drain
 
-            def turn_task(bank):
-                return lambda: turn(bank)
-
-            return (
-                [mx_task(0), lambda: None, mx_task(2), lambda: None] + [turn_task(bank) for bank in range(BANKS)]
-            )
-
-        def pad_columns(g, r0, r1):
+        def pad_columns(t):
+            slot = TROWS * t % RING
+            rows = slice(slot, slot + min(TROWS, HP - TROWS * t))
             for q in range(WP):
                 src = reflect(q - PAD, W) + PAD
                 if src != q:
-                    nc.scalar.copy(out=x3p[g][:, :, r0:r1, q : q + 1], in_=x3p[g][:, :, r0:r1, src : src + 1])
+                    nc.scalar.copy(out=xmap[:, rows, q, :], in_=xmap[:, rows, src, :])
 
-        def roll(g, part):
-            if part == 0:
-                nc.scalar.copy(out=x3p[g][:, :, 0:BAND, :], in_=x3p[g][:, :, BAND : 2 * BAND, :])
-            else:
-                nc.scalar.copy(out=x3p[g][:, :, BAND : ROWS - BAND, :], in_=x3p[g][:, :, 2 * BAND : ROWS, :])
-
-        def first_map_tasks(g):
-            return (
-                window_tasks(g, 0, 0, BAND)
-                + window_tasks(g, BAND, BAND, BAND)
-                + window_tasks(g, 2 * BAND, 2 * BAND, ROWS - 2 * BAND)
-                + [lambda: pad_columns(g, 0, ROWS)]
-            )
-
-        state = {0: {}}
+        state = {u: {} for u in range(UNITS)}
         with tc.tile_pool(name="xin", bufs=3) as xin, tc.tile_pool(name="xg", bufs=2) as xg, tc.tile_pool(
             name="xt", bufs=1
         ) as xt:
             rest = HW - NB
 
             def load_x(b):
-                raw = xin.tile([P, PACK, HW], BF16, tag="inp")
+                raw = xin.tile([P, PACK, HW], BF16, tag="inp", name="raw")
                 nc.sync.dma_start(out=raw[:], in_=x[b].rearrange("(p t) i j -> p t (i j)", t=PACK))
                 return raw
 
@@ -257,8 +269,9 @@ def tile_sam_pb_t_kernel(tc, logits, x, w3c_words, w3c_scales, b3c, out):
                     )
                     first += width
 
-            def first_top(lg):
-                top = xt.tile([P, KK // 2, NB], BF16, name="top")
+            def first_top(u):
+                lg = lgs[u]
+                top = xt.tile([P, KK // 2, NU], BF16, name="top")
                 nc.vector.tensor_tensor(out=top[:], in0=lg[:, 0:24, :], in1=lg[:, 24:48, :], op=ALU.max)
                 for half in (12, 6, 3):
                     nc.vector.tensor_tensor(
@@ -266,10 +279,10 @@ def tile_sam_pb_t_kernel(tc, logits, x, w3c_words, w3c_scales, b3c, out):
                     )
                 for other in (top[:, 1, :], top[:, 2, :], lg[:, KK - 1, :]):
                     nc.vector.tensor_tensor(out=top[:, 0, :], in0=top[:, 0, :], in1=other, op=ALU.max)
-                nc.vector.tensor_scalar_mul(out=neg_top[:, 0:NB], in0=top[:, 0, :], scalar1=-1.0)
+                nc.vector.tensor_scalar_mul(out=neg_top[:, u * NU : (u + 1) * NU], in0=top[:, 0, :], scalar1=-1.0)
 
             def load_rows(dy):
-                rows = xin.tile([P, K + 1, rest], BF16, tag="inp")
+                rows = xin.tile([P, K + 1, rest], BF16, tag="inp", name="rows")
                 nc.sync.dma_start(out=rows[:, 0:K, :], in_=logits_v[:, K * dy : K * (dy + 1), NB:HW])
                 return rows
 
@@ -279,7 +292,8 @@ def tile_sam_pb_t_kernel(tc, logits, x, w3c_words, w3c_scales, b3c, out):
                 nc.vector.tensor_tensor(out=t4[:, 0:2, :], in0=t4[:, 0:2, :], in1=t4[:, 2:4, :], op=ALU.max)
                 nc.vector.tensor_tensor(out=dest, in0=t4[:, 0, :], in1=t4[:, 1, :], op=ALU.max)
 
-            softmax_load(0, state[0])
+            load_logits(0)
+            load_logits(1)
             raws = {b: load_x(b) for b in range(3)}
             nc.vector.memset(w_plane[:].bitcast(I32), 0)
             words_src = w3c_words[0].bitcast(I32).rearrange("p (h g w) -> p g h w", g=GROUPS, h=HEADS)
@@ -293,9 +307,9 @@ def tile_sam_pb_t_kernel(tc, logits, x, w3c_words, w3c_scales, b3c, out):
                 for g in range(GROUPS):
                     nc.sync.dma_start(out=plane_dst[:, g], in_=scales_src[4 * quad : 4 * quad + 4, g])
 
-            first_top(state[0]["lg"])
-            softmax_exp(0, state[0], 0, NB)
-            softmax_recip(state[0])
+            first_top(0)
+            softmax_exp(0, state[0], 0, NU)
+            first_top(1)
             rows_of = {}
             grouped_of = {0: group_x(raws[0])}
             raws[3] = load_x(3)
@@ -308,8 +322,14 @@ def tile_sam_pb_t_kernel(tc, logits, x, w3c_words, w3c_scales, b3c, out):
                 nc.sync.dma_start(
                     out=bias_bf[b * HEADS : (b + 1) * HEADS, :], in_=b3c.rearrange("(h c) -> h c", c=SP)
                 )
-            for t in first_map_tasks(0):
-                t()
+            softmax_recip(state[0])
+            for t in range(2):
+                for g in range(GROUPS):
+                    jobs = [mx_task(t, g, 0), mx_task(t, g, 2)] + [turn_task(t, g, bank) for bank in range(CG // PER_BANK)]
+                    for fill, drain in jobs:
+                        fill()
+                        drain()
+                pad_columns(t)
 
             def later_top(dy):
                 if dy == 0:
@@ -324,148 +344,232 @@ def tile_sam_pb_t_kernel(tc, logits, x, w3c_words, w3c_scales, b3c, out):
 
             later_top(0)
             later_top(1)
+            wl0 = state[0]["wl"]
             nc.vector.tensor_tensor(
-                out=w_nl[:, :, 0:KK],
-                in0=w_nl[:, :, 0:KK],
-                in1=state[0]["inv"][:].unsqueeze(2).to_broadcast([P, NB, KK]),
+                out=wl0[:, :, 0:KK],
+                in0=wl0[:, :, 0:KK],
+                in1=state[0]["inv"][:].unsqueeze(2).to_broadcast([P, NU, KK]),
                 op=ALU.mult,
             )
             for dy in range(2, K):
                 later_top(dy)
             nc.vector.tensor_copy(out=bias[:], in_=bias_bf[:])
-            v_task(0)()
-            gpsimd_weights(state[0], 0)
-            v_task(1)()
+            other_weights(state[0])
+            for k in range(NCHUNKS):
+                for part in v_weights(state[0], k):
+                    part()
+            for b0 in (0, 2):
+                for part in mx_task(2, 0, b0):
+                    part()
 
-        prodv_pool = ctx.enter_context(tc.tile_pool(name="prodv", bufs=4))
-        prodg_pool = ctx.enter_context(tc.tile_pool(name="prodg", bufs=2))
+        prodv_pool = ctx.enter_context(tc.tile_pool(name="prodv", bufs=3))
+        prodg_pool = ctx.enter_context(tc.tile_pool(name="prodg", bufs=3))
+        prods_pool = ctx.enter_context(tc.tile_pool(name="prods", bufs=3))
         sums_pool = ctx.enter_context(tc.tile_pool(name="sums", bufs=1))
-        res_pool = ctx.enter_context(tc.tile_pool(name="res", bufs=2))
+        res_pool = ctx.enter_context(tc.tile_pool(name="res", bufs=1))
 
-        def back_task(band, g, sums_sb, bank):
-            def run():
-                back = stage.tile([P, PER_BANK, NB], F32, tag="stage")
-                for j in range(PER_BANK):
-                    nc.tensor.transpose(back[:, j, :], sums_sb[:, bank * PER_BANK + j, :], ident[:])
-                result = res_pool.tile([P, PER_BANK, NB], F32, name="result")
-                for j in range(PER_BANK):
-                    c = g * CG + bank * PER_BANK + j
-                    nc.scalar.activation(
-                        out=result[:, j, :], in_=back[:, j, :], func=ACT.Identity, bias=bias[:, c : c + 1], scale=1.0
-                    )
-                c0 = g * CG + bank * PER_BANK
-                nc.sync.dma_start(out=out_v[:, c0 : c0 + PER_BANK, band * NB : (band + 1) * NB], in_=result[:])
-
-            return run
-
-        def put(side, step, task):
-            side.setdefault(step, []).append(task)
-
-        def window(g, l, cnt):
+        def window(u, l):
             dy, dx = divmod(l, K)
-            return x3p[g][:, :, dy : dy + cnt * BAND, dx : dx + W]
+            slot = (UROWS * u + dy) % RING
+            if slot + UROWS <= RING:
+                return [(slice(0, UROWS), xmap[:, slot : slot + UROWS, dx : dx + W, :])]
+            return [(slice(r, r + 1), xmap[:, (slot + r) % RING : (slot + r) % RING + 1, dx : dx + W, :]) for r in range(UROWS)]
 
-        def spread(rows, cnt):
-            return rows.rearrange("p a (r q) -> p (a r) q", q=W).unsqueeze(1).to_broadcast([P, CG, cnt * BAND, W])
-
-        wps_of = {(0, 0): load_wps(0), (0, 1): load_wps(1)}
-        finish = []
-        for u, (band, g) in enumerate(units):
-            small = {}
-            side = {}
-            for i, t in enumerate(finish):
-                put(side, i, t)
-            if u == 0:
-                put(side, 0, lambda: gpsimd_weights(state[0], 1))
-                for k in range(2, NCHUNKS):
-                    put(side, 0, v_task(k))
-                for i, t in enumerate(first_map_tasks(1)):
-                    put(side, 1 + i, t)
-            elif u + 1 < len(units):
-                nband, ng = units[u + 1]
-                put(small, 1, lambda ng=ng: roll(ng, 0))
-                put(small, 2, lambda ng=ng: roll(ng, 1))
-                for i, t in enumerate(window_tasks(ng, BAND * nband + ROWS - BAND, ROWS - BAND, BAND)):
-                    put(side, 4 + i, t)
-                put(side, 12, lambda ng=ng: pad_columns(ng, ROWS - BAND, ROWS))
-            if band + 1 < BANDS:
-                if g == 0:
-                    state[band + 1] = {}
-                    st = state[band + 1]
-                    put(small, 0, lambda st=st, nb=band + 1: softmax_load(nb, st))
-                    for i in range(22):
-                        put(small, 1 + i, lambda st=st, nb=band + 1, i=i: softmax_exp(nb, st, 6 * i, min(6 * i + 6, NB)))
-                    put(small, 24, lambda st=st: softmax_recip(st))
-                    for i in range(7):
-                        put(small, 25 + i, lambda st=st, i=i: softmax_norm(st, 8 * i, 8 * i + 8))
-                else:
-                    st = state[band + 1]
-                    for i in range(7, 16):
-                        put(small, i - 7, lambda st=st, i=i: softmax_norm(st, 8 * i, 8 * i + 8))
-                    put(small, 10, lambda st=st: gpsimd_weights(st, 0))
-                    put(small, 11, lambda st=st: gpsimd_weights(st, 1))
-                    for k in range(NCHUNKS):
-                        put(side, max(12 + k, CSTART[max(k - 1, 0)]), v_task(k))
-
-            sums = [acc_pool.tile([P, PER_BANK, P], F32, name="sums%d" % bank) for bank in range(BANKS)]
-            wgtg = state[band]["wgtg"]
-            added = [0]
-
-            def add(prod, a):
-                for c in range(CG):
-                    bank, j = divmod(c, PER_BANK)
-                    nc.tensor.matmul(
-                        out=sums[bank][:, j, :],
-                        lhsT=prod[:, c, a * BAND : (a + 1) * BAND, :].rearrange("p r q -> p (r q)"),
-                        rhs=ident[:],
-                        is_transpose=True,
-                        start=(added[0] == 0 and j == 0),
-                        stop=(added[0] == KK - 1 and j == PER_BANK - 1),
-                    )
-                added[0] += 1
-
-            issued = 0
-            taken = 0
-            prodg = {}
-            for s in range(NV):
-                while issued < len(GJOBS) and GFIRST[issued] * NV <= s * NG:
-                    l, cnt = GJOBS[issued]
-                    pg = prodg_pool.tile([P, CG, 2 * BAND, W], F32, name="pg")
-                    nc.gpsimd.tensor_tensor(
-                        out=pg[:, :, 0 : cnt * BAND, :],
-                        in0=window(g, l, cnt),
-                        in1=spread(wgtg[:, GFIRST[issued] : GFIRST[issued] + cnt, :], cnt),
-                        op=ALU.mult,
-                    )
-                    prodg[issued] = pg
-                    issued += 1
-                pv = prodv_pool.tile([P, CG, BAND, W], F32, name="pv")
-                j0 = s - CSTART[CHUNK_OF[s]]
-                nc.vector.tensor_tensor(
-                    out=pv[:],
-                    in0=window(g, LV[s], 1),
-                    in1=spread(wps_of[(u, CHUNK_OF[s])][:, j0 : j0 + 1, :], 1),
+        def multiply(engine, u, l, prod, weights):
+            prod_v = prod[:].rearrange("p (r q) c -> p r q c", q=W)
+            weights_v = weights.rearrange("p (r q) -> p r q", q=W).unsqueeze(3)
+            for rows, win in window(u, l):
+                cnt = rows.stop - rows.start
+                engine.tensor_tensor(
+                    out=prod_v[:, rows],
+                    in0=win,
+                    in1=weights_v[:, rows].to_broadcast([P, cnt, W, SP]),
                     op=ALU.mult,
                 )
-                for t in small.get(s, []):
-                    t()
-                add(pv, 0)
-                while taken < len(GJOBS) and GFIRST[taken + 1] * NV <= (s + 1) * NG:
-                    for a in range(GJOBS[taken][1]):
-                        add(prodg[taken], a)
-                    taken += 1
-                if s + 1 == CSTART[CHUNK_OF[s] + 1]:
-                    k = CHUNK_OF[s] + 2
-                    if k < NCHUNKS:
-                        wps_of[(u, k)] = load_wps(k)
-                    elif u + 1 < len(units):
-                        wps_of[(u + 1, k - NCHUNKS)] = load_wps(k - NCHUNKS)
-                for t in side.get(s, []):
-                    t()
 
-            sums_sb = sums_pool.tile([P, CG, P], F32, name="sums_sb")
+        sums_of = {}
+        added = {u: 0 for u in range(UNITS)}
+        NADDS = NV + NS + NG - GADD
+
+        def add(u, prod):
+            flat = prod[:].rearrange("p n c -> p (n c)")
+            if added[u] == 0:
+                sums_of[u] = []
+                for bank in range(BANKS):
+                    sums = acc_pool.tile([P, PER_BANK, P], F32, name="sums%d" % bank)
+                    sums_of[u].append(sums)
+            for blk in range(BLOCKS):
+                bank, j = divmod(blk, PER_BANK)
+                nc.tensor.matmul(
+                    out=sums_of[u][bank][:, j, :],
+                    lhsT=flat[:, blk * P : (blk + 1) * P],
+                    rhs=ident[:],
+                    is_transpose=True,
+                    start=(added[u] == 0 and j == 0),
+                    stop=(added[u] == NADDS - 1 and j == PER_BANK - 1),
+                )
+            added[u] += 1
+
+        gprods = {}
+
+        def g_multiply(u, i):
+            pg = prodg_pool.tile([P, NU, SP], F32, name="pg")
+            multiply(nc.gpsimd, u, NV + i, pg, state[u]["wg"][:, i, :])
+            gprods[(u, i)] = pg
+
+        def g_add(u, i):
+            nc.gpsimd.tensor_tensor(
+                out=gprods[(u, i)][:], in0=gprods[(u, i)][:], in1=gprods[(u, i + 1)][:], op=ALU.add
+            )
+
+        sprods = {}
+
+        def s_multiply(u, e):
+            i, n = divmod(e, NU)
+            if n == 0:
+                ps = prods_pool.tile([P, NU, SP], F32, name="ps")
+                sprods[(u, i)] = ps
+            dy, dx = divmod(NV + NG + i, K)
+            r, q = divmod(n, W)
+            nc.scalar.activation(
+                out=sprods[(u, i)][:, n, :],
+                in_=xmap[:, (UROWS * u + dy + r) % RING, q + dx, :],
+                func=ACT.Copy,
+                scale=state[u]["ws"][:, n, i : i + 1],
+            )
+
+        sums_sb_of = {}
+        result_of = {}
+
+        def take_sums(u):
+            sums_sb = sums_pool.tile([P, BLOCKS, P], F32, name="sums_sb")
             for bank in range(BANKS):
-                nc.scalar.copy(out=sums_sb[:, bank * PER_BANK : (bank + 1) * PER_BANK, :], in_=sums[bank][:])
-            finish = [back_task(band, g, sums_sb, bank) for bank in range(BANKS)]
-        for t in finish:
-            t()
+                nc.scalar.copy(out=sums_sb[:, bank * PER_BANK : (bank + 1) * PER_BANK, :], in_=sums_of[u][bank][:])
+            sums_sb_of[u] = sums_sb
+
+        def back_task(u, bank):
+            hold = {}
+
+            def fill():
+                back = stage.tile([P, PER_BANK * P], F32, tag="stage", name="back")
+                for j in range(PER_BANK):
+                    nc.tensor.transpose(
+                        back[:, j * P : (j + 1) * P], sums_sb_of[u][:, bank * PER_BANK + j, :], ident[:]
+                    )
+                hold["back"] = back
+
+            def drain():
+                if bank == 0:
+                    result = res_pool.tile([P, SP, NU], F32, name="result")
+                    result_of[u] = result
+                npos = PER_BANK * P // SP
+                nc.vector.tensor_tensor(
+                    out=result_of[u][:, :, bank * npos : (bank + 1) * npos],
+                    in0=hold["back"][:].rearrange("p (n c) -> p c n", c=SP),
+                    in1=bias[:].unsqueeze(2).to_broadcast([P, SP, npos]),
+                    op=ALU.add,
+                )
+                if bank == BANKS - 1:
+                    nc.sync.dma_start(out=out_v[:, :, u * NU : (u + 1) * NU], in_=result_of[u][:])
+
+            return fill, drain
+
+        GLEAD, GLAG = 1, 1
+        SLEAD, SLAG = 2, 1
+        BACK0 = 1
+        WPS0 = 24
+        wps_of = {}
+
+        def take_wps(u, c):
+            wps_of[(u, c)] = load_wps(c)
+
+        g_at, s_at, take_at, small_at, drain_at, fill_at = {}, {}, {}, {}, {}, {}
+
+        def put(where, t, task):
+            where.setdefault(max(t, 0), []).append(task)
+
+        def stage_tasks(t, task, lag):
+            fill, drain = task
+            put(fill_at, t, fill)
+            put(drain_at, t + lag, drain)
+
+        def spread(t0, first, steps, count, task):
+            for i in range(steps):
+                n0, n1 = i * count // steps, (i + 1) * count // steps
+                put(small_at, t0 + first + i, lambda n0=n0, n1=n1: task(n0, n1))
+
+        for u in range(UNITS):
+            t0 = u * NV
+            last = t0 + NV - 1
+            jobs = []
+            for i in range(NG):
+                jobs.append((g_multiply, i))
+                if i % 2 == 1 and i // 2 < GADD:
+                    jobs.append((g_add, i - 1))
+            for k, (job, i) in enumerate(jobs):
+                put(g_at, t0 + k * NV // len(jobs) - GLEAD, lambda job=job, u=u, i=i: job(u, i))
+                if job is g_add or i >= 2 * GADD:
+                    done = t0 - GLEAD - (-(k + 1) * NV // len(jobs)) + GLAG
+                    put(take_at, min(max(done, t0), last), lambda u=u, i=i: add(u, gprods[(u, i)]))
+            for e in range(NS * NU):
+                put(s_at, t0 + e * NV // (NS * NU) - SLEAD, lambda u=u, e=e: s_multiply(u, e))
+            for i in range(NS):
+                done = t0 - SLEAD - (-(i + 1) * NV // NS) + SLAG
+                put(take_at, min(max(done, t0), last), lambda u=u, i=i: add(u, sprods[(u, i)]))
+            if u:
+                put(drain_at, t0, lambda u=u: take_sums(u - 1))
+                for bank in range(BANKS):
+                    stage_tasks(t0 + BACK0 + bank, back_task(u - 1, bank), 2)
+            k, odd = divmod(u, 2)
+            t = k + 2
+            if not odd:
+                if t < TILES:
+                    for bank in range(4):
+                        stage_tasks(t0 + 5 + bank, turn_task(t, 0, bank), 1)
+                        stage_tasks(t0 + 14 + bank, turn_task(t, 1, bank), 1)
+                    stage_tasks(t0 + 10, mx_task(t, 1, 0), 1)
+                    stage_tasks(t0 + 12, mx_task(t, 1, 2), 1)
+                    put(small_at, t0 + 19, lambda t=t: pad_columns(t))
+            elif t + 1 < TILES:
+                stage_tasks(t0 + 10, mx_task(t + 1, 0, 0), 1)
+                stage_tasks(t0 + 12, mx_task(t + 1, 0, 2), 1)
+            for c in range(NCHUNKS):
+                after = t0 + 2 * CSTART[c + 1] - 1
+                if c + 2 < NCHUNKS:
+                    put(fill_at, after, lambda u=u, c=c: take_wps(u, c + 2))
+                elif u + 1 < UNITS:
+                    put(fill_at, max(after, t0 + WPS0), lambda u=u, c=c: take_wps(u + 1, c + 2 - NCHUNKS))
+            if u + 2 < UNITS:
+                put(small_at, t0 + 1, lambda u=u: load_logits(u + 2))
+            if u + 1 < UNITS:
+                st = state[u + 1]
+                spread(t0, 0, 13, NU, lambda n0, n1, u=u, st=st: softmax_exp(u + 1, st, n0, n1))
+                put(small_at, t0 + 14, lambda st=st: softmax_recip(st))
+                spread(t0, 15, 6, NU, lambda n0, n1, st=st: softmax_norm(st, n0, n1))
+                put(small_at, t0 + 21, lambda st=st: other_weights(st))
+                for c in range(NCHUNKS):
+                    gather, fill, drain = v_weights(st, c)
+                    put(small_at, t0 + 21 + c, gather)
+                    stage_tasks(t0 + 22 + c, (fill, drain), 1)
+
+        take_wps(0, 0)
+        take_wps(0, 1)
+        chunk_of = [k for k in range(NCHUNKS) for i in range(CSTART[k], CSTART[k + 1]) for two in range(2)]
+        for t in range(UNITS * NV):
+            u, s = divmod(t, NV)
+            for job in g_at.get(t, []):
+                job()
+            k = chunk_of[s]
+            pv = prodv_pool.tile([P, NU, SP], F32, name="pv")
+            multiply(nc.vector, u, s, pv, wps_of[(u, k)][:, s - 2 * CSTART[k], :])
+            for job in s_at.get(t, []) + small_at.get(t, []) + drain_at.get(t, []):
+                job()
+            add(u, pv)
+            for job in take_at.get(t, []):
+                job()
+            for job in fill_at.get(t, []):
+                job()
+        take_sums(UNITS - 1)
+        for bank in range(BANKS):
+            for part in back_task(UNITS - 1, bank):
+                part()

@@ -22,8 +22,8 @@ PAD = K // 2
 HW = H * W
 PACK = 4
 WP = W + 2 * PAD
-HP = H + 2 * PAD
-NPAD = HP * W
+XROWS = 36
+NPAD = XROWS * W
 
 BAND = 4
 NB = BAND * W
@@ -32,25 +32,14 @@ NU = UROWS * W
 UNITS = H // UROWS
 RING = 12
 TROWS = 4
-TILES = -(-HP // TROWS)
+TILES = XROWS // TROWS
 CG = 16
 GROUPS = SP // CG
 PER_BANK = 4
 BLOCKS = NU * SP // P
 BANKS = BLOCKS // PER_BANK
+NPOS = NU // BANKS
 LP = 52
-
-NV = 28
-NG = 11
-NS = KK - NV - NG
-GADD = 3
-
-PAIRS = NV // 2
-CHUNK_PAIRS = 4
-NCHUNKS = -(-PAIRS // CHUNK_PAIRS)
-CSTART = [k * PAIRS // NCHUNKS for k in range(NCHUNKS + 1)]
-
-FLOPS = 2 * B * COUT * HW * CIN + 2 * B * COUT * HW * KK
 
 
 def reflect(u, size):
@@ -59,6 +48,39 @@ def reflect(u, size):
     if u > size - 1:
         return 2 * (size - 1) - u
     return u
+
+
+def edge_rows():
+    folds, full, half = [], [], []
+    for u in range(UNITS):
+        keeps, fold = [], []
+        for r in range(UROWS):
+            i = UROWS * u + r
+            stays = [reflect(i + dy - PAD, H) - i + PAD for dy in range(K)]
+            fold.extend([(r, stays[dy], dy) for dy in range(K) if stays[dy] != dy])
+            keeps.append([dy for dy in range(K) if stays[dy] == dy])
+        both = [dy for dy in keeps[0] if dy in keeps[1]]
+        one = [(dy, r) for r in range(UROWS) for dy in keeps[r] if dy not in both]
+        folds.append(fold)
+        full.append((K * both[0], K * (both[-1] + 1)))
+        half.append(one[0] if one else None)
+    return folds, full, half
+
+
+FOLDS, FULL, HALF = edge_rows()
+
+INNER = UNITS - 4
+NV = [18, 26] + [26 + 2 * (i % 2) for i in range(INNER)] + [26, 16]
+NG = [7, 9] + [11 - i % 2 for i in range(INNER)] + [9, 6]
+NS = [FULL[u][1] - FULL[u][0] - NV[u] - NG[u] for u in range(UNITS)]
+GADD = [2, 3] + [4 for i in range(INNER)] + [3, 2]
+
+CHUNK_PAIRS = 4
+NCHUNKS = 4
+CSTART = [[k * (NV[u] // 2) // NCHUNKS for k in range(NCHUNKS + 1)] for u in range(UNITS)]
+TSTART = [sum(NV[:u]) for u in range(UNITS + 1)]
+
+FLOPS = 2 * B * COUT * HW * CIN + 2 * B * COUT * HW * KK
 
 
 def tile_sam_pb_t_kernel(tc, logits, x, w3c_words, w3c_scales, b3c, out):
@@ -70,12 +92,13 @@ def tile_sam_pb_t_kernel(tc, logits, x, w3c_words, w3c_scales, b3c, out):
         ctx.enter_context(tc.manual_schedule())
         const = ctx.enter_context(tc.tile_pool(name="const", bufs=1))
         lg_pool = ctx.enter_context(tc.tile_pool(name="lg", bufs=2))
-        stat_pool = ctx.enter_context(tc.tile_pool(name="stat", bufs=2))
+        stat_pool = ctx.enter_context(tc.tile_pool(name="stat", bufs=3))
         wl_pool = ctx.enter_context(tc.tile_pool(name="wl", bufs=1))
         wg_pool = ctx.enter_context(tc.tile_pool(name="wg", bufs=2))
         ws_pool = ctx.enter_context(tc.tile_pool(name="ws", bufs=2))
         wst_pool = ctx.enter_context(tc.tile_pool(name="wst", bufs=2))
         turn_pool = ctx.enter_context(tc.tile_pool(name="turn", bufs=1))
+        prods_pool = ctx.enter_context(tc.tile_pool(name="prods", bufs=8))
         acc_pool = ctx.enter_context(tc.psum_pool(name="acc", bufs=1))
         wps_pool = ctx.enter_context(tc.psum_pool(name="wps", bufs=2))
         stage = ctx.enter_context(tc.psum_pool(name="stage", bufs=2))
@@ -90,7 +113,7 @@ def tile_sam_pb_t_kernel(tc, logits, x, w3c_words, w3c_scales, b3c, out):
         x_codes = const.tile([P, B, NPAD], U32, align_bytes=64, name="x_codes")
         x_plane = const.tile([P, B, NPAD], U8, align_bytes=64, name="x_plane")
         neg_top = const.tile([P, HW], F32, name="neg_top")
-        wtv = const.tile([P, PAIRS, P], F32, name="wtv")
+        wtv = const.tile([P, max(NV) // 2, P], F32, name="wtv")
         xmap = const.tile([P, RING, WP, SP], F32, name="xmap")
 
         lgs = {}
@@ -116,34 +139,42 @@ def tile_sam_pb_t_kernel(tc, logits, x, w3c_words, w3c_scales, b3c, out):
                     accum_out=st["total"][:, n : n + 1],
                 )
 
+        def fold(engine, u, st):
+            for r, stays, reflects in FOLDS[u]:
+                rows = slice(r * W, (r + 1) * W)
+                engine.tensor_tensor(
+                    out=st["wl"][:, rows, K * stays : K * (stays + 1)],
+                    in0=st["wl"][:, rows, K * stays : K * (stays + 1)],
+                    in1=st["wl"][:, rows, K * reflects : K * (reflects + 1)],
+                    op=ALU.add,
+                )
+
         def softmax_recip(st):
             inv = stat_pool.tile([P, NU], F32, name="inv")
             nc.vector.reciprocal(out=inv[:], in_=st["total"][:])
             st["inv"] = inv
 
-        def softmax_norm(st, n0, n1):
-            for n in range(n0, n1):
-                nc.scalar.activation(
-                    out=st["wl"][:, n, 0:KK], in_=st["wl"][:, n, 0:KK], func=ACT.Copy, scale=st["inv"][:, n : n + 1]
-                )
-
-        def other_weights(st):
-            ws = ws_pool.tile([P, NU, NS], F32, name="ws")
-            nc.scalar.copy(out=ws[:], in_=st["wl"][:, :, NV + NG : KK])
-            wg = wg_pool.tile([P, NG, NU], F32, name="wg")
-            nc.scalar.copy(out=wg[:], in_=st["wl"][:, :, NV : NV + NG].rearrange("p n l -> p l n"))
+        def other_weights(u, st):
+            lg0 = FULL[u][0] + NV[u]
+            ls0 = lg0 + NG[u]
+            ws = ws_pool.tile([P, NU, NS[u] + (K if HALF[u] else 0)], F32, name="ws")
+            nc.scalar.copy(out=ws[:, :, 0 : NS[u]], in_=st["wl"][:, :, ls0 : ls0 + NS[u]])
+            if HALF[u]:
+                lh0 = K * HALF[u][0]
+                nc.scalar.copy(out=ws[:, :, NS[u] : NS[u] + K], in_=st["wl"][:, :, lh0 : lh0 + K])
+            wg = wg_pool.tile([P, NG[u], NU], F32, name="wg")
+            nc.scalar.copy(out=wg[:], in_=st["wl"][:, :, lg0:ls0].rearrange("p n l -> p l n"))
             st["ws"] = ws
             st["wg"] = wg
 
-        def v_weights(st, k):
-            p0, p1 = CSTART[k], CSTART[k + 1]
+        def v_weights(u, st, k):
+            p0, p1 = CSTART[u][k], CSTART[u][k + 1]
             hold = {}
 
             def gather():
                 wst = wst_pool.tile([P, 2 * CHUNK_PAIRS, NU], F32, name="wst")
-                nc.scalar.copy(
-                    out=wst[:, 0 : 2 * (p1 - p0), :], in_=st["wl"][:, :, 2 * p0 : 2 * p1].rearrange("p n l -> p l n")
-                )
+                l0, l1 = FULL[u][0] + 2 * p0, FULL[u][0] + 2 * p1
+                nc.scalar.copy(out=wst[:, 0 : l1 - l0, :], in_=st["wl"][:, :, l0:l1].rearrange("p n l -> p l n"))
                 hold["wst"] = wst
 
             def fill():
@@ -159,19 +190,18 @@ def tile_sam_pb_t_kernel(tc, logits, x, w3c_words, w3c_scales, b3c, out):
 
             return gather, fill, drain
 
-        def load_wps(k):
+        def load_wps(u, k):
             wps = wps_pool.tile([P, 2 * CHUNK_PAIRS, NU], F32, name="wps")
-            for j in range(CSTART[k + 1] - CSTART[k]):
+            for j in range(CSTART[u][k + 1] - CSTART[u][k]):
                 nc.tensor.transpose(
-                    wps[:, 2 * j : 2 * j + 2, :].rearrange("p l n -> p (l n)"), wtv[:, CSTART[k] + j, :], ident[:]
+                    wps[:, 2 * j : 2 * j + 2, :].rearrange("p l n -> p (l n)"), wtv[:, CSTART[u][k] + j, :], ident[:]
                 )
             return wps
 
         turned_of = {}
 
-        def mx_task(t, g, b0):
-            row0 = min(TROWS * t, HP - TROWS)
-            cols = slice(row0 * W, row0 * W + P)
+        def mx_task(t, g, b0, own=False):
+            cols = slice(TROWS * t * W, TROWS * t * W + P)
             hold = {}
 
             def fill():
@@ -179,7 +209,10 @@ def tile_sam_pb_t_kernel(tc, logits, x, w3c_words, w3c_scales, b3c, out):
                     turned = turn_pool.tile([P, CG, B, HEADS], F32, name="turned")
                     turned_of[(t, g)] = turned
                 for b in (b0, b0 + 1):
-                    x3t = stage.tile([P, HEADS * CG], F32, tag="stage", name="x3t")
+                    if not own:
+                        x3t = stage.tile([P, HEADS * CG], F32, tag="stage", name="x3t")
+                    else:
+                        x3t = acc_pool.tile([P, HEADS * CG], F32, tag="sums%d" % b, name="x3t")
                     nc.tensor.matmul_mx(
                         out=x3t[:],
                         lhsT=x_codes[:, b, cols].bitcast(FP8X4),
@@ -200,8 +233,6 @@ def tile_sam_pb_t_kernel(tc, logits, x, w3c_words, w3c_scales, b3c, out):
             return fill, drain
 
         def turn_task(t, g, bank):
-            row0 = min(TROWS * t, HP - TROWS)
-            skip = TROWS * t - row0
             slot = TROWS * t % RING
             c0 = g * CG + bank * PER_BANK
             hold = {}
@@ -217,54 +248,58 @@ def tile_sam_pb_t_kernel(tc, logits, x, w3c_words, w3c_scales, b3c, out):
                 hold["x3"] = x3
 
             def drain():
-                nc.scalar.copy(
-                    out=xmap[:, slot : slot + TROWS - skip, PAD : PAD + W, c0 : c0 + PER_BANK],
-                    in_=hold["x3"][:, :, skip:TROWS, :].rearrange("p j r q -> p r q j"),
+                nc.vector.tensor_tensor(
+                    out=xmap[:, slot : slot + TROWS, PAD : PAD + W, c0 : c0 + PER_BANK],
+                    in0=hold["x3"][:].rearrange("p j r q -> p r q j"),
+                    in1=bias[:, c0 : c0 + PER_BANK].unsqueeze(1).unsqueeze(1).to_broadcast([P, TROWS, W, PER_BANK]),
+                    op=ALU.add,
                 )
 
             return fill, drain
 
         def pad_columns(t):
             slot = TROWS * t % RING
-            rows = slice(slot, slot + min(TROWS, HP - TROWS * t))
+            rows = slice(slot, slot + TROWS)
             for q in range(WP):
                 src = reflect(q - PAD, W) + PAD
                 if src != q:
                     nc.scalar.copy(out=xmap[:, rows, q, :], in_=xmap[:, rows, src, :])
 
         state = {u: {} for u in range(UNITS)}
-        with tc.tile_pool(name="xin", bufs=3) as xin, tc.tile_pool(name="xg", bufs=2) as xg, tc.tile_pool(
-            name="xt", bufs=1
-        ) as xt:
-            rest = HW - NB
+        with tc.tile_pool(name="xin", bufs=3) as xin, tc.tile_pool(name="xa", bufs=4) as xa, tc.tile_pool(
+            name="xg", bufs=2
+        ) as xg, tc.tile_pool(name="xt", bufs=1) as xt:
+            rest = HW - NU
 
-            def load_x(b):
-                raw = xin.tile([P, PACK, HW], BF16, tag="inp", name="raw")
-                nc.sync.dma_start(out=raw[:], in_=x[b].rearrange("(p t) i j -> p t (i j)", t=PACK))
+            def load_x(pool, b, r0, r1):
+                raw = pool.tile([P, PACK, (r1 - r0) * W], BF16, tag="inp", name="raw")
+                nc.sync.dma_start(out=raw[:], in_=x[b].rearrange("(p t) i j -> p t (i j)", t=PACK)[:, :, r0 * W : r1 * W])
                 return raw
 
-            def group_x(raw):
-                grouped = xg.tile([P, NPAD, PACK], BF16, align_bytes=64, name="grouped")
+            def group_x(raw, r0, r1, p0, p1):
+                grouped = xg.tile([P, (p1 - p0) * W, PACK], BF16, align_bytes=64, name="grouped")
+                first, last = max(p0, PAD + r0), min(p1, PAD + r1)
                 nc.vector.tensor_copy(
-                    out=grouped[:, PAD * W : PAD * W + HW, :].rearrange("p (c i) t -> p c t i", i=4),
-                    in_=raw[:].rearrange("p t (c i) -> p c t i", i=4),
+                    out=grouped[:, (first - p0) * W : (last - p0) * W, :].rearrange("p (c i) t -> p c t i", i=4),
+                    in_=raw[:, :, (first - PAD - r0) * W : (last - PAD - r0) * W].rearrange("p t (c i) -> p c t i", i=4),
                 )
-                for r in range(HP):
-                    src = reflect(r - PAD, H)
-                    if src != r - PAD:
+                for r in range(p0, p1):
+                    src = reflect(r - PAD, H) - r0
+                    if src != r - PAD - r0:
                         nc.vector.tensor_copy(
-                            out=grouped[:, r * W : (r + 1) * W, :],
+                            out=grouped[:, (r - p0) * W : (r - p0 + 1) * W, :],
                             in_=raw[:, :, src * W : (src + 1) * W].rearrange("p t n -> p n t"),
                         )
                 return grouped
 
-            def quantise_x(b, grouped):
+            def quantise_x(b, grouped, p0, widths):
                 flat = grouped[:].rearrange("p n t -> p (n t)")
                 first = 0
-                for width in (1024, 128, 64):
+                for width in widths:
+                    n0 = p0 * W + first
                     nc.vector.quantize_mx(
-                        out=x_codes[:, b, first : first + width].bitcast(FP8X4),
-                        scales=x_plane[:, b, first : first + width],
+                        out=x_codes[:, b, n0 : n0 + width].bitcast(FP8X4),
+                        scales=x_plane[:, b, n0 : n0 + width],
                         in_=flat[:, PACK * first : PACK * (first + width)],
                     )
                     first += width
@@ -283,7 +318,7 @@ def tile_sam_pb_t_kernel(tc, logits, x, w3c_words, w3c_scales, b3c, out):
 
             def load_rows(dy):
                 rows = xin.tile([P, K + 1, rest], BF16, tag="inp", name="rows")
-                nc.sync.dma_start(out=rows[:, 0:K, :], in_=logits_v[:, K * dy : K * (dy + 1), NB:HW])
+                nc.sync.dma_start(out=rows[:, 0:K, :], in_=logits_v[:, K * dy : K * (dy + 1), NU:HW])
                 return rows
 
             def best_of(rows, dest):
@@ -292,9 +327,8 @@ def tile_sam_pb_t_kernel(tc, logits, x, w3c_words, w3c_scales, b3c, out):
                 nc.vector.tensor_tensor(out=t4[:, 0:2, :], in0=t4[:, 0:2, :], in1=t4[:, 2:4, :], op=ALU.max)
                 nc.vector.tensor_tensor(out=dest, in0=t4[:, 0, :], in1=t4[:, 1, :], op=ALU.max)
 
+            parts = [(0, 5, 0, 8, (256,)), (5, H, 8, XROWS, (512, 256, 128))]
             load_logits(0)
-            load_logits(1)
-            raws = {b: load_x(b) for b in range(3)}
             nc.vector.memset(w_plane[:].bitcast(I32), 0)
             words_src = w3c_words[0].bitcast(I32).rearrange("p (h g w) -> p g h w", g=GROUPS, h=HEADS)
             words_dst = w_words[:].bitcast(I32).rearrange("p (g h w) -> p g h w", g=GROUPS, h=HEADS)
@@ -306,30 +340,69 @@ def tile_sam_pb_t_kernel(tc, logits, x, w3c_words, w3c_scales, b3c, out):
                 plane_dst = plane_dst.rearrange("q (g h w) -> q g h w", g=GROUPS, h=HEADS)
                 for g in range(GROUPS):
                     nc.sync.dma_start(out=plane_dst[:, g], in_=scales_src[4 * quad : 4 * quad + 4, g])
-
-            first_top(0)
-            softmax_exp(0, state[0], 0, NU)
-            first_top(1)
-            rows_of = {}
-            grouped_of = {0: group_x(raws[0])}
-            raws[3] = load_x(3)
-            for b in range(B):
-                if b + 1 < B:
-                    grouped_of[b + 1] = group_x(raws[b + 1])
-                    rows_of[b] = load_rows(b)
-                quantise_x(b, grouped_of[b])
             for b in range(B):
                 nc.sync.dma_start(
                     out=bias_bf[b * HEADS : (b + 1) * HEADS, :], in_=b3c.rearrange("(h c) -> h c", c=SP)
                 )
-            softmax_recip(state[0])
+            raws = {(b, 0): load_x(xa, b, parts[0][0], parts[0][1]) for b in range(B)}
+            for b in range(3):
+                raws[(b, 1)] = load_x(xin, b, parts[1][0], parts[1][1])
+
+            grouped = {}
+            rows_of = {}
+
+            def group(b, part):
+                r0, r1, p0, p1, widths = parts[part]
+                grouped[(b, part)] = group_x(raws[(b, part)], r0, r1, p0, p1)
+                if part == 1:
+                    if b == 0:
+                        raws[(3, 1)] = load_x(xin, 3, r0, r1)
+                    elif b < 3:
+                        rows_of[b - 1] = load_rows(b - 1)
+
+            def quantise(b, part):
+                r0, r1, p0, p1, widths = parts[part]
+                quantise_x(b, grouped[(b, part)], p0, widths)
+
+            first_top(0)
+            softmax_exp(0, state[0], 0, NU)
+            group(0, 0)
+            for b in range(1, B):
+                group(b, 0)
+                quantise(b - 1, 0)
+            quantise(B - 1, 0)
+            nc.vector.tensor_copy(out=bias[:], in_=bias_bf[:])
+            fold(nc.vector, 0, state[0])
+            between = [
+                [],
+                [lambda: group(0, 1)],
+                [lambda: group(1, 1)],
+                [lambda: quantise(0, 1), lambda: group(2, 1)],
+            ]
             for t in range(2):
                 for g in range(GROUPS):
-                    jobs = [mx_task(t, g, 0), mx_task(t, g, 2)] + [turn_task(t, g, bank) for bank in range(CG // PER_BANK)]
+                    for task in between[2 * t + g]:
+                        task()
+                    jobs = [mx_task(t, g, 0, True), mx_task(t, g, 2, True)]
                     for fill, drain in jobs:
                         fill()
+                    for fill, drain in jobs:
                         drain()
-                pad_columns(t)
+                    for bank in range(CG // PER_BANK):
+                        fill, drain = turn_task(t, g, bank)
+                        fill()
+                        drain()
+            pad_columns(0)
+            pad_columns(1)
+            quantise(1, 1)
+            group(3, 1)
+            quantise(2, 1)
+            quantise(3, 1)
+            softmax_recip(state[0])
+            other_weights(0, state[0])
+            for k in range(NCHUNKS):
+                for part in v_weights(0, state[0], k):
+                    part()
 
             def later_top(dy):
                 if dy == 0:
@@ -338,33 +411,16 @@ def tile_sam_pb_t_kernel(tc, logits, x, w3c_words, w3c_scales, b3c, out):
                     best_of(rows_of[dy], rows_of[dy + 1][:, K, :])
                 else:
                     best_of(rows_of[dy], rows_of[dy][:, K, :])
-                    nc.vector.tensor_scalar_mul(out=neg_top[:, NB:HW], in0=rows_of[dy][:, K, :], scalar1=-1.0)
+                    nc.vector.tensor_scalar_mul(out=neg_top[:, NU:HW], in0=rows_of[dy][:, K, :], scalar1=-1.0)
                 if dy + 3 < K:
                     rows_of[dy + 3] = load_rows(dy + 3)
 
-            later_top(0)
-            later_top(1)
-            wl0 = state[0]["wl"]
-            nc.vector.tensor_tensor(
-                out=wl0[:, :, 0:KK],
-                in0=wl0[:, :, 0:KK],
-                in1=state[0]["inv"][:].unsqueeze(2).to_broadcast([P, NU, KK]),
-                op=ALU.mult,
-            )
-            for dy in range(2, K):
+            rows_of[2] = load_rows(2)
+            for dy in range(K):
                 later_top(dy)
-            nc.vector.tensor_copy(out=bias[:], in_=bias_bf[:])
-            other_weights(state[0])
-            for k in range(NCHUNKS):
-                for part in v_weights(state[0], k):
-                    part()
-            for b0 in (0, 2):
-                for part in mx_task(2, 0, b0):
-                    part()
-
+            load_logits(1)
         prodv_pool = ctx.enter_context(tc.tile_pool(name="prodv", bufs=3))
-        prodg_pool = ctx.enter_context(tc.tile_pool(name="prodg", bufs=3))
-        prods_pool = ctx.enter_context(tc.tile_pool(name="prods", bufs=3))
+        prodg_pool = ctx.enter_context(tc.tile_pool(name="prodg", bufs=4))
         sums_pool = ctx.enter_context(tc.tile_pool(name="sums", bufs=1))
         res_pool = ctx.enter_context(tc.tile_pool(name="res", bufs=1))
 
@@ -388,33 +444,45 @@ def tile_sam_pb_t_kernel(tc, logits, x, w3c_words, w3c_scales, b3c, out):
                 )
 
         sums_of = {}
-        added = {u: 0 for u in range(UNITS)}
-        NADDS = NV + NS + NG - GADD
+        added = {(u, bank): 0 for u in range(UNITS) for bank in range(BANKS)}
+        S_ITEMS = []
+        for u in range(UNITS):
+            ls0 = FULL[u][0] + NV[u] + NG[u]
+            items = [(i, ls0 + i, n) for i in range(NS[u]) for n in range(NU)]
+            if HALF[u]:
+                dy, r = HALF[u]
+                items = [(NS[u] + dx, K * dy + dx, n) for dx in range(K) for n in range(r * W, (r + 1) * W)] + items
+            S_ITEMS.append(items)
+        NADDS = {}
+        for u in range(UNITS):
+            for bank in range(BANKS):
+                pieces = len([1 for i, l, n in S_ITEMS[u] if n == bank * NPOS])
+                NADDS[(u, bank)] = NV[u] + NG[u] - GADD[u] + pieces
 
-        def add(u, prod):
-            flat = prod[:].rearrange("p n c -> p (n c)")
-            if added[u] == 0:
-                sums_of[u] = []
-                for bank in range(BANKS):
-                    sums = acc_pool.tile([P, PER_BANK, P], F32, name="sums%d" % bank)
-                    sums_of[u].append(sums)
-            for blk in range(BLOCKS):
-                bank, j = divmod(blk, PER_BANK)
+        def add_bank(u, bank, flat):
+            if added[(u, bank)] == 0:
+                sums = acc_pool.tile([P, PER_BANK, P], F32, tag="sums%d" % bank, name="sums")
+                sums_of[(u, bank)] = sums
+            for j in range(PER_BANK):
                 nc.tensor.matmul(
-                    out=sums_of[u][bank][:, j, :],
-                    lhsT=flat[:, blk * P : (blk + 1) * P],
+                    out=sums_of[(u, bank)][:, j, :],
+                    lhsT=flat[:, j * P : (j + 1) * P],
                     rhs=ident[:],
                     is_transpose=True,
-                    start=(added[u] == 0 and j == 0),
-                    stop=(added[u] == NADDS - 1 and j == PER_BANK - 1),
+                    start=(added[(u, bank)] == 0 and j == 0),
+                    stop=(added[(u, bank)] == NADDS[(u, bank)] - 1 and j == PER_BANK - 1),
                 )
-            added[u] += 1
+            added[(u, bank)] += 1
+
+        def add(u, prod):
+            for bank in range(BANKS):
+                add_bank(u, bank, prod[:, bank * NPOS : (bank + 1) * NPOS, :].rearrange("p n c -> p (n c)"))
 
         gprods = {}
 
         def g_multiply(u, i):
             pg = prodg_pool.tile([P, NU, SP], F32, name="pg")
-            multiply(nc.gpsimd, u, NV + i, pg, state[u]["wg"][:, i, :])
+            multiply(nc.gpsimd, u, FULL[u][0] + NV[u] + i, pg, state[u]["wg"][:, i, :])
             gprods[(u, i)] = pg
 
         def g_add(u, i):
@@ -425,18 +493,23 @@ def tile_sam_pb_t_kernel(tc, logits, x, w3c_words, w3c_scales, b3c, out):
         sprods = {}
 
         def s_multiply(u, e):
-            i, n = divmod(e, NU)
-            if n == 0:
-                ps = prods_pool.tile([P, NU, SP], F32, name="ps")
-                sprods[(u, i)] = ps
-            dy, dx = divmod(NV + NG + i, K)
+            i, l, n = S_ITEMS[u][e]
+            piece, k = divmod(e, NPOS)
+            if k == 0:
+                ps = prods_pool.tile([P, NPOS, SP], F32, name="ps")
+                sprods[(u, piece)] = ps
+            dy, dx = divmod(l, K)
             r, q = divmod(n, W)
             nc.scalar.activation(
-                out=sprods[(u, i)][:, n, :],
+                out=sprods[(u, piece)][:, k, :],
                 in_=xmap[:, (UROWS * u + dy + r) % RING, q + dx, :],
                 func=ACT.Copy,
                 scale=state[u]["ws"][:, n, i : i + 1],
             )
+
+        def add_piece(u, i):
+            bank = S_ITEMS[u][i * NPOS][2] // NPOS
+            add_bank(u, bank, sprods[(u, i)][:].rearrange("p n c -> p (n c)"))
 
         sums_sb_of = {}
         result_of = {}
@@ -444,7 +517,7 @@ def tile_sam_pb_t_kernel(tc, logits, x, w3c_words, w3c_scales, b3c, out):
         def take_sums(u):
             sums_sb = sums_pool.tile([P, BLOCKS, P], F32, name="sums_sb")
             for bank in range(BANKS):
-                nc.scalar.copy(out=sums_sb[:, bank * PER_BANK : (bank + 1) * PER_BANK, :], in_=sums_of[u][bank][:])
+                nc.scalar.copy(out=sums_sb[:, bank * PER_BANK : (bank + 1) * PER_BANK, :], in_=sums_of[(u, bank)][:])
             sums_sb_of[u] = sums_sb
 
         def back_task(u, bank):
@@ -462,12 +535,12 @@ def tile_sam_pb_t_kernel(tc, logits, x, w3c_words, w3c_scales, b3c, out):
                 if bank == 0:
                     result = res_pool.tile([P, SP, NU], F32, name="result")
                     result_of[u] = result
-                npos = PER_BANK * P // SP
+                inv = state[u]["inv"][:, bank * NPOS : (bank + 1) * NPOS]
                 nc.vector.tensor_tensor(
-                    out=result_of[u][:, :, bank * npos : (bank + 1) * npos],
+                    out=result_of[u][:, :, bank * NPOS : (bank + 1) * NPOS],
                     in0=hold["back"][:].rearrange("p (n c) -> p c n", c=SP),
-                    in1=bias[:].unsqueeze(2).to_broadcast([P, SP, npos]),
-                    op=ALU.add,
+                    in1=inv.unsqueeze(1).to_broadcast([P, SP, NPOS]),
+                    op=ALU.mult,
                 )
                 if bank == BANKS - 1:
                     nc.sync.dma_start(out=out_v[:, :, u * NU : (u + 1) * NU], in_=result_of[u][:])
@@ -477,13 +550,11 @@ def tile_sam_pb_t_kernel(tc, logits, x, w3c_words, w3c_scales, b3c, out):
         GLEAD, GLAG = 1, 1
         SLEAD, SLAG = 2, 1
         BACK0 = 1
-        WPS0 = 24
+        g_at, s_at, take_at, small_at, drain_at, fill_at = {}, {}, {}, {}, {}, {}
         wps_of = {}
 
         def take_wps(u, c):
-            wps_of[(u, c)] = load_wps(c)
-
-        g_at, s_at, take_at, small_at, drain_at, fill_at = {}, {}, {}, {}, {}, {}
+            wps_of[(u, c)] = load_wps(u, c)
 
         def put(where, t, task):
             where.setdefault(max(t, 0), []).append(task)
@@ -499,23 +570,24 @@ def tile_sam_pb_t_kernel(tc, logits, x, w3c_words, w3c_scales, b3c, out):
                 put(small_at, t0 + first + i, lambda n0=n0, n1=n1: task(n0, n1))
 
         for u in range(UNITS):
-            t0 = u * NV
-            last = t0 + NV - 1
+            t0, nv, ng = TSTART[u], NV[u], NG[u]
+            last = t0 + nv - 1
             jobs = []
-            for i in range(NG):
+            for i in range(ng):
                 jobs.append((g_multiply, i))
-                if i % 2 == 1 and i // 2 < GADD:
+                if i % 2 == 1 and i // 2 < GADD[u]:
                     jobs.append((g_add, i - 1))
             for k, (job, i) in enumerate(jobs):
-                put(g_at, t0 + k * NV // len(jobs) - GLEAD, lambda job=job, u=u, i=i: job(u, i))
-                if job is g_add or i >= 2 * GADD:
-                    done = t0 - GLEAD - (-(k + 1) * NV // len(jobs)) + GLAG
+                put(g_at, t0 + k * nv // len(jobs) - GLEAD, lambda job=job, u=u, i=i: job(u, i))
+                if job is g_add or i >= 2 * GADD[u]:
+                    done = t0 - GLEAD - (-(k + 1) * nv // len(jobs)) + GLAG
                     put(take_at, min(max(done, t0), last), lambda u=u, i=i: add(u, gprods[(u, i)]))
-            for e in range(NS * NU):
-                put(s_at, t0 + e * NV // (NS * NU) - SLEAD, lambda u=u, e=e: s_multiply(u, e))
-            for i in range(NS):
-                done = t0 - SLEAD - (-(i + 1) * NV // NS) + SLAG
-                put(take_at, min(max(done, t0), last), lambda u=u, i=i: add(u, sprods[(u, i)]))
+            count = len(S_ITEMS[u]) if u else 0
+            for e in range(count):
+                put(s_at, t0 + e * nv // count - SLEAD, lambda u=u, e=e: s_multiply(u, e))
+            for i in range(count // NPOS):
+                done = t0 - SLEAD - (-(i + 1) * NPOS * nv // count) + SLAG
+                put(take_at, min(max(done, t0), last), lambda u=u, i=i: add_piece(u, i))
             if u:
                 put(drain_at, t0, lambda u=u: take_sums(u - 1))
                 for bank in range(BANKS):
@@ -524,51 +596,59 @@ def tile_sam_pb_t_kernel(tc, logits, x, w3c_words, w3c_scales, b3c, out):
             t = k + 2
             if not odd:
                 if t < TILES:
+                    first = 5 if u else 0
                     for bank in range(4):
-                        stage_tasks(t0 + 5 + bank, turn_task(t, 0, bank), 1)
-                        stage_tasks(t0 + 14 + bank, turn_task(t, 1, bank), 1)
-                    stage_tasks(t0 + 10, mx_task(t, 1, 0), 1)
-                    stage_tasks(t0 + 12, mx_task(t, 1, 2), 1)
-                    put(small_at, t0 + 19, lambda t=t: pad_columns(t))
+                        stage_tasks(t0 + first + bank, turn_task(t, 0, bank), 2)
+                        stage_tasks(t0 + first + 9 + bank, turn_task(t, 1, bank), 2)
+                    stage_tasks(t0 + first + 5, mx_task(t, 1, 0), 1)
+                    stage_tasks(t0 + first + 7, mx_task(t, 1, 2), 1)
+                    put(small_at, t0 + first + 15, lambda t=t: pad_columns(t))
             elif t + 1 < TILES:
                 stage_tasks(t0 + 10, mx_task(t + 1, 0, 0), 1)
                 stage_tasks(t0 + 12, mx_task(t + 1, 0, 2), 1)
             for c in range(NCHUNKS):
-                after = t0 + 2 * CSTART[c + 1] - 1
+                after = t0 + 2 * CSTART[u][c + 1] - 1
                 if c + 2 < NCHUNKS:
                     put(fill_at, after, lambda u=u, c=c: take_wps(u, c + 2))
                 elif u + 1 < UNITS:
-                    put(fill_at, max(after, t0 + WPS0), lambda u=u, c=c: take_wps(u + 1, c + 2 - NCHUNKS))
+                    put(fill_at, max(after, last - 3 if u else last - 2), lambda u=u, c=c: take_wps(u + 1, c + 2 - NCHUNKS))
             if u + 2 < UNITS:
                 put(small_at, t0 + 1, lambda u=u: load_logits(u + 2))
             if u + 1 < UNITS:
                 st = state[u + 1]
-                spread(t0, 0, 13, NU, lambda n0, n1, u=u, st=st: softmax_exp(u + 1, st, n0, n1))
-                put(small_at, t0 + 14, lambda st=st: softmax_recip(st))
-                spread(t0, 15, 6, NU, lambda n0, n1, st=st: softmax_norm(st, n0, n1))
-                put(small_at, t0 + 21, lambda st=st: other_weights(st))
+                spread(t0, 0, nv - 10, NU, lambda n0, n1, u=u, st=st: softmax_exp(u + 1, st, n0, n1))
+                wv = last - 6 if u else last - 4
+                put(g_at, wv - 3, lambda u=u, st=st: fold(nc.gpsimd, u + 1, st))
+                put(small_at, wv - 2, lambda u=u, st=st: other_weights(u + 1, st))
+                put(small_at, last - 2, lambda st=st: softmax_recip(st))
                 for c in range(NCHUNKS):
-                    gather, fill, drain = v_weights(st, c)
-                    put(small_at, t0 + 21 + c, gather)
-                    stage_tasks(t0 + 22 + c, (fill, drain), 1)
+                    gather, fill, drain = v_weights(u + 1, st, c)
+                    put(small_at, wv - 1 + c, gather)
+                    stage_tasks(wv + c, (fill, drain), 1)
 
         take_wps(0, 0)
         take_wps(0, 1)
-        chunk_of = [k for k in range(NCHUNKS) for i in range(CSTART[k], CSTART[k + 1]) for two in range(2)]
-        for t in range(UNITS * NV):
-            u, s = divmod(t, NV)
-            for job in g_at.get(t, []):
-                job()
-            k = chunk_of[s]
-            pv = prodv_pool.tile([P, NU, SP], F32, name="pv")
-            multiply(nc.vector, u, s, pv, wps_of[(u, k)][:, s - 2 * CSTART[k], :])
-            for job in s_at.get(t, []) + small_at.get(t, []) + drain_at.get(t, []):
-                job()
-            add(u, pv)
-            for job in take_at.get(t, []):
-                job()
-            for job in fill_at.get(t, []):
-                job()
+        for e in range(len(S_ITEMS[0])):
+            s_multiply(0, e)
+            if e % NPOS == NPOS - 1:
+                add_piece(0, e // NPOS)
+        for b0 in (0, 2):
+            for part in mx_task(2, 0, b0):
+                part()
+        for u in range(UNITS):
+            chunk_of = [k for k in range(NCHUNKS) for i in range(CSTART[u][k], CSTART[u][k + 1]) for two in range(2)]
+            for s in range(NV[u]):
+                t = TSTART[u] + s
+                for job in g_at.get(t, []):
+                    job()
+                k = chunk_of[s]
+                pv = prodv_pool.tile([P, NU, SP], F32, name="pv")
+                multiply(nc.vector, u, FULL[u][0] + s, pv, wps_of[(u, k)][:, s - 2 * CSTART[u][k], :])
+                for job in s_at.get(t, []) + small_at.get(t, []) + drain_at.get(t, []):
+                    job()
+                add(u, pv)
+                for job in take_at.get(t, []) + fill_at.get(t, []):
+                    job()
         take_sums(UNITS - 1)
         for bank in range(BANKS):
             for part in back_task(UNITS - 1, bank):

@@ -70,15 +70,18 @@ def edge_rows():
 FOLDS, FULL, HALF = edge_rows()
 
 INNER = UNITS - 4
-NV = [18, 26] + [26 + 2 * (i % 2) for i in range(INNER)] + [26, 16]
-NG = [7, 9] + [11 - i % 2 for i in range(INNER)] + [9, 6]
+NV = [14, 26] + [26 + 2 * (i % 2) for i in range(INNER)] + [26, 16]
+NG = [8, 9] + [11 - i % 2 for i in range(INNER)] + [9, 6]
 NS = [FULL[u][1] - FULL[u][0] - NV[u] - NG[u] for u in range(UNITS)]
-GADD = [2, 3] + [4 for i in range(INNER)] + [3, 2]
+GADD = [2, 3] + [4 for i in range(INNER)] + [3, 3]
 
 CHUNK_PAIRS = 4
 NCHUNKS = 4
 CSTART = [[k * (NV[u] // 2) // NCHUNKS for k in range(NCHUNKS + 1)] for u in range(UNITS)]
-TSTART = [sum(NV[:u]) for u in range(UNITS + 1)]
+STEPS = [18] + NV[1:]
+TSTART = [sum(STEPS[:u]) for u in range(UNITS + 1)]
+
+EARLY = 6 * NU
 
 FLOPS = 2 * B * COUT * HW * CIN + 2 * B * COUT * HW * KK
 
@@ -233,7 +236,8 @@ def tile_sam_pb_t_kernel(tc, logits, x, w3c_words, w3c_scales, b3c, out):
             return fill, drain
 
         def turn_task(t, g, bank):
-            slot = TROWS * t % RING
+            r0 = PAD if t == 0 else 0
+            slot = TROWS * t % RING + r0
             c0 = g * CG + bank * PER_BANK
             hold = {}
 
@@ -249,9 +253,9 @@ def tile_sam_pb_t_kernel(tc, logits, x, w3c_words, w3c_scales, b3c, out):
 
             def drain():
                 nc.vector.tensor_tensor(
-                    out=xmap[:, slot : slot + TROWS, PAD : PAD + W, c0 : c0 + PER_BANK],
-                    in0=hold["x3"][:].rearrange("p j r q -> p r q j"),
-                    in1=bias[:, c0 : c0 + PER_BANK].unsqueeze(1).unsqueeze(1).to_broadcast([P, TROWS, W, PER_BANK]),
+                    out=xmap[:, slot : slot + TROWS - r0, PAD : PAD + W, c0 : c0 + PER_BANK],
+                    in0=hold["x3"][:, :, r0:TROWS, :].rearrange("p j r q -> p r q j"),
+                    in1=bias[:, c0 : c0 + PER_BANK].unsqueeze(1).unsqueeze(1).to_broadcast([P, TROWS - r0, W, PER_BANK]),
                     op=ALU.add,
                 )
 
@@ -259,165 +263,154 @@ def tile_sam_pb_t_kernel(tc, logits, x, w3c_words, w3c_scales, b3c, out):
 
         def pad_columns(t):
             slot = TROWS * t % RING
-            rows = slice(slot, slot + TROWS)
+            rows = slice(slot + (PAD if t == 0 else 0), slot + TROWS)
             for q in range(WP):
                 src = reflect(q - PAD, W) + PAD
                 if src != q:
                     nc.scalar.copy(out=xmap[:, rows, q, :], in_=xmap[:, rows, src, :])
 
         state = {u: {} for u in range(UNITS)}
-        with tc.tile_pool(name="xin", bufs=3) as xin, tc.tile_pool(name="xa", bufs=4) as xa, tc.tile_pool(
-            name="xg", bufs=2
-        ) as xg, tc.tile_pool(name="xt", bufs=1) as xt:
-            rest = HW - NU
+        rest = HW - NU
 
-            def load_x(pool, b, r0, r1):
-                raw = pool.tile([P, PACK, (r1 - r0) * W], BF16, tag="inp", name="raw")
-                nc.sync.dma_start(out=raw[:], in_=x[b].rearrange("(p t) i j -> p t (i j)", t=PACK)[:, :, r0 * W : r1 * W])
-                return raw
+        def load_rows(pool, dy):
+            rows = pool.tile([P, K, rest], BF16, tag="inp", name="rows")
+            nc.sync.dma_start(out=rows[:], in_=logits_v[:, K * dy : K * (dy + 1), NU:HW])
+            return rows
 
-            def group_x(raw, r0, r1, p0, p1):
-                grouped = xg.tile([P, (p1 - p0) * W, PACK], BF16, align_bytes=64, name="grouped")
-                first, last = max(p0, PAD + r0), min(p1, PAD + r1)
-                nc.vector.tensor_copy(
-                    out=grouped[:, (first - p0) * W : (last - p0) * W, :].rearrange("p (c i) t -> p c t i", i=4),
-                    in_=raw[:, :, (first - PAD - r0) * W : (last - PAD - r0) * W].rearrange("p t (c i) -> p c t i", i=4),
-                )
-                for r in range(p0, p1):
-                    src = reflect(r - PAD, H) - r0
-                    if src != r - PAD - r0:
-                        nc.vector.tensor_copy(
-                            out=grouped[:, (r - p0) * W : (r - p0 + 1) * W, :],
-                            in_=raw[:, :, src * W : (src + 1) * W].rearrange("p t n -> p n t"),
+        rows_of = {}
+        with tc.tile_pool(name="xin", bufs=3) as xin:
+            with tc.tile_pool(name="xa", bufs=4) as xa, tc.tile_pool(name="xb", bufs=2) as xb, tc.tile_pool(
+                name="xg", bufs=2
+            ) as xg, tc.tile_pool(name="xt", bufs=1) as xt:
+
+                def load_x(pool, b, r0, r1):
+                    raw = pool.tile([P, PACK, (r1 - r0) * W], BF16, tag="inp", name="raw")
+                    nc.sync.dma_start(out=raw[:], in_=x[b].rearrange("(p t) i j -> p t (i j)", t=PACK)[:, :, r0 * W : r1 * W])
+                    return raw
+
+                def group_x(raw, r0, r1, p0, p1):
+                    grouped = xg.tile([P, (p1 - p0) * W, PACK], BF16, align_bytes=64, name="grouped")
+                    first, last = max(p0, PAD + r0), min(p1, PAD + r1)
+                    nc.vector.tensor_copy(
+                        out=grouped[:, (first - p0) * W : (last - p0) * W, :].rearrange("p (c i) t -> p c t i", i=4),
+                        in_=raw[:, :, (first - PAD - r0) * W : (last - PAD - r0) * W].rearrange("p t (c i) -> p c t i", i=4),
+                    )
+                    for f0, f1 in ((p0, first), (last, p1)):
+                        if f0 < f1:
+                            nc.vector.tensor_copy(
+                                out=grouped[:, (f0 - p0) * W : (f1 - p0) * W, :],
+                                in_=raw[:, :, 0 : (f1 - f0) * W].rearrange("p t n -> p n t"),
+                            )
+                    return grouped
+
+                def quantise_x(b, grouped, p0, widths):
+                    flat = grouped[:].rearrange("p n t -> p (n t)")
+                    first = 0
+                    for width in widths:
+                        n0 = p0 * W + first
+                        nc.vector.quantize_mx(
+                            out=x_codes[:, b, n0 : n0 + width].bitcast(FP8X4),
+                            scales=x_plane[:, b, n0 : n0 + width],
+                            in_=flat[:, PACK * first : PACK * (first + width)],
                         )
-                return grouped
+                        first += width
 
-            def quantise_x(b, grouped, p0, widths):
-                flat = grouped[:].rearrange("p n t -> p (n t)")
-                first = 0
-                for width in widths:
-                    n0 = p0 * W + first
-                    nc.vector.quantize_mx(
-                        out=x_codes[:, b, n0 : n0 + width].bitcast(FP8X4),
-                        scales=x_plane[:, b, n0 : n0 + width],
-                        in_=flat[:, PACK * first : PACK * (first + width)],
-                    )
-                    first += width
+                def first_top(u):
+                    lg = lgs[u]
+                    top = xt.tile([P, KK // 2, NU], BF16, name="top")
+                    nc.vector.tensor_tensor(out=top[:], in0=lg[:, 0:24, :], in1=lg[:, 24:48, :], op=ALU.max)
+                    for half in (12, 6, 3):
+                        nc.vector.tensor_tensor(
+                            out=top[:, 0:half, :], in0=top[:, 0:half, :], in1=top[:, half : 2 * half, :], op=ALU.max
+                        )
+                    for other in (top[:, 1, :], top[:, 2, :], lg[:, KK - 1, :]):
+                        nc.vector.tensor_tensor(out=top[:, 0, :], in0=top[:, 0, :], in1=other, op=ALU.max)
+                    nc.vector.tensor_scalar_mul(out=neg_top[:, u * NU : (u + 1) * NU], in0=top[:, 0, :], scalar1=-1.0)
 
-            def first_top(u):
-                lg = lgs[u]
-                top = xt.tile([P, KK // 2, NU], BF16, name="top")
-                nc.vector.tensor_tensor(out=top[:], in0=lg[:, 0:24, :], in1=lg[:, 24:48, :], op=ALU.max)
-                for half in (12, 6, 3):
-                    nc.vector.tensor_tensor(
-                        out=top[:, 0:half, :], in0=top[:, 0:half, :], in1=top[:, half : 2 * half, :], op=ALU.max
-                    )
-                for other in (top[:, 1, :], top[:, 2, :], lg[:, KK - 1, :]):
-                    nc.vector.tensor_tensor(out=top[:, 0, :], in0=top[:, 0, :], in1=other, op=ALU.max)
-                nc.vector.tensor_scalar_mul(out=neg_top[:, u * NU : (u + 1) * NU], in0=top[:, 0, :], scalar1=-1.0)
-
-            def load_rows(dy):
-                rows = xin.tile([P, K + 1, rest], BF16, tag="inp", name="rows")
-                nc.sync.dma_start(out=rows[:, 0:K, :], in_=logits_v[:, K * dy : K * (dy + 1), NU:HW])
-                return rows
-
-            def best_of(rows, dest):
-                t4 = xt.tile([P, 4, rest], BF16, name="t4")
-                nc.vector.tensor_tensor(out=t4[:], in0=rows[:, 0:4, :], in1=rows[:, 4:8, :], op=ALU.max)
-                nc.vector.tensor_tensor(out=t4[:, 0:2, :], in0=t4[:, 0:2, :], in1=t4[:, 2:4, :], op=ALU.max)
-                nc.vector.tensor_tensor(out=dest, in0=t4[:, 0, :], in1=t4[:, 1, :], op=ALU.max)
-
-            parts = [(0, 5, 0, 8, (256,)), (5, H, 8, XROWS, (512, 256, 128))]
-            load_logits(0)
-            nc.vector.memset(w_plane[:].bitcast(I32), 0)
-            words_src = w3c_words[0].bitcast(I32).rearrange("p (h g w) -> p g h w", g=GROUPS, h=HEADS)
-            words_dst = w_words[:].bitcast(I32).rearrange("p (g h w) -> p g h w", g=GROUPS, h=HEADS)
-            scales_src = w3c_scales[0].bitcast(I32).rearrange("q (h g w) -> q g h w", g=GROUPS, h=HEADS)
-            for g in range(GROUPS):
-                nc.sync.dma_start(out=words_dst[:, g], in_=words_src[:, g])
-            for quad in range(4):
-                plane_dst = w_plane[32 * quad : 32 * quad + 4, :].bitcast(I32)
-                plane_dst = plane_dst.rearrange("q (g h w) -> q g h w", g=GROUPS, h=HEADS)
+                parts = [(0, 5, 0, 8, (256,)), (5, H, 8, XROWS, (512, 256, 128))]
+                raws = {(b, 0): load_x(xa, b, parts[0][0], parts[0][1]) for b in range(B)}
+                load_logits(0)
+                for b in range(2):
+                    raws[(b, 1)] = load_x(xb, b, parts[1][0], parts[1][1])
+                nc.vector.memset(w_plane[:].bitcast(I32), 0)
+                words_src = w3c_words[0].bitcast(I32).rearrange("p (h g w) -> p g h w", g=GROUPS, h=HEADS)
+                words_dst = w_words[:].bitcast(I32).rearrange("p (g h w) -> p g h w", g=GROUPS, h=HEADS)
+                scales_src = w3c_scales[0].bitcast(I32).rearrange("q (h g w) -> q g h w", g=GROUPS, h=HEADS)
                 for g in range(GROUPS):
-                    nc.sync.dma_start(out=plane_dst[:, g], in_=scales_src[4 * quad : 4 * quad + 4, g])
-            for b in range(B):
-                nc.sync.dma_start(
-                    out=bias_bf[b * HEADS : (b + 1) * HEADS, :], in_=b3c.rearrange("(h c) -> h c", c=SP)
-                )
-            raws = {(b, 0): load_x(xa, b, parts[0][0], parts[0][1]) for b in range(B)}
-            for b in range(3):
-                raws[(b, 1)] = load_x(xin, b, parts[1][0], parts[1][1])
+                    nc.sync.dma_start(out=words_dst[:, g], in_=words_src[:, g])
+                for quad in range(4):
+                    plane_dst = w_plane[32 * quad : 32 * quad + 4, :].bitcast(I32)
+                    plane_dst = plane_dst.rearrange("q (g h w) -> q g h w", g=GROUPS, h=HEADS)
+                    for g in range(GROUPS):
+                        nc.sync.dma_start(out=plane_dst[:, g], in_=scales_src[4 * quad : 4 * quad + 4, g])
+                for b in range(B):
+                    nc.sync.dma_start(
+                        out=bias_bf[b * HEADS : (b + 1) * HEADS, :], in_=b3c.rearrange("(h c) -> h c", c=SP)
+                    )
 
-            grouped = {}
-            rows_of = {}
+                grouped = {}
 
-            def group(b, part):
-                r0, r1, p0, p1, widths = parts[part]
-                grouped[(b, part)] = group_x(raws[(b, part)], r0, r1, p0, p1)
-                if part == 1:
-                    if b == 0:
-                        raws[(3, 1)] = load_x(xin, 3, r0, r1)
-                    elif b < 3:
-                        rows_of[b - 1] = load_rows(b - 1)
+                def group(b, part):
+                    r0, r1, p0, p1, widths = parts[part]
+                    grouped[(b, part)] = group_x(raws[(b, part)], r0, r1, p0, p1)
+                    if part == 1:
+                        if b + 2 < B:
+                            raws[(b + 2, 1)] = load_x(xb, b + 2, r0, r1)
+                        if b < 3:
+                            rows_of[b] = load_rows(xin, b)
 
-            def quantise(b, part):
-                r0, r1, p0, p1, widths = parts[part]
-                quantise_x(b, grouped[(b, part)], p0, widths)
+                def quantise(b, part):
+                    r0, r1, p0, p1, widths = parts[part]
+                    quantise_x(b, grouped[(b, part)], p0, widths)
 
-            first_top(0)
-            softmax_exp(0, state[0], 0, NU)
-            group(0, 0)
-            for b in range(1, B):
-                group(b, 0)
-                quantise(b - 1, 0)
-            quantise(B - 1, 0)
-            nc.vector.tensor_copy(out=bias[:], in_=bias_bf[:])
-            fold(nc.vector, 0, state[0])
-            between = [
-                [],
-                [lambda: group(0, 1)],
-                [lambda: group(1, 1)],
-                [lambda: quantise(0, 1), lambda: group(2, 1)],
-            ]
-            for t in range(2):
-                for g in range(GROUPS):
-                    for task in between[2 * t + g]:
-                        task()
-                    jobs = [mx_task(t, g, 0, True), mx_task(t, g, 2, True)]
-                    for fill, drain in jobs:
-                        fill()
-                    for fill, drain in jobs:
-                        drain()
-                    for bank in range(CG // PER_BANK):
-                        fill, drain = turn_task(t, g, bank)
-                        fill()
-                        drain()
-            pad_columns(0)
-            pad_columns(1)
-            quantise(1, 1)
-            group(3, 1)
-            quantise(2, 1)
-            quantise(3, 1)
-            softmax_recip(state[0])
-            other_weights(0, state[0])
-            for k in range(NCHUNKS):
-                for part in v_weights(0, state[0], k):
-                    part()
+                group(0, 0)
+                for b in range(1, B):
+                    group(b, 0)
+                    quantise(b - 1, 0)
+                quantise(B - 1, 0)
+                first_top(0)
+                softmax_exp(0, state[0], 0, NU)
+                group(0, 1)
+                group(1, 1)
+                quantise(0, 1)
+                nc.vector.tensor_copy(out=bias[:], in_=bias_bf[:])
+                fold(nc.vector, 0, state[0])
+                between = [[], [lambda: group(2, 1)], [lambda: quantise(1, 1)], [lambda: group(3, 1)]]
+                for t in range(2):
+                    for g in range(GROUPS):
+                        for task in between[2 * t + g]:
+                            task()
+                        jobs = [mx_task(t, g, 0, True), mx_task(t, g, 2, True)]
+                        for fill, drain in jobs:
+                            fill()
+                        for fill, drain in jobs:
+                            drain()
+                        for bank in range(CG // PER_BANK):
+                            fill, drain = turn_task(t, g, bank)
+                            fill()
+                            drain()
+                pad_columns(0)
+                pad_columns(1)
+                quantise(2, 1)
+                quantise(3, 1)
+                softmax_recip(state[0])
+                other_weights(0, state[0])
+                for k in range(NCHUNKS):
+                    for part in v_weights(0, state[0], k):
+                        part()
 
-            def later_top(dy):
-                if dy == 0:
-                    nc.vector.tensor_copy(out=rows_of[0][:, K, :], in_=rows_of[0][:, 0, :])
-                if dy + 1 < K:
-                    best_of(rows_of[dy], rows_of[dy + 1][:, K, :])
-                else:
-                    best_of(rows_of[dy], rows_of[dy][:, K, :])
-                    nc.vector.tensor_scalar_mul(out=neg_top[:, NU:HW], in0=rows_of[dy][:, K, :], scalar1=-1.0)
-                if dy + 3 < K:
-                    rows_of[dy + 3] = load_rows(dy + 3)
-
-            rows_of[2] = load_rows(2)
-            for dy in range(K):
-                later_top(dy)
+            with tc.tile_pool(name="more", bufs=2) as more:
+                for dy in (3, 4):
+                    rows_of[dy] = load_rows(more, dy)
+                for dy in range(1, K):
+                    best = rows_of[dy]
+                    nc.vector.tensor_tensor(out=best[:], in0=rows_of[dy - 1][:], in1=best[:], op=ALU.max)
+                    if dy + 4 < K:
+                        rows_of[dy + 4] = load_rows(xin, dy + 4)
+            nc.vector.tensor_tensor(out=best[:, 0:3, :], in0=best[:, 0:3, :], in1=best[:, 3:6, :], op=ALU.max)
+            nc.vector.tensor_tensor(out=best[:, 0:2, :], in0=best[:, 0:2, :], in1=best[:, 2:7:4, :], op=ALU.max)
+            nc.vector.tensor_tensor(out=best[:, 0, :], in0=best[:, 0, :], in1=best[:, 1, :], op=ALU.max)
+            nc.vector.tensor_scalar_mul(out=neg_top[:, NU:HW], in0=best[:, 0, :], scalar1=-1.0)
             load_logits(1)
         prodv_pool = ctx.enter_context(tc.tile_pool(name="prodv", bufs=3))
         prodg_pool = ctx.enter_context(tc.tile_pool(name="prodg", bufs=4))
@@ -570,7 +563,7 @@ def tile_sam_pb_t_kernel(tc, logits, x, w3c_words, w3c_scales, b3c, out):
                 put(small_at, t0 + first + i, lambda n0=n0, n1=n1: task(n0, n1))
 
         for u in range(UNITS):
-            t0, nv, ng = TSTART[u], NV[u], NG[u]
+            t0, nv, ng = TSTART[u], STEPS[u], NG[u]
             last = t0 + nv - 1
             jobs = []
             for i in range(ng):
@@ -582,12 +575,13 @@ def tile_sam_pb_t_kernel(tc, logits, x, w3c_words, w3c_scales, b3c, out):
                 if job is g_add or i >= 2 * GADD[u]:
                     done = t0 - GLEAD - (-(k + 1) * nv // len(jobs)) + GLAG
                     put(take_at, min(max(done, t0), last), lambda u=u, i=i: add(u, gprods[(u, i)]))
-            count = len(S_ITEMS[u]) if u else 0
+            early = 0 if u else EARLY
+            count = len(S_ITEMS[u]) - early
             for e in range(count):
-                put(s_at, t0 + e * nv // count - SLEAD, lambda u=u, e=e: s_multiply(u, e))
+                put(s_at, t0 + e * nv // count - SLEAD, lambda u=u, e=early + e: s_multiply(u, e))
             for i in range(count // NPOS):
                 done = t0 - SLEAD - (-(i + 1) * NPOS * nv // count) + SLAG
-                put(take_at, min(max(done, t0), last), lambda u=u, i=i: add_piece(u, i))
+                put(take_at, min(max(done, t0), last), lambda u=u, i=early // NPOS + i: add_piece(u, i))
             if u:
                 put(drain_at, t0, lambda u=u: take_sums(u - 1))
                 for bank in range(BANKS):
@@ -607,7 +601,7 @@ def tile_sam_pb_t_kernel(tc, logits, x, w3c_words, w3c_scales, b3c, out):
                 stage_tasks(t0 + 10, mx_task(t + 1, 0, 0), 1)
                 stage_tasks(t0 + 12, mx_task(t + 1, 0, 2), 1)
             for c in range(NCHUNKS):
-                after = t0 + 2 * CSTART[u][c + 1] - 1
+                after = t0 + (2 * CSTART[u][c + 1] - 1) * STEPS[u] // NV[u]
                 if c + 2 < NCHUNKS:
                     put(fill_at, after, lambda u=u, c=c: take_wps(u, c + 2))
                 elif u + 1 < UNITS:
@@ -628,7 +622,7 @@ def tile_sam_pb_t_kernel(tc, logits, x, w3c_words, w3c_scales, b3c, out):
 
         take_wps(0, 0)
         take_wps(0, 1)
-        for e in range(len(S_ITEMS[0])):
+        for e in range(EARLY):
             s_multiply(0, e)
             if e % NPOS == NPOS - 1:
                 add_piece(0, e // NPOS)
@@ -637,16 +631,20 @@ def tile_sam_pb_t_kernel(tc, logits, x, w3c_words, w3c_scales, b3c, out):
                 part()
         for u in range(UNITS):
             chunk_of = [k for k in range(NCHUNKS) for i in range(CSTART[u][k], CSTART[u][k + 1]) for two in range(2)]
-            for s in range(NV[u]):
+            step_of = [i * STEPS[u] // NV[u] for i in range(NV[u])]
+            for s in range(STEPS[u]):
                 t = TSTART[u] + s
                 for job in g_at.get(t, []):
                     job()
-                k = chunk_of[s]
-                pv = prodv_pool.tile([P, NU, SP], F32, name="pv")
-                multiply(nc.vector, u, FULL[u][0] + s, pv, wps_of[(u, k)][:, s - 2 * CSTART[u][k], :])
+                if s in step_of:
+                    i = step_of.index(s)
+                    k = chunk_of[i]
+                    pv = prodv_pool.tile([P, NU, SP], F32, name="pv")
+                    multiply(nc.vector, u, FULL[u][0] + i, pv, wps_of[(u, k)][:, i - 2 * CSTART[u][k], :])
                 for job in s_at.get(t, []) + small_at.get(t, []) + drain_at.get(t, []):
                     job()
-                add(u, pv)
+                if s in step_of:
+                    add(u, pv)
                 for job in take_at.get(t, []) + fill_at.get(t, []):
                     job()
         take_sums(UNITS - 1)

@@ -70,14 +70,13 @@ def edge_rows():
 FOLDS, FULL, HALF = edge_rows()
 
 INNER = UNITS - 4
-NV = [14, 26] + [26 + 2 * (i % 2) for i in range(INNER)] + [26, 16]
-NG = [8, 9] + [11 - i % 2 for i in range(INNER)] + [9, 6]
-NS = [FULL[u][1] - FULL[u][0] - NV[u] - NG[u] for u in range(UNITS)]
-GADD = [2, 3] + [4 for i in range(INNER)] + [3, 3]
+NV = [14, 26] + [27] * INNER + [26, 16]
+NG = [8, 9] + [10] * INNER + [9, 6]
+GADD = [2, 3] + [4] * INNER + [3, 3]
 
 CHUNK_PAIRS = 4
 NCHUNKS = 4
-CSTART = [[k * (NV[u] // 2) // NCHUNKS for k in range(NCHUNKS + 1)] for u in range(UNITS)]
+CSTART = [[k * ((NV[u] + 1) // 2) // NCHUNKS for k in range(NCHUNKS + 1)] for u in range(UNITS)]
 STEPS = [18] + NV[1:]
 TSTART = [sum(STEPS[:u]) for u in range(UNITS + 1)]
 
@@ -96,11 +95,8 @@ def tile_sam_pb_t_kernel(tc, logits, x, w3c_words, w3c_scales, b3c, out):
         const = ctx.enter_context(tc.tile_pool(name="const", bufs=1))
         lg_pool = ctx.enter_context(tc.tile_pool(name="lg", bufs=2))
         stat_pool = ctx.enter_context(tc.tile_pool(name="stat", bufs=3))
-        wl_pool = ctx.enter_context(tc.tile_pool(name="wl", bufs=1))
-        wg_pool = ctx.enter_context(tc.tile_pool(name="wg", bufs=2))
-        ws_pool = ctx.enter_context(tc.tile_pool(name="ws", bufs=2))
+        wl_pool = ctx.enter_context(tc.tile_pool(name="wl", bufs=2))
         wst_pool = ctx.enter_context(tc.tile_pool(name="wst", bufs=2))
-        turn_pool = ctx.enter_context(tc.tile_pool(name="turn", bufs=1))
         prods_pool = ctx.enter_context(tc.tile_pool(name="prods", bufs=8))
         acc_pool = ctx.enter_context(tc.psum_pool(name="acc", bufs=1))
         wps_pool = ctx.enter_context(tc.psum_pool(name="wps", bufs=2))
@@ -112,11 +108,12 @@ def tile_sam_pb_t_kernel(tc, logits, x, w3c_words, w3c_scales, b3c, out):
         w_words = const.tile([P, 2 * COUT], U8, align_bytes=64, name="w_words")
         w_plane = const.tile([P, COUT], U8, align_bytes=64, name="w_plane")
         bias_bf = const.tile([P, SP], BF16, name="bias_bf")
+        bias_row = const.tile([P, HEADS, SP], BF16, name="bias_row")
         bias = const.tile([P, SP], F32, name="bias")
         x_codes = const.tile([P, B, NPAD], U32, align_bytes=64, name="x_codes")
         x_plane = const.tile([P, B, NPAD], U8, align_bytes=64, name="x_plane")
         neg_top = const.tile([P, HW], F32, name="neg_top")
-        wtv = const.tile([P, max(NV) // 2, P], F32, name="wtv")
+        wtv = const.tile([P, (max(NV) + 1) // 2, P], F32, name="wtv")
         xmap = const.tile([P, RING, WP, SP], F32, name="xmap")
 
         lgs = {}
@@ -157,19 +154,6 @@ def tile_sam_pb_t_kernel(tc, logits, x, w3c_words, w3c_scales, b3c, out):
             nc.vector.reciprocal(out=inv[:], in_=st["total"][:])
             st["inv"] = inv
 
-        def other_weights(u, st):
-            lg0 = FULL[u][0] + NV[u]
-            ls0 = lg0 + NG[u]
-            ws = ws_pool.tile([P, NU, NS[u] + (K if HALF[u] else 0)], F32, name="ws")
-            nc.scalar.copy(out=ws[:, :, 0 : NS[u]], in_=st["wl"][:, :, ls0 : ls0 + NS[u]])
-            if HALF[u]:
-                lh0 = K * HALF[u][0]
-                nc.scalar.copy(out=ws[:, :, NS[u] : NS[u] + K], in_=st["wl"][:, :, lh0 : lh0 + K])
-            wg = wg_pool.tile([P, NG[u], NU], F32, name="wg")
-            nc.scalar.copy(out=wg[:], in_=st["wl"][:, :, lg0:ls0].rearrange("p n l -> p l n"))
-            st["ws"] = ws
-            st["wg"] = wg
-
         def v_weights(u, st, k):
             p0, p1 = CSTART[u][k], CSTART[u][k + 1]
             hold = {}
@@ -203,7 +187,7 @@ def tile_sam_pb_t_kernel(tc, logits, x, w3c_words, w3c_scales, b3c, out):
 
         turned_of = {}
 
-        def mx_task(t, g, b0, own=False):
+        def mx_task(t, g, b0, turn_pool):
             cols = slice(TROWS * t * W, TROWS * t * W + P)
             hold = {}
 
@@ -212,10 +196,7 @@ def tile_sam_pb_t_kernel(tc, logits, x, w3c_words, w3c_scales, b3c, out):
                     turned = turn_pool.tile([P, CG, B, HEADS], F32, name="turned")
                     turned_of[(t, g)] = turned
                 for b in (b0, b0 + 1):
-                    if not own:
-                        x3t = stage.tile([P, HEADS * CG], F32, tag="stage", name="x3t")
-                    else:
-                        x3t = acc_pool.tile([P, HEADS * CG], F32, tag="sums%d" % b, name="x3t")
+                    x3t = acc_pool.tile([P, HEADS * CG], F32, tag="sums%d" % b, name="x3t")
                     nc.tensor.matmul_mx(
                         out=x3t[:],
                         lhsT=x_codes[:, b, cols].bitcast(FP8X4),
@@ -261,6 +242,53 @@ def tile_sam_pb_t_kernel(tc, logits, x, w3c_words, w3c_scales, b3c, out):
 
             return fill, drain
 
+        PARK = HW - TROWS * W
+
+        def map_task(t, b):
+            cols = slice(TROWS * t * W, TROWS * t * W + P)
+            hold = {}
+
+            def fill():
+                for g in range(GROUPS):
+                    x3t = stage.tile([P, HEADS, CG], F32, tag="stage", name="x3t")
+                    nc.tensor.matmul_mx(
+                        out=x3t[:].rearrange("p h c -> p (h c)"),
+                        lhsT=x_codes[:, b, cols].bitcast(FP8X4),
+                        lhsT_scale=x_plane[:, b, cols],
+                        rhs=w_words[:, 2 * g * 512 : 2 * (g + 1) * 512].bitcast(FP4X4),
+                        rhs_scale=w_plane[:, g * 512 : (g + 1) * 512],
+                        start=True,
+                        stop=True,
+                    )
+                    hold[g] = x3t
+
+            def drain():
+                xs = xs_pool.tile([P, HEADS, SP], F32, name="xs")
+                for g in range(GROUPS):
+                    part = slice(g * CG, (g + 1) * CG)
+                    nc.vector.tensor_tensor(out=xs[:, :, part], in0=hold[g][:], in1=bias_row[:, :, part], op=ALU.add)
+                rows_v = out[b].rearrange("(h q) i j -> q h (i j)", q=W)
+                for r in range(TROWS):
+                    nc.sync.dma_start(
+                        out=rows_v[:, :, PARK + r * W : PARK + (r + 1) * W], in_=xs[r * W : (r + 1) * W, :, :]
+                    )
+
+            return fill, drain
+
+        def load_map(t):
+            slot = TROWS * t % RING
+            for r in range(TROWS):
+                nc.sync.dma_start(
+                    out=xmap[:, slot + r, PAD : PAD + W, :], in_=out_v[:, :, PARK + r * W : PARK + (r + 1) * W]
+                )
+            for q in range(WP):
+                src = reflect(q - PAD, W)
+                if src != q - PAD:
+                    nc.sync.dma_start(
+                        out=xmap[:, slot : slot + TROWS, q, :],
+                        in_=out_v[:, src, PARK:HW].rearrange("p (r c) -> p r c", c=SP),
+                    )
+
         def pad_columns(t):
             slot = TROWS * t % RING
             rows = slice(slot + (PAD if t == 0 else 0), slot + TROWS)
@@ -281,7 +309,7 @@ def tile_sam_pb_t_kernel(tc, logits, x, w3c_words, w3c_scales, b3c, out):
         with tc.tile_pool(name="xin", bufs=3) as xin:
             with tc.tile_pool(name="xa", bufs=4) as xa, tc.tile_pool(name="xb", bufs=2) as xb, tc.tile_pool(
                 name="xg", bufs=2
-            ) as xg, tc.tile_pool(name="xt", bufs=1) as xt:
+            ) as xg, tc.tile_pool(name="xt", bufs=1) as xt, tc.tile_pool(name="turn", bufs=1) as turn_pool:
 
                 def load_x(pool, b, r0, r1):
                     raw = pool.tile([P, PACK, (r1 - r0) * W], BF16, tag="inp", name="raw")
@@ -343,6 +371,9 @@ def tile_sam_pb_t_kernel(tc, logits, x, w3c_words, w3c_scales, b3c, out):
                     plane_dst = plane_dst.rearrange("q (g h w) -> q g h w", g=GROUPS, h=HEADS)
                     for g in range(GROUPS):
                         nc.sync.dma_start(out=plane_dst[:, g], in_=scales_src[4 * quad : 4 * quad + 4, g])
+                nc.sync.dma_start(
+                    out=bias_row[:].rearrange("p h c -> p (h c)"), in_=b3c.partition_broadcast(P)
+                )
                 for b in range(B):
                     nc.sync.dma_start(
                         out=bias_bf[b * HEADS : (b + 1) * HEADS, :], in_=b3c.rearrange("(h c) -> h c", c=SP)
@@ -380,7 +411,7 @@ def tile_sam_pb_t_kernel(tc, logits, x, w3c_words, w3c_scales, b3c, out):
                     for g in range(GROUPS):
                         for task in between[2 * t + g]:
                             task()
-                        jobs = [mx_task(t, g, 0, True), mx_task(t, g, 2, True)]
+                        jobs = [mx_task(t, g, 0, turn_pool), mx_task(t, g, 2, turn_pool)]
                         for fill, drain in jobs:
                             fill()
                         for fill, drain in jobs:
@@ -394,7 +425,6 @@ def tile_sam_pb_t_kernel(tc, logits, x, w3c_words, w3c_scales, b3c, out):
                 quantise(2, 1)
                 quantise(3, 1)
                 softmax_recip(state[0])
-                other_weights(0, state[0])
                 for k in range(NCHUNKS):
                     for part in v_weights(0, state[0], k):
                         part()
@@ -414,6 +444,7 @@ def tile_sam_pb_t_kernel(tc, logits, x, w3c_words, w3c_scales, b3c, out):
             load_logits(1)
         prodv_pool = ctx.enter_context(tc.tile_pool(name="prodv", bufs=3))
         prodg_pool = ctx.enter_context(tc.tile_pool(name="prodg", bufs=4))
+        xs_pool = ctx.enter_context(tc.tile_pool(name="xs", bufs=2))
         sums_pool = ctx.enter_context(tc.tile_pool(name="sums", bufs=1))
         res_pool = ctx.enter_context(tc.tile_pool(name="res", bufs=1))
 
@@ -441,15 +472,15 @@ def tile_sam_pb_t_kernel(tc, logits, x, w3c_words, w3c_scales, b3c, out):
         S_ITEMS = []
         for u in range(UNITS):
             ls0 = FULL[u][0] + NV[u] + NG[u]
-            items = [(i, ls0 + i, n) for i in range(NS[u]) for n in range(NU)]
+            items = [(l, n) for l in range(ls0, FULL[u][1]) for n in range(NU)]
             if HALF[u]:
                 dy, r = HALF[u]
-                items = [(NS[u] + dx, K * dy + dx, n) for dx in range(K) for n in range(r * W, (r + 1) * W)] + items
+                items = [(K * dy + dx, n) for dx in range(K) for n in range(r * W, (r + 1) * W)] + items
             S_ITEMS.append(items)
         NADDS = {}
         for u in range(UNITS):
             for bank in range(BANKS):
-                pieces = len([1 for i, l, n in S_ITEMS[u] if n == bank * NPOS])
+                pieces = len([1 for l, n in S_ITEMS[u] if n == bank * NPOS])
                 NADDS[(u, bank)] = NV[u] + NG[u] - GADD[u] + pieces
 
         def add_bank(u, bank, flat):
@@ -475,7 +506,8 @@ def tile_sam_pb_t_kernel(tc, logits, x, w3c_words, w3c_scales, b3c, out):
 
         def g_multiply(u, i):
             pg = prodg_pool.tile([P, NU, SP], F32, name="pg")
-            multiply(nc.gpsimd, u, FULL[u][0] + NV[u] + i, pg, state[u]["wg"][:, i, :])
+            l = FULL[u][0] + NV[u] + i
+            multiply(nc.gpsimd, u, l, pg, state[u]["wl"][:, :, l])
             gprods[(u, i)] = pg
 
         def g_add(u, i):
@@ -486,7 +518,7 @@ def tile_sam_pb_t_kernel(tc, logits, x, w3c_words, w3c_scales, b3c, out):
         sprods = {}
 
         def s_multiply(u, e):
-            i, l, n = S_ITEMS[u][e]
+            l, n = S_ITEMS[u][e]
             piece, k = divmod(e, NPOS)
             if k == 0:
                 ps = prods_pool.tile([P, NPOS, SP], F32, name="ps")
@@ -497,11 +529,11 @@ def tile_sam_pb_t_kernel(tc, logits, x, w3c_words, w3c_scales, b3c, out):
                 out=sprods[(u, piece)][:, k, :],
                 in_=xmap[:, (UROWS * u + dy + r) % RING, q + dx, :],
                 func=ACT.Copy,
-                scale=state[u]["ws"][:, n, i : i + 1],
+                scale=state[u]["wl"][:, n, l : l + 1],
             )
 
         def add_piece(u, i):
-            bank = S_ITEMS[u][i * NPOS][2] // NPOS
+            bank = S_ITEMS[u][i * NPOS][1] // NPOS
             add_bank(u, bank, sprods[(u, i)][:].rearrange("p n c -> p (n c)"))
 
         sums_sb_of = {}
@@ -588,20 +620,19 @@ def tile_sam_pb_t_kernel(tc, logits, x, w3c_words, w3c_scales, b3c, out):
                     stage_tasks(t0 + BACK0 + bank, back_task(u - 1, bank), 2)
             k, odd = divmod(u, 2)
             t = k + 2
-            if not odd:
-                if t < TILES:
-                    first = 5 if u else 0
-                    for bank in range(4):
-                        stage_tasks(t0 + first + bank, turn_task(t, 0, bank), 2)
-                        stage_tasks(t0 + first + 9 + bank, turn_task(t, 1, bank), 2)
-                    stage_tasks(t0 + first + 5, mx_task(t, 1, 0), 1)
-                    stage_tasks(t0 + first + 7, mx_task(t, 1, 2), 1)
-                    put(small_at, t0 + first + 15, lambda t=t: pad_columns(t))
-            elif t + 1 < TILES:
-                stage_tasks(t0 + 10, mx_task(t + 1, 0, 0), 1)
-                stage_tasks(t0 + 12, mx_task(t + 1, 0, 2), 1)
+            if u == 0:
+                for b in range(B):
+                    stage_tasks(t0 + 2 * b, map_task(t, b), 2)
+                put(small_at, t0 + 11, lambda t=t: load_map(t))
+            elif odd and t + 1 < TILES:
+                for b in (0, 1):
+                    stage_tasks(t0 + 8 + 2 * b, map_task(t + 1, b), 2)
+            elif not odd and t < TILES:
+                for b in (2, 3):
+                    stage_tasks(t0 + 4 + 2 * b, map_task(t, b), 2)
+                put(small_at, t0 + 14, lambda t=t: load_map(t))
             for c in range(NCHUNKS):
-                after = t0 + (2 * CSTART[u][c + 1] - 1) * STEPS[u] // NV[u]
+                after = t0 + min(2 * CSTART[u][c + 1], NV[u]) * STEPS[u] // NV[u] - 1
                 if c + 2 < NCHUNKS:
                     put(fill_at, after, lambda u=u, c=c: take_wps(u, c + 2))
                 elif u + 1 < UNITS:
@@ -613,7 +644,6 @@ def tile_sam_pb_t_kernel(tc, logits, x, w3c_words, w3c_scales, b3c, out):
                 spread(t0, 0, nv - 10, NU, lambda n0, n1, u=u, st=st: softmax_exp(u + 1, st, n0, n1))
                 wv = last - 6 if u else last - 4
                 put(g_at, wv - 3, lambda u=u, st=st: fold(nc.gpsimd, u + 1, st))
-                put(small_at, wv - 2, lambda u=u, st=st: other_weights(u + 1, st))
                 put(small_at, last - 2, lambda st=st: softmax_recip(st))
                 for c in range(NCHUNKS):
                     gather, fill, drain = v_weights(u + 1, st, c)
@@ -626,9 +656,6 @@ def tile_sam_pb_t_kernel(tc, logits, x, w3c_words, w3c_scales, b3c, out):
             s_multiply(0, e)
             if e % NPOS == NPOS - 1:
                 add_piece(0, e // NPOS)
-        for b0 in (0, 2):
-            for part in mx_task(2, 0, b0):
-                part()
         for u in range(UNITS):
             chunk_of = [k for k in range(NCHUNKS) for i in range(CSTART[u][k], CSTART[u][k + 1]) for two in range(2)]
             step_of = [i * STEPS[u] // NV[u] for i in range(NV[u])]

@@ -70,7 +70,7 @@ def edge_rows():
 FOLDS, FULL, HALF = edge_rows()
 
 INNER = UNITS - 4
-NV = [14, 26] + [27] * INNER + [26, 16]
+NV = [12, 25] + [26 + i % 2 for i in range(INNER)] + [25, 16]
 NG = [8, 9] + [10] * INNER + [9, 6]
 GADD = [2, 3] + [4] * INNER + [3, 3]
 
@@ -80,7 +80,7 @@ CSTART = [[k * ((NV[u] + 1) // 2) // NCHUNKS for k in range(NCHUNKS + 1)] for u 
 STEPS = [18] + NV[1:]
 TSTART = [sum(STEPS[:u]) for u in range(UNITS + 1)]
 
-EARLY = 6 * NU
+EARLY = 9 * NU
 
 FLOPS = 2 * B * COUT * HW * CIN + 2 * B * COUT * HW * KK
 
@@ -161,7 +161,11 @@ def tile_sam_pb_t_kernel(tc, logits, x, w3c_words, w3c_scales, b3c, out):
             def gather():
                 wst = wst_pool.tile([P, 2 * CHUNK_PAIRS, NU], F32, name="wst")
                 l0, l1 = FULL[u][0] + 2 * p0, FULL[u][0] + 2 * p1
-                nc.scalar.copy(out=wst[:, 0 : l1 - l0, :], in_=st["wl"][:, :, l0:l1].rearrange("p n l -> p l n"))
+                for a in range(l0, l1, 4):
+                    z = min(a + 4, l1)
+                    nc.scalar.copy(
+                        out=wst[:, a - l0 : z - l0, :].rearrange("p l n -> p n l"), in_=st["wl"][:, :, a:z]
+                    )
                 hold["wst"] = wst
 
             def fill():
@@ -357,9 +361,6 @@ def tile_sam_pb_t_kernel(tc, logits, x, w3c_words, w3c_scales, b3c, out):
 
                 parts = [(0, 5, 0, 8, (256,)), (5, H, 8, XROWS, (512, 256, 128))]
                 raws = {(b, 0): load_x(xa, b, parts[0][0], parts[0][1]) for b in range(B)}
-                load_logits(0)
-                for b in range(2):
-                    raws[(b, 1)] = load_x(xb, b, parts[1][0], parts[1][1])
                 nc.vector.memset(w_plane[:].bitcast(I32), 0)
                 words_src = w3c_words[0].bitcast(I32).rearrange("p (h g w) -> p g h w", g=GROUPS, h=HEADS)
                 words_dst = w_words[:].bitcast(I32).rearrange("p (g h w) -> p g h w", g=GROUPS, h=HEADS)
@@ -371,13 +372,13 @@ def tile_sam_pb_t_kernel(tc, logits, x, w3c_words, w3c_scales, b3c, out):
                     plane_dst = plane_dst.rearrange("q (g h w) -> q g h w", g=GROUPS, h=HEADS)
                     for g in range(GROUPS):
                         nc.sync.dma_start(out=plane_dst[:, g], in_=scales_src[4 * quad : 4 * quad + 4, g])
-                nc.sync.dma_start(
-                    out=bias_row[:].rearrange("p h c -> p (h c)"), in_=b3c.partition_broadcast(P)
-                )
                 for b in range(B):
                     nc.sync.dma_start(
                         out=bias_bf[b * HEADS : (b + 1) * HEADS, :], in_=b3c.rearrange("(h c) -> h c", c=SP)
                     )
+                load_logits(0)
+                for b in range(2):
+                    raws[(b, 1)] = load_x(xb, b, parts[1][0], parts[1][1])
 
                 grouped = {}
 
@@ -399,14 +400,13 @@ def tile_sam_pb_t_kernel(tc, logits, x, w3c_words, w3c_scales, b3c, out):
                     group(b, 0)
                     quantise(b - 1, 0)
                 quantise(B - 1, 0)
-                first_top(0)
-                softmax_exp(0, state[0], 0, NU)
-                group(0, 1)
-                group(1, 1)
-                quantise(0, 1)
                 nc.vector.tensor_copy(out=bias[:], in_=bias_bf[:])
-                fold(nc.vector, 0, state[0])
-                between = [[], [lambda: group(2, 1)], [lambda: quantise(1, 1)], [lambda: group(3, 1)]]
+                between = [
+                    [],
+                    [lambda: first_top(0)],
+                    [lambda: softmax_exp(0, state[0], 0, 20), lambda: group(0, 1)],
+                    [lambda: softmax_exp(0, state[0], 20, 40), lambda: group(1, 1)],
+                ]
                 for t in range(2):
                     for g in range(GROUPS):
                         for task in between[2 * t + g]:
@@ -420,8 +420,14 @@ def tile_sam_pb_t_kernel(tc, logits, x, w3c_words, w3c_scales, b3c, out):
                             fill, drain = turn_task(t, g, bank)
                             fill()
                             drain()
+                softmax_exp(0, state[0], 40, NU)
                 pad_columns(0)
                 pad_columns(1)
+                fold(nc.vector, 0, state[0])
+                quantise(0, 1)
+                group(2, 1)
+                quantise(1, 1)
+                group(3, 1)
                 quantise(2, 1)
                 quantise(3, 1)
                 softmax_recip(state[0])
@@ -442,6 +448,7 @@ def tile_sam_pb_t_kernel(tc, logits, x, w3c_words, w3c_scales, b3c, out):
             nc.vector.tensor_tensor(out=best[:, 0, :], in0=best[:, 0, :], in1=best[:, 1, :], op=ALU.max)
             nc.vector.tensor_scalar_mul(out=neg_top[:, NU:HW], in0=best[:, 0, :], scalar1=-1.0)
             load_logits(1)
+            nc.sync.dma_start(out=bias_row[:].rearrange("p h c -> p (h c)"), in_=b3c.partition_broadcast(P))
         prodv_pool = ctx.enter_context(tc.tile_pool(name="prodv", bufs=3))
         prodg_pool = ctx.enter_context(tc.tile_pool(name="prodg", bufs=4))
         xs_pool = ctx.enter_context(tc.tile_pool(name="xs", bufs=2))

@@ -70,9 +70,9 @@ def edge_rows():
 FOLDS, FULL, HALF = edge_rows()
 
 INNER = UNITS - 4
-NV = [12, 25] + [26 + i % 2 for i in range(INNER)] + [25, 16]
-NG = [8, 9] + [10] * INNER + [9, 6]
-GADD = [2, 3] + [4] * INNER + [3, 3]
+NV = [12, 25] + [26] * INNER + [25, 16]
+NG = [8, 9] + [11 - i % 2 for i in range(INNER)] + [9, 6]
+GADD = [2, 3] + [4 - i % 2 for i in range(INNER)] + [3, 3]
 
 CHUNK_PAIRS = 4
 NCHUNKS = 4

@@ -76,6 +76,7 @@ GADD = [2, 3] + [4 - i % 2 for i in range(INNER)] + [3, 3]
 
 CHUNK_PAIRS = 4
 NCHUNKS = 4
+SCALAR_CHUNKS = 2
 CSTART = [[k * ((NV[u] + 1) // 2) // NCHUNKS for k in range(NCHUNKS + 1)] for u in range(UNITS)]
 STEPS = [18] + NV[1:]
 TSTART = [sum(STEPS[:u]) for u in range(UNITS + 1)]
@@ -93,11 +94,11 @@ def tile_sam_pb_t_kernel(tc, logits, x, w3c_words, w3c_scales, b3c, out):
     with ExitStack() as ctx:
         ctx.enter_context(tc.manual_schedule())
         const = ctx.enter_context(tc.tile_pool(name="const", bufs=1))
-        lg_pool = ctx.enter_context(tc.tile_pool(name="lg", bufs=2))
+        lg_pool = ctx.enter_context(tc.tile_pool(name="lg", bufs=1))
         stat_pool = ctx.enter_context(tc.tile_pool(name="stat", bufs=3))
         wl_pool = ctx.enter_context(tc.tile_pool(name="wl", bufs=2))
         wst_pool = ctx.enter_context(tc.tile_pool(name="wst", bufs=2))
-        prods_pool = ctx.enter_context(tc.tile_pool(name="prods", bufs=8))
+        prods_pool = ctx.enter_context(tc.tile_pool(name="prods", bufs=11))
         acc_pool = ctx.enter_context(tc.psum_pool(name="acc", bufs=1))
         wps_pool = ctx.enter_context(tc.psum_pool(name="wps", bufs=2))
         stage = ctx.enter_context(tc.psum_pool(name="stage", bufs=2))
@@ -177,7 +178,8 @@ def tile_sam_pb_t_kernel(tc, logits, x, w3c_words, w3c_scales, b3c, out):
                 hold["ps"] = ps
 
             def drain():
-                nc.scalar.copy(out=wtv[:, p0:p1, :], in_=hold["ps"][:, 0 : p1 - p0, :])
+                copy = nc.scalar.copy if k < SCALAR_CHUNKS else nc.vector.tensor_copy
+                copy(out=wtv[:, p0:p1, :], in_=hold["ps"][:, 0 : p1 - p0, :])
 
             return gather, fill, drain
 
@@ -645,7 +647,7 @@ def tile_sam_pb_t_kernel(tc, logits, x, w3c_words, w3c_scales, b3c, out):
                 elif u + 1 < UNITS:
                     put(fill_at, max(after, last - 3 if u else last - 2), lambda u=u, c=c: take_wps(u + 1, c + 2 - NCHUNKS))
             if u + 2 < UNITS:
-                put(small_at, t0 + 1, lambda u=u: load_logits(u + 2))
+                put(small_at, t0 + nv - 9, lambda u=u: load_logits(u + 2))
             if u + 1 < UNITS:
                 st = state[u + 1]
                 spread(t0, 0, nv - 10, NU, lambda n0, n1, u=u, st=st: softmax_exp(u + 1, st, n0, n1))
@@ -655,7 +657,7 @@ def tile_sam_pb_t_kernel(tc, logits, x, w3c_words, w3c_scales, b3c, out):
                 for c in range(NCHUNKS):
                     gather, fill, drain = v_weights(u + 1, st, c)
                     put(small_at, wv - 1 + c, gather)
-                    stage_tasks(wv + c, (fill, drain), 1)
+                    stage_tasks(wv + c, (fill, drain), 1 if c < SCALAR_CHUNKS else 2)
 
         take_wps(0, 0)
         take_wps(0, 1)

from contextlib import ExitStack

import concourse.mybir as mybir
from concourse.masks import make_identity

F32 = mybir.dt.float32
BF16 = mybir.dt.bfloat16
U8 = mybir.dt.uint8
U32 = mybir.dt.uint32
I32 = mybir.dt.int32
FP8X4 = mybir.dt.float8_e4m3fn_x4
FP4X4 = mybir.dt.float4_e2m1fn_x4
ALU = mybir.AluOpType
ACT = mybir.ActivationFunctionType

P = 128
B, CIN, H, W, COUT = 4, 512, 32, 32, 1024
HEADS, SP = 32, 32
K = 7
KK = K * K
PAD = K // 2
HW = H * W
PACK = 4
WP = W + 2 * PAD
XROWS = 36
NPAD = XROWS * W

BAND = 4
NB = BAND * W
UROWS = 2
NU = UROWS * W
UNITS = H // UROWS
RING = 12
TROWS = 4
TILES = XROWS // TROWS
CG = 16
GROUPS = SP // CG
PER_BANK = 4
BLOCKS = NU * SP // P
BANKS = BLOCKS // PER_BANK
NPOS = NU // BANKS
LP = 52


def reflect(u, size):
    if u < 0:
        return -u
    if u > size - 1:
        return 2 * (size - 1) - u
    return u


def edge_rows():
    folds, full, half = [], [], []
    for u in range(UNITS):
        keeps, fold = [], []
        for r in range(UROWS):
            i = UROWS * u + r
            stays = [reflect(i + dy - PAD, H) - i + PAD for dy in range(K)]
            fold.extend([(r, stays[dy], dy) for dy in range(K) if stays[dy] != dy])
            keeps.append([dy for dy in range(K) if stays[dy] == dy])
        both = [dy for dy in keeps[0] if dy in keeps[1]]
        one = [(dy, r) for r in range(UROWS) for dy in keeps[r] if dy not in both]
        folds.append(fold)
        full.append((K * both[0], K * (both[-1] + 1)))
        half.append(one[0] if one else None)
    return folds, full, half


FOLDS, FULL, HALF = edge_rows()

INNER = UNITS - 4
NV = [12, 25] + [26] * INNER + [25, 16]
NG = [8, 9] + [11 - i % 2 for i in range(INNER)] + [9, 6]
GADD = [2, 3] + [4 - i % 2 for i in range(INNER)] + [3, 3]

CHUNK_PAIRS = 4
NCHUNKS = 4
SCALAR_CHUNKS = 2
CSTART = [[k * ((NV[u] + 1) // 2) // NCHUNKS for k in range(NCHUNKS + 1)] for u in range(UNITS)]
STEPS = [18] + NV[1:]
TSTART = [sum(STEPS[:u]) for u in range(UNITS + 1)]

EARLY = 9 * NU

FLOPS = 2 * B * COUT * HW * CIN + 2 * B * COUT * HW * KK


def tile_sam_pb_t_kernel(tc, logits, x, w3c_words, w3c_scales, b3c, out):
    nc = tc.nc
    logits_v = logits.rearrange("b h l n -> (b h) l n")
    out_v = out.rearrange("b (h c) i j -> (b h) c (i j)", c=SP)

    with ExitStack() as ctx:
        ctx.enter_context(tc.manual_schedule())
        const = ctx.enter_context(tc.tile_pool(name="const", bufs=1))
        lg_pool = ctx.enter_context(tc.tile_pool(name="lg", bufs=1))
        stat_pool = ctx.enter_context(tc.tile_pool(name="stat", bufs=3))
        wl_pool = ctx.enter_context(tc.tile_pool(name="wl", bufs=2))
        wst_pool = ctx.enter_context(tc.tile_pool(name="wst", bufs=2))
        prods_pool = ctx.enter_context(tc.tile_pool(name="prods", bufs=11))
        acc_pool = ctx.enter_context(tc.psum_pool(name="acc", bufs=1))
        wps_pool = ctx.enter_context(tc.psum_pool(name="wps", bufs=2))
        stage = ctx.enter_context(tc.psum_pool(name="stage", bufs=2))

        ident = const.tile([P, P], F32, name="ident")
        make_identity(nc, ident[:])

        w_words = const.tile([P, 2 * COUT], U8, align_bytes=64, name="w_words")
        w_plane = const.tile([P, COUT], U8, align_bytes=64, name="w_plane")
        bias_bf = const.tile([P, SP], BF16, name="bias_bf")
        bias_row = const.tile([P, HEADS, SP], BF16, name="bias_row")
        bias = const.tile([P, SP], F32, name="bias")
        x_codes = const.tile([P, B, NPAD], U32, align_bytes=64, name="x_codes")
        x_plane = const.tile([P, B, NPAD], U8, align_bytes=64, name="x_plane")
        neg_top = const.tile([P, HW], F32, name="neg_top")
        wtv = const.tile([P, (max(NV) + 1) // 2, P], F32, name="wtv")
        xmap = const.tile([P, RING, WP, SP], F32, name="xmap")

        lgs = {}

        def load_logits(u):
            lg = lg_pool.tile([P, KK, NU], BF16, name="lg")
            nc.sync.dma_start(out=lg[:], in_=logits_v[:, :, u * NU : (u + 1) * NU])
            lgs[u] = lg

        def softmax_exp(u, st, n0, n1):
            if n0 == 0:
                wl = wl_pool.tile([P, NU, LP], F32, name="wl")
                total = stat_pool.tile([P, NU], F32, name="total")
                st["wl"] = wl
                st["total"] = total
            for n in range(n0, n1):
                nc.scalar.activation(
                    out=st["wl"][:, n, 0:KK],
                    in_=lgs[u][:, :, n],
                    func=ACT.Exp,
                    bias=neg_top[:, u * NU + n : u * NU + n + 1],
                    scale=1.0,
                    accum_out=st["total"][:, n : n + 1],
                )

        def fold(engine, u, st):
            for r, stays, reflects in FOLDS[u]:
                rows = slice(r * W, (r + 1) * W)
                engine.tensor_tensor(
                    out=st["wl"][:, rows, K * stays : K * (stays + 1)],
                    in0=st["wl"][:, rows, K * stays : K * (stays + 1)],
                    in1=st["wl"][:, rows, K * reflects : K * (reflects + 1)],
                    op=ALU.add,
                )

        def softmax_recip(st):
            inv = stat_pool.tile([P, NU], F32, name="inv")
            nc.vector.reciprocal(out=inv[:], in_=st["total"][:])
            st["inv"] = inv

        def v_weights(u, st, k):
            p0, p1 = CSTART[u][k], CSTART[u][k + 1]
            hold = {}

            def gather():
                wst = wst_pool.tile([P, 2 * CHUNK_PAIRS, NU], F32, name="wst")
                l0, l1 = FULL[u][0] + 2 * p0, FULL[u][0] + 2 * p1
                for a in range(l0, l1, 4):
                    z = min(a + 4, l1)
                    nc.scalar.copy(
                        out=wst[:, a - l0 : z - l0, :].rearrange("p l n -> p n l"), in_=st["wl"][:, :, a:z]
                    )
                hold["wst"] = wst

            def fill():
                ps = stage.tile([P, PER_BANK, P], F32, tag="stage", name="ps")
                for j in range(p1 - p0):
                    nc.tensor.transpose(
                        ps[:, j, :], hold["wst"][:, 2 * j : 2 * j + 2, :].rearrange("p l n -> p (l n)"), ident[:]
                    )
                hold["ps"] = ps

            def drain():
                copy = nc.scalar.copy if k < SCALAR_CHUNKS else nc.vector.tensor_copy
                copy(out=wtv[:, p0:p1, :], in_=hold["ps"][:, 0 : p1 - p0, :])

            return gather, fill, drain

        def load_wps(u, k):
            wps = wps_pool.tile([P, 2 * CHUNK_PAIRS, NU], F32, name="wps")
            for j in range(CSTART[u][k + 1] - CSTART[u][k]):
                nc.tensor.transpose(
                    wps[:, 2 * j : 2 * j + 2, :].rearrange("p l n -> p (l n)"), wtv[:, CSTART[u][k] + j, :], ident[:]
                )
            return wps

        turned_of = {}

        def mx_task(t, g, b0, turn_pool):
            cols = slice(TROWS * t * W, TROWS * t * W + P)
            hold = {}

            def fill():
                if b0 == 0:
                    turned = turn_pool.tile([P, CG, B, HEADS], F32, name="turned")
                    turned_of[(t, g)] = turned
                for b in (b0, b0 + 1):
                    x3t = acc_pool.tile([P, HEADS * CG], F32, tag="sums%d" % b, name="x3t")
                    nc.tensor.matmul_mx(
                        out=x3t[:],
                        lhsT=x_codes[:, b, cols].bitcast(FP8X4),
                        lhsT_scale=x_plane[:, b, cols],
                        rhs=w_words[:, 2 * g * 512 : 2 * (g + 1) * 512].bitcast(FP4X4),
                        rhs_scale=w_plane[:, g * 512 : (g + 1) * 512],
                        start=True,
                        stop=True,
                    )
                    hold[b] = x3t

            def drain():
                for b in (b0, b0 + 1):
                    nc.scalar.copy(
                        out=turned_of[(t, g)][:, :, b, :], in_=hold[b][:].rearrange("p (h c) -> p c h", c=CG)
                    )

            return fill, drain

        def turn_task(t, g, bank):
            r0 = PAD if t == 0 else 0
            slot = TROWS * t % RING + r0
            c0 = g * CG + bank * PER_BANK
            hold = {}

            def fill():
                x3 = stage.tile([P, PER_BANK, TROWS, W], F32, tag="stage", name="x3")
                for j in range(PER_BANK):
                    nc.tensor.transpose(
                        x3[:, j].rearrange("p r q -> p (r q)"),
                        turned_of[(t, g)][:, bank * PER_BANK + j].rearrange("p b h -> p (b h)"),
                        ident[:],
                    )
                hold["x3"] = x3

            def drain():
                nc.vector.tensor_tensor(
                    out=xmap[:, slot : slot + TROWS - r0, PAD : PAD + W, c0 : c0 + PER_BANK],
                    in0=hold["x3"][:, :, r0:TROWS, :].rearrange("p j r q -> p r q j"),
                    in1=bias[:, c0 : c0 + PER_BANK].unsqueeze(1).unsqueeze(1).to_broadcast([P, TROWS - r0, W, PER_BANK]),
                    op=ALU.add,
                )

            return fill, drain

        PARK = HW - TROWS * W

        def map_task(t, b):
            cols = slice(TROWS * t * W, TROWS * t * W + P)
            hold = {}

            def fill():
                for g in range(GROUPS):
                    x3t = stage.tile([P, HEADS, CG], F32, tag="stage", name="x3t")
                    nc.tensor.matmul_mx(
                        out=x3t[:].rearrange("p h c -> p (h c)"),
                        lhsT=x_codes[:, b, cols].bitcast(FP8X4),
                        lhsT_scale=x_plane[:, b, cols],
                        rhs=w_words[:, 2 * g * 512 : 2 * (g + 1) * 512].bitcast(FP4X4),
                        rhs_scale=w_plane[:, g * 512 : (g + 1) * 512],
                        start=True,
                        stop=True,
                    )
                    hold[g] = x3t

            def drain():
                xs = xs_pool.tile([P, HEADS, SP], F32, name="xs")
                for g in range(GROUPS):
                    part = slice(g * CG, (g + 1) * CG)
                    nc.vector.tensor_tensor(out=xs[:, :, part], in0=hold[g][:], in1=bias_row[:, :, part], op=ALU.add)
                rows_v = out[b].rearrange("(h q) i j -> q h (i j)", q=W)
                for r in range(TROWS):
                    nc.sync.dma_start(
                        out=rows_v[:, :, PARK + r * W : PARK + (r + 1) * W], in_=xs[r * W : (r + 1) * W, :, :]
                    )

            return fill, drain

        def load_map(t):
            slot = TROWS * t % RING
            for r in range(TROWS):
                nc.sync.dma_start(
                    out=xmap[:, slot + r, PAD : PAD + W, :], in_=out_v[:, :, PARK + r * W : PARK + (r + 1) * W]
                )
            for q in range(WP):
                src = reflect(q - PAD, W)
                if src != q - PAD:
                    nc.sync.dma_start(
                        out=xmap[:, slot : slot + TROWS, q, :],
                        in_=out_v[:, src, PARK:HW].rearrange("p (r c) -> p r c", c=SP),
                    )

        def pad_columns(t):
            slot = TROWS * t % RING
            rows = slice(slot + (PAD if t == 0 else 0), slot + TROWS)
            for q in range(WP):
                src = reflect(q - PAD, W) + PAD
                if src != q:
                    nc.scalar.copy(out=xmap[:, rows, q, :], in_=xmap[:, rows, src, :])

        state = {u: {} for u in range(UNITS)}
        rest = HW - NU

        def load_rows(pool, dy):
            rows = pool.tile([P, K, rest], BF16, tag="inp", name="rows")
            nc.sync.dma_start(out=rows[:], in_=logits_v[:, K * dy : K * (dy + 1), NU:HW])
            return rows

        rows_of = {}
        with tc.tile_pool(name="xin", bufs=3) as xin:
            with tc.tile_pool(name="xa", bufs=4) as xa, tc.tile_pool(name="xb", bufs=2) as xb, tc.tile_pool(
                name="xg", bufs=2
            ) as xg, tc.tile_pool(name="xt", bufs=1) as xt, tc.tile_pool(name="turn", bufs=1) as turn_pool:

                def load_x(pool, b, r0, r1):
                    raw = pool.tile([P, PACK, (r1 - r0) * W], BF16, tag="inp", name="raw")
                    nc.sync.dma_start(out=raw[:], in_=x[b].rearrange("(p t) i j -> p t (i j)", t=PACK)[:, :, r0 * W : r1 * W])
                    return raw

                def group_x(raw, r0, r1, p0, p1):
                    grouped = xg.tile([P, (p1 - p0) * W, PACK], BF16, align_bytes=64, name="grouped")
                    first, last = max(p0, PAD + r0), min(p1, PAD + r1)
                    nc.vector.tensor_copy(
                        out=grouped[:, (first - p0) * W : (last - p0) * W, :].rearrange("p (c i) t -> p c t i", i=4),
                        in_=raw[:, :, (first - PAD - r0) * W : (last - PAD - r0) * W].rearrange("p t (c i) -> p c t i", i=4),
                    )
                    for f0, f1 in ((p0, first), (last, p1)):
                        if f0 < f1:
                            nc.vector.tensor_copy(
                                out=grouped[:, (f0 - p0) * W : (f1 - p0) * W, :],
                                in_=raw[:, :, 0 : (f1 - f0) * W].rearrange("p t n -> p n t"),
                            )
                    return grouped

                def quantise_x(b, grouped, p0, widths):
                    flat = grouped[:].rearrange("p n t -> p (n t)")
                    first = 0
                    for width in widths:
                        n0 = p0 * W + first
                        nc.vector.quantize_mx(
                            out=x_codes[:, b, n0 : n0 + width].bitcast(FP8X4),
                            scales=x_plane[:, b, n0 : n0 + width],
                            in_=flat[:, PACK * first : PACK * (first + width)],
                        )
                        first += width

                def first_top(u):
                    lg = lgs[u]
                    top = xt.tile([P, KK // 2, NU], BF16, name="top")
                    nc.vector.tensor_tensor(out=top[:], in0=lg[:, 0:24, :], in1=lg[:, 24:48, :], op=ALU.max)
                    for half in (12, 6, 3):
                        nc.vector.tensor_tensor(
                            out=top[:, 0:half, :], in0=top[:, 0:half, :], in1=top[:, half : 2 * half, :], op=ALU.max
                        )
                    for other in (top[:, 1, :], top[:, 2, :], lg[:, KK - 1, :]):
                        nc.vector.tensor_tensor(out=top[:, 0, :], in0=top[:, 0, :], in1=other, op=ALU.max)
                    nc.vector.tensor_scalar_mul(out=neg_top[:, u * NU : (u + 1) * NU], in0=top[:, 0, :], scalar1=-1.0)

                parts = [(0, 5, 0, 8, (256,)), (5, H, 8, XROWS, (512, 256, 128))]
                raws = {(b, 0): load_x(xa, b, parts[0][0], parts[0][1]) for b in range(B)}
                nc.vector.memset(w_plane[:].bitcast(I32), 0)
                words_src = w3c_words[0].bitcast(I32).rearrange("p (h g w) -> p g h w", g=GROUPS, h=HEADS)
                words_dst = w_words[:].bitcast(I32).rearrange("p (g h w) -> p g h w", g=GROUPS, h=HEADS)
                scales_src = w3c_scales[0].bitcast(I32).rearrange("q (h g w) -> q g h w", g=GROUPS, h=HEADS)
                for g in range(GROUPS):
                    nc.sync.dma_start(out=words_dst[:, g], in_=words_src[:, g])
                for quad in range(4):
                    plane_dst = w_plane[32 * quad : 32 * quad + 4, :].bitcast(I32)
                    plane_dst = plane_dst.rearrange("q (g h w) -> q g h w", g=GROUPS, h=HEADS)
                    for g in range(GROUPS):
                        nc.sync.dma_start(out=plane_dst[:, g], in_=scales_src[4 * quad : 4 * quad + 4, g])
                for b in range(B):
                    nc.sync.dma_start(
                        out=bias_bf[b * HEADS : (b + 1) * HEADS, :], in_=b3c.rearrange("(h c) -> h c", c=SP)
                    )
                load_logits(0)
                for b in range(2):
                    raws[(b, 1)] = load_x(xb, b, parts[1][0], parts[1][1])

                grouped = {}

                def group(b, part):
                    r0, r1, p0, p1, widths = parts[part]
                    grouped[(b, part)] = group_x(raws[(b, part)], r0, r1, p0, p1)
                    if part == 1:
                        if b + 2 < B:
                            raws[(b + 2, 1)] = load_x(xb, b + 2, r0, r1)
                        if b < 3:
                            rows_of[b] = load_rows(xin, b)

                def quantise(b, part):
                    r0, r1, p0, p1, widths = parts[part]
                    quantise_x(b, grouped[(b, part)], p0, widths)

                group(0, 0)
                for b in range(1, B):
                    group(b, 0)
                    quantise(b - 1, 0)
                quantise(B - 1, 0)
                nc.vector.tensor_copy(out=bias[:], in_=bias_bf[:])
                between = [
                    [],
                    [lambda: first_top(0)],
                    [lambda: softmax_exp(0, state[0], 0, 20), lambda: group(0, 1)],
                    [lambda: softmax_exp(0, state[0], 20, 40), lambda: group(1, 1)],
                ]
                for t in range(2):
                    for g in range(GROUPS):
                        for task in between[2 * t + g]:
                            task()
                        jobs = [mx_task(t, g, 0, turn_pool), mx_task(t, g, 2, turn_pool)]
                        for fill, drain in jobs:
                            fill()
                        for fill, drain in jobs:
                            drain()
                        for bank in range(CG // PER_BANK):
                            fill, drain = turn_task(t, g, bank)
                            fill()
                            drain()
                softmax_exp(0, state[0], 40, NU)
                pad_columns(0)
                pad_columns(1)
                fold(nc.vector, 0, state[0])
                quantise(0, 1)
                group(2, 1)
                quantise(1, 1)
                group(3, 1)
                quantise(2, 1)
                quantise(3, 1)
                softmax_recip(state[0])
                for k in range(NCHUNKS):
                    for part in v_weights(0, state[0], k):
                        part()

            with tc.tile_pool(name="more", bufs=2) as more:
                for dy in (3, 4):
                    rows_of[dy] = load_rows(more, dy)
                for dy in range(1, K):
                    best = rows_of[dy]
                    nc.vector.tensor_tensor(out=best[:], in0=rows_of[dy - 1][:], in1=best[:], op=ALU.max)
                    if dy + 4 < K:
                        rows_of[dy + 4] = load_rows(xin, dy + 4)
            nc.vector.tensor_tensor(out=best[:, 0:3, :], in0=best[:, 0:3, :], in1=best[:, 3:6, :], op=ALU.max)
            nc.vector.tensor_tensor(out=best[:, 0:2, :], in0=best[:, 0:2, :], in1=best[:, 2:7:4, :], op=ALU.max)
            nc.vector.tensor_tensor(out=best[:, 0, :], in0=best[:, 0, :], in1=best[:, 1, :], op=ALU.max)
            nc.vector.tensor_scalar_mul(out=neg_top[:, NU:HW], in0=best[:, 0, :], scalar1=-1.0)
            load_logits(1)
            nc.sync.dma_start(out=bias_row[:].rearrange("p h c -> p (h c)"), in_=b3c.partition_broadcast(P))
        prodv_pool = ctx.enter_context(tc.tile_pool(name="prodv", bufs=3))
        prodg_pool = ctx.enter_context(tc.tile_pool(name="prodg", bufs=4))
        xs_pool = ctx.enter_context(tc.tile_pool(name="xs", bufs=2))
        sums_pool = ctx.enter_context(tc.tile_pool(name="sums", bufs=1))
        res_pool = ctx.enter_context(tc.tile_pool(name="res", bufs=1))

        def window(u, l):
            dy, dx = divmod(l, K)
            slot = (UROWS * u + dy) % RING
            if slot + UROWS <= RING:
                return [(slice(0, UROWS), xmap[:, slot : slot + UROWS, dx : dx + W, :])]
            return [(slice(r, r + 1), xmap[:, (slot + r) % RING : (slot + r) % RING + 1, dx : dx + W, :]) for r in range(UROWS)]

        def multiply(engine, u, l, prod, weights):
            prod_v = prod[:].rearrange("p (r q) c -> p r q c", q=W)
            weights_v = weights.rearrange("p (r q) -> p r q", q=W).unsqueeze(3)
            for rows, win in window(u, l):
                cnt = rows.stop - rows.start
                engine.tensor_tensor(
                    out=prod_v[:, rows],
                    in0=win,
                    in1=weights_v[:, rows].to_broadcast([P, cnt, W, SP]),
                    op=ALU.mult,
                )

        sums_of = {}
        added = {(u, bank): 0 for u in range(UNITS) for bank in range(BANKS)}
        S_ITEMS = []
        for u in range(UNITS):
            ls0 = FULL[u][0] + NV[u] + NG[u]
            items = [(l, n) for l in range(ls0, FULL[u][1]) for n in range(NU)]
            if HALF[u]:
                dy, r = HALF[u]
                items = [(K * dy + dx, n) for dx in range(K) for n in range(r * W, (r + 1) * W)] + items
            S_ITEMS.append(items)
        NADDS = {}
        for u in range(UNITS):
            for bank in range(BANKS):
                pieces = len([1 for l, n in S_ITEMS[u] if n == bank * NPOS])
                NADDS[(u, bank)] = NV[u] + NG[u] - GADD[u] + pieces

        def add_bank(u, bank, flat):
            if added[(u, bank)] == 0:
                sums = acc_pool.tile([P, PER_BANK, P], F32, tag="sums%d" % bank, name="sums")
                sums_of[(u, bank)] = sums
            for j in range(PER_BANK):
                nc.tensor.matmul(
                    out=sums_of[(u, bank)][:, j, :],
                    lhsT=flat[:, j * P : (j + 1) * P],
                    rhs=ident[:],
                    is_transpose=True,
                    start=(added[(u, bank)] == 0 and j == 0),
                    stop=(added[(u, bank)] == NADDS[(u, bank)] - 1 and j == PER_BANK - 1),
                )
            added[(u, bank)] += 1

        def add(u, prod):
            for bank in range(BANKS):
                add_bank(u, bank, prod[:, bank * NPOS : (bank + 1) * NPOS, :].rearrange("p n c -> p (n c)"))

        gprods = {}

        def g_multiply(u, i):
            pg = prodg_pool.tile([P, NU, SP], F32, name="pg")
            l = FULL[u][0] + NV[u] + i
            multiply(nc.gpsimd, u, l, pg, state[u]["wl"][:, :, l])
            gprods[(u, i)] = pg

        def g_add(u, i):
            nc.gpsimd.tensor_tensor(
                out=gprods[(u, i)][:], in0=gprods[(u, i)][:], in1=gprods[(u, i + 1)][:], op=ALU.add
            )

        sprods = {}

        def s_multiply(u, e):
            l, n = S_ITEMS[u][e]
            piece, k = divmod(e, NPOS)
            if k == 0:
                ps = prods_pool.tile([P, NPOS, SP], F32, name="ps")
                sprods[(u, piece)] = ps
            dy, dx = divmod(l, K)
            r, q = divmod(n, W)
            nc.scalar.activation(
                out=sprods[(u, piece)][:, k, :],
                in_=xmap[:, (UROWS * u + dy + r) % RING, q + dx, :],
                func=ACT.Copy,
                scale=state[u]["wl"][:, n, l : l + 1],
            )

        def add_piece(u, i):
            bank = S_ITEMS[u][i * NPOS][1] // NPOS
            add_bank(u, bank, sprods[(u, i)][:].rearrange("p n c -> p (n c)"))

        sums_sb_of = {}
        result_of = {}

        def take_sums(u):
            sums_sb = sums_pool.tile([P, BLOCKS, P], F32, name="sums_sb")
            for bank in range(BANKS):
                nc.scalar.copy(out=sums_sb[:, bank * PER_BANK : (bank + 1) * PER_BANK, :], in_=sums_of[(u, bank)][:])
            sums_sb_of[u] = sums_sb

        def back_task(u, bank):
            hold = {}

            def fill():
                back = stage.tile([P, PER_BANK * P], F32, tag="stage", name="back")
                for j in range(PER_BANK):
                    nc.tensor.transpose(
                        back[:, j * P : (j + 1) * P], sums_sb_of[u][:, bank * PER_BANK + j, :], ident[:]
                    )
                hold["back"] = back

            def drain():
                if bank == 0:
                    result = res_pool.tile([P, SP, NU], F32, name="result")
                    result_of[u] = result
                inv = state[u]["inv"][:, bank * NPOS : (bank + 1) * NPOS]
                nc.vector.tensor_tensor(
                    out=result_of[u][:, :, bank * NPOS : (bank + 1) * NPOS],
                    in0=hold["back"][:].rearrange("p (n c) -> p c n", c=SP),
                    in1=inv.unsqueeze(1).to_broadcast([P, SP, NPOS]),
                    op=ALU.mult,
                )
                if bank == BANKS - 1:
                    nc.sync.dma_start(out=out_v[:, :, u * NU : (u + 1) * NU], in_=result_of[u][:])

            return fill, drain

        GLEAD, GLAG = 1, 1
        SLEAD, SLAG = 2, 1
        BACK0 = 1
        g_at, s_at, take_at, small_at, drain_at, fill_at = {}, {}, {}, {}, {}, {}
        wps_of = {}

        def take_wps(u, c):
            wps_of[(u, c)] = load_wps(u, c)

        def put(where, t, task):
            where.setdefault(max(t, 0), []).append(task)

        def stage_tasks(t, task, lag):
            fill, drain = task
            put(fill_at, t, fill)
            put(drain_at, t + lag, drain)

        def spread(t0, first, steps, count, task):
            for i in range(steps):
                n0, n1 = i * count // steps, (i + 1) * count // steps
                put(small_at, t0 + first + i, lambda n0=n0, n1=n1: task(n0, n1))

        for u in range(UNITS):
            t0, nv, ng = TSTART[u], STEPS[u], NG[u]
            last = t0 + nv - 1
            jobs = []
            for i in range(ng):
                jobs.append((g_multiply, i))
                if i % 2 == 1 and i // 2 < GADD[u]:
                    jobs.append((g_add, i - 1))
            for k, (job, i) in enumerate(jobs):
                put(g_at, t0 + k * nv // len(jobs) - GLEAD, lambda job=job, u=u, i=i: job(u, i))
                if job is g_add or i >= 2 * GADD[u]:
                    done = t0 - GLEAD - (-(k + 1) * nv // len(jobs)) + GLAG
                    put(take_at, min(max(done, t0), last), lambda u=u, i=i: add(u, gprods[(u, i)]))
            early = 0 if u else EARLY
            count = len(S_ITEMS[u]) - early
            for e in range(count):
                put(s_at, t0 + e * nv // count - SLEAD, lambda u=u, e=early + e: s_multiply(u, e))
            for i in range(count // NPOS):
                done = t0 - SLEAD - (-(i + 1) * NPOS * nv // count) + SLAG
                put(take_at, min(max(done, t0), last), lambda u=u, i=early // NPOS + i: add_piece(u, i))
            if u:
                put(drain_at, t0, lambda u=u: take_sums(u - 1))
                for bank in range(BANKS):
                    stage_tasks(t0 + BACK0 + bank, back_task(u - 1, bank), 2)
            k, odd = divmod(u, 2)
            t = k + 2
            if u == 0:
                for b in range(B):
                    stage_tasks(t0 + 2 * b, map_task(t, b), 2)
                put(small_at, t0 + 11, lambda t=t: load_map(t))
            elif odd and t + 1 < TILES:
                for b in (0, 1):
                    stage_tasks(t0 + 8 + 2 * b, map_task(t + 1, b), 2)
            elif not odd and t < TILES:
                for b in (2, 3):
                    stage_tasks(t0 + 4 + 2 * b, map_task(t, b), 2)
                put(small_at, t0 + 14, lambda t=t: load_map(t))
            for c in range(NCHUNKS):
                after = t0 + min(2 * CSTART[u][c + 1], NV[u]) * STEPS[u] // NV[u] - 1
                if c + 2 < NCHUNKS:
                    put(fill_at, after, lambda u=u, c=c: take_wps(u, c + 2))
                elif u + 1 < UNITS:
                    put(fill_at, max(after, last - 3 if u else last - 2), lambda u=u, c=c: take_wps(u + 1, c + 2 - NCHUNKS))
            if u + 2 < UNITS:
                put(small_at, t0 + nv - 9, lambda u=u: load_logits(u + 2))
            if u + 1 < UNITS:
                st = state[u + 1]
                spread(t0, 0, nv - 10, NU, lambda n0, n1, u=u, st=st: softmax_exp(u + 1, st, n0, n1))
                wv = last - 6 if u else last - 4
                put(g_at, wv - 3, lambda u=u, st=st: fold(nc.gpsimd, u + 1, st))
                put(small_at, last - 2, lambda st=st: softmax_recip(st))
                for c in range(NCHUNKS):
                    gather, fill, drain = v_weights(u + 1, st, c)
                    put(small_at, wv - 1 + c, gather)
                    stage_tasks(wv + c, (fill, drain), 1 if c < SCALAR_CHUNKS else 2)

        take_wps(0, 0)
        take_wps(0, 1)
        for e in range(EARLY):
            s_multiply(0, e)
            if e % NPOS == NPOS - 1:
                add_piece(0, e // NPOS)
        for u in range(UNITS):
            chunk_of = [k for k in range(NCHUNKS) for i in range(CSTART[u][k], CSTART[u][k + 1]) for two in range(2)]
            step_of = [i * STEPS[u] // NV[u] for i in range(NV[u])]
            for s in range(STEPS[u]):
                t = TSTART[u] + s
                for job in g_at.get(t, []):
                    job()
                if s in step_of:
                    i = step_of.index(s)
                    k = chunk_of[i]
                    pv = prodv_pool.tile([P, NU, SP], F32, name="pv")
                    multiply(nc.vector, u, FULL[u][0] + i, pv, wps_of[(u, k)][:, i - 2 * CSTART[u][k], :])
                for job in s_at.get(t, []) + small_at.get(t, []) + drain_at.get(t, []):
                    job()
                if s in step_of:
                    add(u, pv)
                for job in take_at.get(t, []) + fill_at.get(t, []):
                    job()
        take_sums(UNITS - 1)
        for bank in range(BANKS):
            for part in back_task(UNITS - 1, bank):
                part()
